import numpy as np
import ml_dtypes


def mxq(x, axis, fmt="e4m3"):
    dtype, down = {"e4m3": (ml_dtypes.float8_e4m3fn, 7), "e5m2": (ml_dtypes.float8_e5m2, 14)}[fmt]
    v = np.moveaxis(np.asarray(x, np.float32).astype(ml_dtypes.bfloat16).astype(np.float64), axis, -1)
    blocks = v.reshape(v.shape[:-1] + (-1, 32))
    amax = np.abs(blocks).max(-1, keepdims=True)
    byte = np.maximum(np.where(amax > 0, np.frexp(amax)[1] - 1 + 127, 0) - down, 1)
    scale = np.exp2(byte - 127.0)
    codes = (blocks / scale).astype(np.float32).astype(dtype).astype(np.float64)
    return np.moveaxis((codes * scale).reshape(v.shape), -1, axis)


WIDE = False


def mx_kscale(k):
    if not WIDE:
        return np.ones(k)
    levels = np.array([10, -10, 5, -5, 0])
    a = np.random.permutation(np.resize(levels, k // 512 * 4)).reshape(k // 512, 4)
    idx = np.arange(k)
    return np.exp2(a[idx // 512, idx % 128 // 32])


BF16 = ml_dtypes.bfloat16


def bf(x):
    return np.asarray(x, np.float32).astype(BF16)


def f64(x):
    return np.asarray(x).astype(np.float64)


B, T, U, De, Dd, V = 8, 32, 16, 512, 512, 1024
F = De + Dd


def log_sigmoid(v):
    return -np.logaddexp(0.0, -v)


def log_softmax(v):
    z = v - v.max(-1, keepdims=True)
    return z - np.log(np.exp(z).sum(-1, keepdims=True))


def setup_inputs():
    s, r = mx_kscale(De), mx_kscale(Dd)
    return {"encoder_output": bf(np.random.standard_normal((B, T, De)) * s),
            "decoder_output": bf(np.random.standard_normal((B, U, Dd)) * r),
            "W_enc": bf(np.random.standard_normal((F, De)) * 0.7 / np.sqrt(De) / s[None, :]),
            "b_enc": bf(np.random.standard_normal(F) * 0.3),
            "W_dec": bf(np.random.standard_normal((F, Dd)) * 0.7 / np.sqrt(Dd) / r[None, :]),
            "b_dec": bf(np.random.standard_normal(F) * 0.3),
            "W_fc": bf(np.random.standard_normal((V, F)) * 1.5 / np.sqrt(F)),
            "b_fc": bf(np.random.standard_normal(V) * 0.3)}


def reference(encoder_output, decoder_output, W_enc, b_enc, W_dec, b_dec, W_fc, b_fc):
    enc = (mxq(f64(encoder_output), 2, "e4m3") @ mxq(f64(W_enc), 1, "e4m3").T) + f64(b_enc)
    dec = (mxq(f64(decoder_output), 2, "e4m3") @ mxq(f64(W_dec), 1, "e4m3").T) + f64(b_dec)
    combined = enc[:, :, None, :] + dec[:, None, :, :]
    h = np.tanh(combined)
    vocab_logits = (mxq(h, 3, "e4m3") @ mxq(f64(W_fc), 1, "e4m3").T) + f64(b_fc)
    blk_logit = vocab_logits[..., :1]
    log_blk = log_sigmoid(blk_logit)
    log_not_blk = log_sigmoid(-blk_logit)
    vocab_log_probs = log_not_blk + log_softmax(vocab_logits[..., 1:])
    return np.concatenate([log_blk, vocab_log_probs], axis=-1)

@@ -1,0 +1,314 @@
+from contextlib import ExitStack
+
+import concourse.mybir as mybir
+from concourse.masks import make_identity
+
+F32 = mybir.dt.float32
+BF16 = mybir.dt.bfloat16
+U32 = mybir.dt.uint32
+U8 = mybir.dt.uint8
+I32 = mybir.dt.int32
+FP8X4 = mybir.dt.float8_e4m3fn_x4
+ALU = mybir.AluOpType
+ACT = mybir.ActivationFunctionType
+AX = mybir.AxisListType
+
+P = 128
+B, T, U, V = 8, 32, 16, 1024
+FLOPS = 2 * (256 * 512 * 1024 + 128 * 512 * 1024 + 4096 * 1024 * 1024)
+
+LN2 = 0.6931471805599453
+K1 = LN2 / 8388608.0
+K2 = (0.043 - 127.0) * LN2
+NEWTON = 4
+
+
+def tile_jointnet_kernel(
+    tc, encoder_output, decoder_output, W_enc, b_enc, W_dec, b_dec, W_fc, b_fc, out
+):
+    nc = tc.nc
+    out_rows = out.flatten_outer_dims()
+    with ExitStack() as ctx:
+        const = ctx.enter_context(tc.tile_pool(name="const", bufs=1))
+        work = ctx.enter_context(tc.tile_pool(name="work", bufs=3))
+        codes = ctx.enter_context(tc.tile_pool(name="codes", bufs=4))
+        zpool = ctx.enter_context(tc.tile_pool(name="zpool", bufs=4))
+        stat = ctx.enter_context(tc.tile_pool(name="stat", bufs=3))
+        psum = ctx.enter_context(tc.psum_pool(name="psum", bufs=8))
+
+        ident = const.tile([P, P], F32, name="ident")
+        make_identity(nc, ident[:])
+        warm = const.tile([P, 8], F32, name="warm")
+        nc.vector.memset(warm[:], 0.0)
+        warm2 = const.tile([P, 8], F32, name="warm2")
+        nc.scalar.activation(out=warm2[:], in_=warm[:], func=ACT.Exp)
+        braw = const.tile([P, 256], BF16, name="braw")
+        nc.vector.memset(braw[:], 0.0)
+
+        xin = const.tile([P, 1536], BF16, name="xin")
+        we = const.tile([P, 4096], BF16, name="we")
+        wd = const.tile([P, 4096], BF16, name="wd")
+        wf = const.tile([P, 8192], BF16, name="wf")
+        bfc = const.tile([P, V], BF16, name="bfc")
+
+        nc.sync.dma_start(
+            out=xin[:, 0:1024].rearrange("p (r k) -> p r k", r=2),
+            in_=encoder_output.flatten_outer_dims().rearrange("(r p) k -> p r k", p=P),
+        )
+        nc.sync.dma_start(out=xin[:, 1024:1536], in_=decoder_output.flatten_outer_dims())
+        we_src = W_enc.rearrange("(c p e) k -> p c (e k)", c=4, p=P, e=2)
+        wd_src = W_dec.rearrange("(c p e) k -> p c (e k)", c=4, p=P, e=2)
+        we_dst = we[:].rearrange("p (c x) -> p c x", c=4)
+        wd_dst = wd[:].rearrange("p (c x) -> p c x", c=4)
+        nc.sync.dma_start(out=we_dst[:, 0:2, :], in_=we_src[:, 0:2, :])
+        nc.sync.dma_start(out=wd_dst[:, 0:2, :], in_=wd_src[:, 0:2, :])
+        nc.sync.dma_start(out=braw[0:4, :], in_=b_enc.rearrange("(c x) -> c x", c=4))
+        nc.sync.dma_start(out=braw[4:8, :], in_=b_dec.rearrange("(c x) -> c x", c=4))
+        nc.sync.dma_start(out=we_dst[:, 2:4, :], in_=we_src[:, 2:4, :])
+        nc.sync.dma_start(out=wd_dst[:, 2:4, :], in_=wd_src[:, 2:4, :])
+        wf_src = W_fc.rearrange("(r p) f -> p r f", p=P)
+        wf_dst = wf[:].rearrange("p (r f) -> p r f", r=8)
+        nc.sync.dma_start(out=wf_dst[:, 0:4, :], in_=wf_src[:, 0:4, :])
+        nc.sync.dma_start(out=wf_dst[:, 4:8, :], in_=wf_src[:, 4:8, :])
+        nc.sync.dma_start(out=bfc[:], in_=b_fc.partition_broadcast(P))
+
+        evac_count = [0]
+
+        def evacuate(dst, src):
+            if evac_count[0] % 2 == 0:
+                nc.vector.tensor_copy(out=dst, in_=src)
+            else:
+                nc.scalar.copy(out=dst, in_=src)
+            evac_count[0] += 1
+
+        def transpose_words(src32, dst32, n_units):
+            for u0 in range(0, n_units, 2):
+                n = min(2, n_units - u0)
+                pt = psum.tile([P, 512], F32, name="pt", tag="bank")
+                for i in range(2 * n):
+                    nc.tensor.transpose(
+                        out=pt[:, i * P : (i + 1) * P],
+                        in_=src32[:, u0 * 256 + i * P : u0 * 256 + (i + 1) * P],
+                        identity=ident[:],
+                    )
+                evacuate(
+                    dst32[:, u0 * 256 : (u0 + n) * 256].rearrange(
+                        "q (c r h) -> q c r h", c=n, h=2
+                    ),
+                    pt[:, 0 : n * 256].rearrange("q (c h r) -> q c r h", c=n, h=2),
+                )
+
+        xg = const.tile([P, 1536], BF16, name="xg", align_bytes=64)
+        xc = const.tile([P, 384], U32, name="xc", align_bytes=64)
+        xs = const.tile([P, 384], U8, name="xs", align_bytes=64)
+        transpose_words(xin[:].bitcast(F32), xg[:].bitcast(F32), 3)
+        nc.vector.quantize_mx(
+            out=xc[:, 0:256].bitcast(FP8X4), scales=xs[:, 0:256], in_=xg[:, 0:1024]
+        )
+        nc.vector.quantize_mx(
+            out=xc[:, 256:384].bitcast(FP8X4), scales=xs[:, 256:384], in_=xg[:, 1024:1536]
+        )
+
+        ptb = psum.tile([P, 512], F32, name="ptb", tag="bank")
+        nc.tensor.transpose(out=ptb[:, 0:P], in_=braw[:].bitcast(F32), identity=ident[:])
+        bT = const.tile([P, 8], F32, name="bT")
+        nc.vector.tensor_copy(out=bT[:], in_=ptb[:, 0:8])
+        bsum = const.tile([P, 8], F32, name="bsum")
+        bT16 = bT[:].bitcast(BF16)
+        nc.vector.tensor_tensor(out=bsum[:], in0=bT16[:, 0:8], in1=bT16[:, 8:16], op=ALU.add)
+
+        weg = const.tile([P, 4096], BF16, name="weg", align_bytes=64)
+        wdg = const.tile([P, 4096], BF16, name="wdg", align_bytes=64)
+        wec = const.tile([P, 1024], U32, name="wec", align_bytes=64)
+        wes = const.tile([P, 1024], U8, name="wes", align_bytes=64)
+        wdc = const.tile([P, 1024], U32, name="wdc", align_bytes=64)
+        wds = const.tile([P, 1024], U8, name="wds", align_bytes=64)
+        encT = const.tile([P, 2048], F32, name="encT")
+        decT = const.tile([P, 1024], F32, name="decT")
+        enc_v = encT[:].rearrange("p (g w j) -> p g w j", g=2, j=4)
+        dec_v = decT[:].rearrange("p (g w j) -> p g w j", g=2, j=4)
+
+        for g in range(2):
+            for raw, grp, cod, sca in ((we, weg, wec, wes), (wd, wdg, wdc, wds)):
+                transpose_words(
+                    raw[:].bitcast(F32)[:, g * 1024 : (g + 1) * 1024],
+                    grp[:].bitcast(F32)[:, g * 1024 : (g + 1) * 1024],
+                    4,
+                )
+                nc.vector.quantize_mx(
+                    out=cod[:, g * 512 : (g + 1) * 512].bitcast(FP8X4),
+                    scales=sca[:, g * 512 : (g + 1) * 512],
+                    in_=grp[:, g * 2048 : (g + 1) * 2048],
+                )
+            for r in range(3):
+                cod, sca = (wec, wes) if r < 2 else (wdc, wds)
+                ps = psum.tile([P, 512], F32, name="ps", tag="bank")
+                for j in range(4):
+                    c0 = (g * 4 + j) * P
+                    nc.tensor.matmul_mx(
+                        out=ps[:, j * P : (j + 1) * P],
+                        lhsT=cod[:, c0 : c0 + P].bitcast(FP8X4),
+                        lhsT_scale=sca[:, c0 : c0 + P],
+                        rhs=xc[:, r * P : (r + 1) * P].bitcast(FP8X4),
+                        rhs_scale=xs[:, r * P : (r + 1) * P],
+                        start=True,
+                        stop=True,
+                    )
+                ps_wj = ps[:].rearrange("p (j w) -> p w j", j=4)
+                if r < 2:
+                    nc.vector.tensor_tensor(
+                        out=enc_v[:, g, r * P : (r + 1) * P, :],
+                        in0=ps_wj,
+                        in1=bsum[:, g * 4 : (g + 1) * 4].unsqueeze(1).to_broadcast([P, P, 4]),
+                        op=ALU.add,
+                    )
+                else:
+                    nc.scalar.copy(out=dec_v[:, g, :, :], in_=ps_wj)
+
+        wfc = const.tile([P, 2048], U32, name="wfc", align_bytes=64)
+        wfs = const.tile([P, 2048], U8, name="wfs", align_bytes=64)
+        wf32 = wf[:].bitcast(F32).rearrange("p (r g x) -> p r g x", r=8, g=2)
+        for g in range(2):
+            wfg = const.tile([P, 4096], BF16, name="wfg%d" % g, align_bytes=64)
+            wfg32 = wfg[:].bitcast(F32)
+            for r0 in range(0, 8, 2):
+                pt = psum.tile([P, 512], F32, name="ptf", tag="bank")
+                for c in range(2):
+                    for h in range(2):
+                        i = c * 2 + h
+                        nc.tensor.transpose(
+                            out=pt[:, i * P : (i + 1) * P],
+                            in_=wf32[:, r0 + c, g, h * P : (h + 1) * P],
+                            identity=ident[:],
+                        )
+                evacuate(
+                    wfg32[:, r0 * 256 : (r0 + 2) * 256].rearrange(
+                        "q (c r h) -> q c r h", c=2, h=2
+                    ),
+                    pt[:].rearrange("q (c h r) -> q c r h", c=2, h=2),
+                )
+            nc.vector.quantize_mx(
+                out=wfc[:, g * 1024 : (g + 1) * 1024].bitcast(FP8X4),
+                scales=wfs[:, g * 1024 : (g + 1) * 1024],
+                in_=wfg[:],
+            )
+
+        for b in range(B):
+            hc, hs = [], []
+            for g in range(2):
+                comb = work.tile([P, 2048], F32, name="comb", tag="comb")
+                add_eng = nc.vector if (b == 0 and g == 0) else nc.gpsimd
+                add_eng.tensor_tensor(
+                    out=comb[:].rearrange("p (t u j) -> p t u j", t=T, u=U),
+                    in0=enc_v[:, g, b * T : (b + 1) * T, :].unsqueeze(2).to_broadcast([P, T, U, 4]),
+                    in1=dec_v[:, g, b * U : (b + 1) * U, :].unsqueeze(1).to_broadcast([P, T, U, 4]),
+                    op=ALU.add,
+                )
+                h = work.tile([P, 2048], BF16, name="h", tag="h", align_bytes=64)
+                nc.scalar.activation(out=h[:], in_=comb[:], func=ACT.Tanh)
+                hcg = codes.tile([P, 512], U32, name="hc", tag="hc", align_bytes=64)
+                hsg = codes.tile([P, 512], U8, name="hs", tag="hs", align_bytes=64)
+                nc.vector.quantize_mx(out=hcg[:].bitcast(FP8X4), scales=hsg[:], in_=h[:])
+                hc.append(hcg)
+                hs.append(hsg)
+
+            zb = zpool.tile([P, 4 * V], F32, name="zb", tag="zb")
+            zv = zb[:].rearrange("p (n v) -> p n v", n=4)
+            z0 = zv[:, :, 0]
+            negm = stat.tile([P, 4], F32, name="negm", tag="negm")
+            xx = stat.tile([P, 16], F32, name="xx", tag="xx")
+            for n in range(4):
+                ys = [psum.tile([P, 512], F32, name="y%d" % v, tag="bank") for v in range(2)]
+                for g in range(2):
+                    for v in range(2):
+                        c0 = g * 1024 + v * 512
+                        nc.tensor.matmul_mx(
+                            out=ys[v][:],
+                            lhsT=hc[g][:, n * P : (n + 1) * P].bitcast(FP8X4),
+                            lhsT_scale=hs[g][:, n * P : (n + 1) * P],
+                            rhs=wfc[:, c0 : c0 + 512].bitcast(FP8X4),
+                            rhs_scale=wfs[:, c0 : c0 + 512],
+                            start=(g == 0),
+                            stop=(g == 1),
+                        )
+                for v in range(2):
+                    nc.vector.tensor_tensor(
+                        out=zv[:, n, v * 512 : (v + 1) * 512],
+                        in0=ys[v][:],
+                        in1=bfc[:, v * 512 : (v + 1) * 512],
+                        op=ALU.add,
+                    )
+                nc.vector.tensor_reduce(
+                    out=negm[:, n : n + 1], in_=zv[:, n, 1:V], axis=AX.X, op=ALU.max, negate=True
+                )
+                junk = work.tile([P, V], BF16, name="junk", tag="junk")
+                nc.scalar.activation(
+                    out=junk[:, 0 : V - 1],
+                    in_=zv[:, n, 1:V],
+                    func=ACT.Exp,
+                    bias=negm[:, n : n + 1],
+                    scale=1.0,
+                    accum_out=xx[:, n : n + 1],
+                )
+
+            mx = stat.tile([P, 4], F32, name="mx", tag="mx")
+            nc.vector.tensor_scalar(out=mx[:], in0=z0, scalar1=0.0, scalar2=None, op0=ALU.max)
+            na = stat.tile([P, 4], F32, name="na", tag="na")
+            nc.vector.scalar_tensor_tensor(
+                out=na[:], in0=mx[:], scalar=-2.0, in1=z0, op0=ALU.mult, op1=ALU.add
+            )
+            ev = stat.tile([P, 4], F32, name="ev", tag="ev")
+            nc.scalar.activation(out=ev[:], in_=na[:], func=ACT.Exp)
+            nc.vector.tensor_scalar(
+                out=xx[:, 8:12], in0=ev[:], scalar1=1.0, scalar2=None, op0=ALU.add
+            )
+            xv = xx[:].rearrange("p (a c) -> p a c", a=2)[:, :, 0:4]
+            xi = xx[:].bitcast(I32).rearrange("p (a c) -> p a c", a=2)[:, :, 0:4]
+            lg = stat.tile([P, 8], F32, name="lg", tag="lg")
+            lgv = lg[:].rearrange("p (a c) -> p a c", a=2)
+            nc.vector.tensor_scalar(
+                out=lgv, in0=xi, scalar1=K1, scalar2=K2, op0=ALU.mult, op1=ALU.add
+            )
+            for it in range(NEWTON):
+                en = stat.tile([P, 8], F32, name="en", tag="en")
+                nc.scalar.activation(out=en[:], in_=lg[:], func=ACT.Exp, scale=-1.0)
+                tn = stat.tile([P, 8], F32, name="tn", tag="tn")
+                nc.vector.tensor_tensor(
+                    out=tn[:].rearrange("p (a c) -> p a c", a=2),
+                    in0=en[:].rearrange("p (a c) -> p a c", a=2),
+                    in1=xv,
+                    op=ALU.mult,
+                )
+                nc.vector.scalar_tensor_tensor(
+                    out=lg[:], in0=lg[:], scalar=-1.0, in1=tn[:], op0=ALU.add, op1=ALU.add
+                )
+            aa = stat.tile([P, 4], F32, name="aa", tag="aa")
+            nc.vector.tensor_tensor(out=aa[:], in0=lg[:, 0:4], in1=negm[:], op=ALU.subtract)
+            nc.vector.tensor_tensor(out=z0, in0=z0, in1=aa[:], op=ALU.add)
+            bb = stat.tile([P, 4], F32, name="bb", tag="bb")
+            nc.vector.tensor_tensor(out=bb[:], in0=mx[:], in1=lg[:, 4:8], op=ALU.add)
+            negc = stat.tile([P, 4], F32, name="negc", tag="negc")
+            nc.vector.scalar_tensor_tensor(
+                out=negc[:], in0=aa[:], scalar=-1.0, in1=bb[:], op0=ALU.mult, op1=ALU.subtract
+            )
+
+            for n in range(4):
+                if n % 2 == 0:
+                    nc.gpsimd.tensor_scalar(
+                        out=zv[:, n, :],
+                        in0=zv[:, n, :],
+                        scalar1=1.0,
+                        scalar2=negc[:, n : n + 1],
+                        op0=ALU.mult,
+                        op1=ALU.add,
+                    )
+                else:
+                    nc.scalar.activation(
+                        out=zv[:, n, :],
+                        in_=zv[:, n, :],
+                        func=ACT.Identity,
+                        bias=negc[:, n : n + 1],
+                        scale=1.0,
+                    )
+                r0 = (b * 4 + n) * P
+                nc.sync.dma_start(out=out_rows[r0 : r0 + P, :], in_=zv[:, n, :])

@@ -19,8 +19,9 @@ FLOPS = 2 * (256 * 512 * 1024 + 128 * 512 * 1024 + 4096 * 1024 * 1024)
 
 LN2 = 0.6931471805599453
 K1 = LN2 / 8388608.0
-K2 = (0.043 - 127.0) * LN2
-NEWTON = 4
+C0 = (0.043 - 127.0) * 8388608.0
+
+FIN = ("G", "S", "G", "S")
 
 
 def tile_jointnet_kernel(
@@ -29,286 +30,452 @@ def tile_jointnet_kernel(
     nc = tc.nc
     out_rows = out.flatten_outer_dims()
     with ExitStack() as ctx:
+        ctx.enter_context(tc.manual_schedule())
         const = ctx.enter_context(tc.tile_pool(name="const", bufs=1))
-        work = ctx.enter_context(tc.tile_pool(name="work", bufs=3))
-        codes = ctx.enter_context(tc.tile_pool(name="codes", bufs=4))
-        zpool = ctx.enter_context(tc.tile_pool(name="zpool", bufs=4))
-        stat = ctx.enter_context(tc.tile_pool(name="stat", bufs=3))
+        work = ctx.enter_context(tc.tile_pool(name="work", bufs=4))
+        stat = ctx.enter_context(tc.tile_pool(name="stat", bufs=4))
         psum = ctx.enter_context(tc.psum_pool(name="psum", bufs=8))
 
-        ident = const.tile([P, P], F32, name="ident")
-        make_identity(nc, ident[:])
-        warm = const.tile([P, 8], F32, name="warm")
-        nc.vector.memset(warm[:], 0.0)
-        warm2 = const.tile([P, 8], F32, name="warm2")
-        nc.scalar.activation(out=warm2[:], in_=warm[:], func=ACT.Exp)
-        braw = const.tile([P, 256], BF16, name="braw")
-        nc.vector.memset(braw[:], 0.0)
-
-        xin = const.tile([P, 1536], BF16, name="xin")
-        we = const.tile([P, 4096], BF16, name="we")
-        wd = const.tile([P, 4096], BF16, name="wd")
-        wf = const.tile([P, 8192], BF16, name="wf")
-        bfc = const.tile([P, V], BF16, name="bfc")
-
-        nc.sync.dma_start(
-            out=xin[:, 0:1024].rearrange("p (r k) -> p r k", r=2),
-            in_=encoder_output.flatten_outer_dims().rearrange("(r p) k -> p r k", p=P),
-        )
-        nc.sync.dma_start(out=xin[:, 1024:1536], in_=decoder_output.flatten_outer_dims())
-        we_src = W_enc.rearrange("(c p e) k -> p c (e k)", c=4, p=P, e=2)
-        wd_src = W_dec.rearrange("(c p e) k -> p c (e k)", c=4, p=P, e=2)
-        we_dst = we[:].rearrange("p (c x) -> p c x", c=4)
-        wd_dst = wd[:].rearrange("p (c x) -> p c x", c=4)
-        nc.sync.dma_start(out=we_dst[:, 0:2, :], in_=we_src[:, 0:2, :])
-        nc.sync.dma_start(out=wd_dst[:, 0:2, :], in_=wd_src[:, 0:2, :])
-        nc.sync.dma_start(out=braw[0:4, :], in_=b_enc.rearrange("(c x) -> c x", c=4))
-        nc.sync.dma_start(out=braw[4:8, :], in_=b_dec.rearrange("(c x) -> c x", c=4))
-        nc.sync.dma_start(out=we_dst[:, 2:4, :], in_=we_src[:, 2:4, :])
-        nc.sync.dma_start(out=wd_dst[:, 2:4, :], in_=wd_src[:, 2:4, :])
-        wf_src = W_fc.rearrange("(r p) f -> p r f", p=P)
-        wf_dst = wf[:].rearrange("p (r f) -> p r f", r=8)
-        nc.sync.dma_start(out=wf_dst[:, 0:4, :], in_=wf_src[:, 0:4, :])
-        nc.sync.dma_start(out=wf_dst[:, 4:8, :], in_=wf_src[:, 4:8, :])
-        nc.sync.dma_start(out=bfc[:], in_=b_fc.partition_broadcast(P))
-
-        evac_count = [0]
-
-        def evacuate(dst, src):
-            if evac_count[0] % 2 == 0:
-                nc.vector.tensor_copy(out=dst, in_=src)
-            else:
-                nc.scalar.copy(out=dst, in_=src)
-            evac_count[0] += 1
-
-        def transpose_words(src32, dst32, n_units):
-            for u0 in range(0, n_units, 2):
-                n = min(2, n_units - u0)
-                pt = psum.tile([P, 512], F32, name="pt", tag="bank")
-                for i in range(2 * n):
-                    nc.tensor.transpose(
-                        out=pt[:, i * P : (i + 1) * P],
-                        in_=src32[:, u0 * 256 + i * P : u0 * 256 + (i + 1) * P],
-                        identity=ident[:],
-                    )
-                evacuate(
-                    dst32[:, u0 * 256 : (u0 + n) * 256].rearrange(
-                        "q (c r h) -> q c r h", c=n, h=2
-                    ),
-                    pt[:, 0 : n * 256].rearrange("q (c h r) -> q c r h", c=n, h=2),
-                )
-
-        xg = const.tile([P, 1536], BF16, name="xg", align_bytes=64)
         xc = const.tile([P, 384], U32, name="xc", align_bytes=64)
         xs = const.tile([P, 384], U8, name="xs", align_bytes=64)
-        transpose_words(xin[:].bitcast(F32), xg[:].bitcast(F32), 3)
-        nc.vector.quantize_mx(
-            out=xc[:, 0:256].bitcast(FP8X4), scales=xs[:, 0:256], in_=xg[:, 0:1024]
-        )
-        nc.vector.quantize_mx(
-            out=xc[:, 256:384].bitcast(FP8X4), scales=xs[:, 256:384], in_=xg[:, 1024:1536]
-        )
-
-        ptb = psum.tile([P, 512], F32, name="ptb", tag="bank")
-        nc.tensor.transpose(out=ptb[:, 0:P], in_=braw[:].bitcast(F32), identity=ident[:])
-        bT = const.tile([P, 8], F32, name="bT")
-        nc.vector.tensor_copy(out=bT[:], in_=ptb[:, 0:8])
-        bsum = const.tile([P, 8], F32, name="bsum")
-        bT16 = bT[:].bitcast(BF16)
-        nc.vector.tensor_tensor(out=bsum[:], in0=bT16[:, 0:8], in1=bT16[:, 8:16], op=ALU.add)
-
-        weg = const.tile([P, 4096], BF16, name="weg", align_bytes=64)
-        wdg = const.tile([P, 4096], BF16, name="wdg", align_bytes=64)
         wec = const.tile([P, 1024], U32, name="wec", align_bytes=64)
         wes = const.tile([P, 1024], U8, name="wes", align_bytes=64)
         wdc = const.tile([P, 1024], U32, name="wdc", align_bytes=64)
         wds = const.tile([P, 1024], U8, name="wds", align_bytes=64)
+        wfc = const.tile([P, 2048], U32, name="wfc", align_bytes=64)
+        wfs = const.tile([P, 2048], U8, name="wfs", align_bytes=64)
         encT = const.tile([P, 2048], F32, name="encT")
         decT = const.tile([P, 1024], F32, name="decT")
+        bfc = const.tile([P, V], BF16, name="bfc")
+        ident = const.tile([P, P], F32, name="ident")
+        bT = const.tile([P, 8], F32, name="bT")
+        bsum = const.tile([P, 8], F32, name="bsum")
+        warm = const.tile([P, 8], F32, name="warm")
+        warm2 = const.tile([P, 8], F32, name="warm2")
+        one = const.tile([P, 1], F32, name="one")
         enc_v = encT[:].rearrange("p (g w j) -> p g w j", g=2, j=4)
         dec_v = decT[:].rearrange("p (g w j) -> p g w j", g=2, j=4)
 
-        for g in range(2):
-            for raw, grp, cod, sca in ((we, weg, wec, wes), (wd, wdg, wdc, wds)):
-                transpose_words(
-                    raw[:].bitcast(F32)[:, g * 1024 : (g + 1) * 1024],
-                    grp[:].bitcast(F32)[:, g * 1024 : (g + 1) * 1024],
-                    4,
+        comb, hid, hc, hs = {}, {}, {}, {}
+        ybank, zbt, negm, xx, st = {}, {}, {}, {}, {}
+
+        def add(b, g, eng, t0=0, t1=T):
+            if t0 == 0:
+                comb[b, g] = work.tile([P, 2048], F32, name="comb", tag="comb")
+            nt = t1 - t0
+            eng.tensor_tensor(
+                out=comb[b, g][:, t0 * 64 : t1 * 64].rearrange("p (t u j) -> p t u j", t=nt, u=U),
+                in0=enc_v[:, g, b * T + t0 : b * T + t1, :].unsqueeze(2).to_broadcast([P, nt, U, 4]),
+                in1=dec_v[:, g, b * U : (b + 1) * U, :].unsqueeze(1).to_broadcast([P, nt, U, 4]),
+                op=ALU.add,
+            )
+
+        def tanh(b, g, t0=0, t1=T):
+            if t0 == 0:
+                hid[b, g] = work.tile([P, 2048], BF16, name="hid", tag="hid", align_bytes=64)
+            nc.scalar.activation(
+                out=hid[b, g][:, t0 * 64 : t1 * 64], in_=comb[b, g][:, t0 * 64 : t1 * 64], func=ACT.Tanh
+            )
+
+        def quant(b, g, t0=0, t1=T):
+            if t0 == 0:
+                hc[b, g] = work.tile([P, 512], U32, name="hc", tag="hc", align_bytes=64)
+                hs[b, g] = work.tile([P, 512], U8, name="hs", tag="hs", align_bytes=64)
+            nc.vector.quantize_mx(
+                out=hc[b, g][:, t0 * 16 : t1 * 16].bitcast(FP8X4),
+                scales=hs[b, g][:, t0 * 16 : t1 * 16],
+                in_=hid[b, g][:, t0 * 64 : t1 * 64],
+            )
+
+        def matmul(i):
+            b, n = divmod(i, 4)
+            for v in range(2):
+                ybank[i, v] = psum.tile([P, 512], F32, name="y", tag="bank")
+            for g in range(2):
+                for v in range(2):
+                    c0 = g * 1024 + v * 512
+                    nc.tensor.matmul_mx(
+                        out=ybank[i, v][:],
+                        lhsT=hc[b, g][:, n * P : (n + 1) * P].bitcast(FP8X4),
+                        lhsT_scale=hs[b, g][:, n * P : (n + 1) * P],
+                        rhs=wfc[:, c0 : c0 + 512].bitcast(FP8X4),
+                        rhs_scale=wfs[:, c0 : c0 + 512],
+                        start=(g == 0),
+                        stop=(g == 1),
+                    )
+
+        def zrow(i):
+            b, n = divmod(i, 4)
+            return zbt[b][:].rearrange("p (n v) -> p n v", n=4)[:, n, :]
+
+        def bias_add(i, v):
+            nc.vector.tensor_tensor(
+                out=zrow(i)[:, v * 512 : (v + 1) * 512],
+                in0=ybank[i, v][:],
+                in1=bfc[:, v * 512 : (v + 1) * 512],
+                op=ALU.add,
+            )
+
+        def row_max(i):
+            b, n = divmod(i, 4)
+            nc.vector.tensor_reduce(
+                out=negm[b][:, n : n + 1], in_=zrow(i)[:, 1:V], axis=AX.X, op=ALU.max, negate=True
+            )
+
+        def exp_sum(i):
+            b, n = divmod(i, 4)
+            junk = work.tile([P, V], BF16, name="junk", tag="junk", bufs=2)
+            nc.scalar.activation(
+                out=junk[:, 0 : V - 1],
+                in_=zrow(i)[:, 1:V],
+                func=ACT.Exp,
+                bias=negm[b][:, n : n + 1],
+                scale=1.0,
+                accum_out=xx[b][:, n : n + 1],
+            )
+
+        def two(ap):
+            return ap.rearrange("p (a c) -> p a c", a=2)
+
+        def small(b, name, width=4):
+            st[b, name] = stat.tile([P, width], F32, name=name, tag=name)
+            return st[b, name]
+
+        def chain(b, step):
+            z0 = zbt[b][:].rearrange("p (n v) -> p n v", n=4)[:, :, 0]
+            xv = two(xx[b][:])[:, :, 0:4]
+            if step == "ab":
+                nc.scalar.activation(out=small(b, "ab")[:], in_=z0, func=ACT.Abs)
+            elif step == "ev":
+                nc.scalar.activation(
+                    out=small(b, "ev")[:], in_=st[b, "ab"][:], func=ACT.Exp, scale=-1.0
                 )
+            elif step == "q":
+                nc.scalar.activation(
+                    out=xx[b][:, 8:12], in_=st[b, "ev"][:], func=ACT.Identity, bias=one[:], scale=1.0
+                )
+            elif step == "mx":
+                nc.scalar.activation(out=small(b, "mx")[:], in_=z0, func=ACT.Relu)
+            elif step == "x0":
+                nc.vector.tensor_scalar(
+                    out=two(small(b, "lg", 8)[:]),
+                    in0=two(xx[b][:].bitcast(I32))[:, :, 0:4],
+                    scalar1=C0,
+                    scalar2=K1,
+                    op0=ALU.add,
+                    op1=ALU.mult,
+                )
+            elif step == "e0":
+                nc.scalar.activation(
+                    out=small(b, "e0", 8)[:], in_=st[b, "lg"][:], func=ACT.Exp, scale=-1.0
+                )
+            elif step == "t0":
+                nc.vector.tensor_tensor(
+                    out=two(small(b, "t0", 8)[:]), in0=two(st[b, "e0"][:]), in1=xv, op=ALU.mult
+                )
+            elif step in ("g1", "g2"):
+                src = "t0" if step == "g1" else "t1"
+                nc.scalar.activation(
+                    out=small(b, step, 8)[:], in_=st[b, src][:], func=ACT.Exp, bias=one[:], scale=-1.0
+                )
+            elif step in ("a1", "a2"):
+                src = "t0" if step == "a1" else "t1"
+                nc.vector.tensor_tensor(
+                    out=st[b, "lg"][:], in0=st[b, "lg"][:], in1=st[b, src][:], op=ALU.add
+                )
+            elif step in ("t1", "t2"):
+                src, fac = ("t0", "g1") if step == "t1" else ("t1", "g2")
+                nc.vector.tensor_tensor(
+                    out=small(b, step, 8)[:], in0=st[b, src][:], in1=st[b, fac][:], op=ALU.mult
+                )
+            elif step == "lg":
+                nc.vector.scalar_tensor_tensor(
+                    out=st[b, "lg"][:],
+                    in0=st[b, "lg"][:],
+                    scalar=-3.0,
+                    in1=st[b, "t2"][:],
+                    op0=ALU.add,
+                    op1=ALU.add,
+                )
+            elif step == "aa":
+                nc.vector.tensor_tensor(
+                    out=small(b, "aa")[:], in0=st[b, "lg"][:, 0:4], in1=negm[b][:], op=ALU.subtract
+                )
+            elif step == "bb":
+                nc.vector.tensor_tensor(
+                    out=small(b, "bb")[:], in0=st[b, "mx"][:], in1=st[b, "lg"][:, 4:8], op=ALU.add
+                )
+            elif step == "z0":
+                nc.vector.tensor_tensor(out=z0, in0=z0, in1=st[b, "aa"][:], op=ALU.add)
+            elif step == "nc":
+                nc.vector.scalar_tensor_tensor(
+                    out=small(b, "negc")[:],
+                    in0=st[b, "aa"][:],
+                    scalar=-1.0,
+                    in1=st[b, "bb"][:],
+                    op0=ALU.mult,
+                    op1=ALU.subtract,
+                )
+
+        def finish(i):
+            b, n = divmod(i, 4)
+            z = zrow(i)
+            c = st[b, "negc"][:, n : n + 1]
+            if FIN[n] == "G":
+                nc.gpsimd.tensor_scalar(
+                    out=z, in0=z, scalar1=1.0, scalar2=c, op0=ALU.mult, op1=ALU.add
+                )
+            elif FIN[n] == "S":
+                nc.scalar.activation(out=z, in_=z, func=ACT.Identity, bias=c, scale=1.0)
+            else:
+                nc.vector.tensor_scalar(out=z, in0=z, scalar1=c, scalar2=None, op0=ALU.add)
+            nc.sync.dma_start(out=out_rows[i * P : (i + 1) * P, :], in_=z)
+
+        with tc.tile_pool(name="staging", bufs=1) as staging:
+            make_identity(nc, ident[:])
+            nc.vector.memset(warm[:], 0.0)
+            nc.vector.memset(one[:], 1.0)
+            nc.scalar.activation(out=warm2[:], in_=warm[:], func=ACT.Exp)
+            braw = staging.tile([P, 256], BF16, name="braw")
+            nc.vector.memset(braw[:], 0.0)
+            xin = staging.tile([P, 1536], BF16, name="xin")
+            we = staging.tile([P, 4096], BF16, name="we")
+            wd = staging.tile([P, 4096], BF16, name="wd")
+            wf = staging.tile([P, 8192], BF16, name="wf")
+            xg = staging.tile([P, 1536], BF16, name="xg", align_bytes=64)
+            weg = staging.tile([P, 4096], BF16, name="weg", align_bytes=64)
+            wdg = staging.tile([P, 4096], BF16, name="wdg", align_bytes=64)
+            wfg = [
+                staging.tile([P, 4096], BF16, name="wfg%d" % g, align_bytes=64) for g in range(2)
+            ]
+
+            nc.sync.dma_start(
+                out=xin[:, 0:1024].rearrange("p (r k) -> p r k", r=2),
+                in_=encoder_output.flatten_outer_dims().rearrange("(r p) k -> p r k", p=P),
+            )
+            nc.sync.dma_start(out=xin[:, 1024:1536], in_=decoder_output.flatten_outer_dims())
+            we_src = W_enc.rearrange("(c p e) k -> p c (e k)", c=4, p=P, e=2)
+            wd_src = W_dec.rearrange("(c p e) k -> p c (e k)", c=4, p=P, e=2)
+            we_dst = we[:].rearrange("p (c x) -> p c x", c=4)
+            wd_dst = wd[:].rearrange("p (c x) -> p c x", c=4)
+            nc.sync.dma_start(out=we_dst[:, 0:2, :], in_=we_src[:, 0:2, :])
+            nc.sync.dma_start(out=wd_dst[:, 0:2, :], in_=wd_src[:, 0:2, :])
+            nc.sync.dma_start(out=braw[0:4, :], in_=b_enc.rearrange("(c x) -> c x", c=4))
+            nc.sync.dma_start(out=braw[4:8, :], in_=b_dec.rearrange("(c x) -> c x", c=4))
+            nc.sync.dma_start(out=we_dst[:, 2:4, :], in_=we_src[:, 2:4, :])
+            nc.sync.dma_start(out=wd_dst[:, 2:4, :], in_=wd_src[:, 2:4, :])
+            wf_src = W_fc.rearrange("(r p) f -> p r f", p=P)
+            wf_dst = wf[:].rearrange("p (r f) -> p r f", r=8)
+            for r0 in range(0, 8, 2):
+                nc.sync.dma_start(out=wf_dst[:, r0 : r0 + 2, :], in_=wf_src[:, r0 : r0 + 2, :])
+            nc.sync.dma_start(out=bfc[:], in_=b_fc.partition_broadcast(P))
+
+            def turn(srcs, dst32, eng):
+                n = len(srcs) // 2
+                pt = psum.tile([P, 512], F32, name="pt", tag="bank")
+                for i, s in enumerate(srcs):
+                    nc.tensor.transpose(out=pt[:, i * P : (i + 1) * P], in_=s, identity=ident[:])
+                dst = dst32.rearrange("q (c r h) -> q c r h", c=n, h=2)
+                src = pt[:, 0 : n * 256].rearrange("q (c h r) -> q c r h", c=n, h=2)
+                if eng == "V":
+                    nc.vector.tensor_copy(out=dst, in_=src)
+                else:
+                    nc.scalar.copy(out=dst, in_=src)
+
+            def blocks(src32, first, count):
+                return [src32[:, (first + i) * P : (first + i + 1) * P] for i in range(count)]
+
+            xin32, xg32 = xin[:].bitcast(F32), xg[:].bitcast(F32)
+            turn(blocks(xin32, 0, 4), xg32[:, 0:512], "V")
+            turn(blocks(xin32, 4, 2), xg32[:, 512:768], "S")
+            nc.vector.quantize_mx(
+                out=xc[:, 0:256].bitcast(FP8X4), scales=xs[:, 0:256], in_=xg[:, 0:1024]
+            )
+            nc.vector.quantize_mx(
+                out=xc[:, 256:384].bitcast(FP8X4), scales=xs[:, 256:384], in_=xg[:, 1024:1536]
+            )
+
+            def weights(raw, grp, cod, sca, g):
+                r32, g32 = raw[:].bitcast(F32), grp[:].bitcast(F32)
+                turn(blocks(r32, g * 8, 4), g32[:, g * 1024 : g * 1024 + 512], "V")
+                turn(blocks(r32, g * 8 + 4, 4), g32[:, g * 1024 + 512 : g * 1024 + 1024], "S")
                 nc.vector.quantize_mx(
                     out=cod[:, g * 512 : (g + 1) * 512].bitcast(FP8X4),
                     scales=sca[:, g * 512 : (g + 1) * 512],
                     in_=grp[:, g * 2048 : (g + 1) * 2048],
                 )
-            for r in range(3):
-                cod, sca = (wec, wes) if r < 2 else (wdc, wds)
-                ps = psum.tile([P, 512], F32, name="ps", tag="bank")
-                for j in range(4):
-                    c0 = (g * 4 + j) * P
-                    nc.tensor.matmul_mx(
-                        out=ps[:, j * P : (j + 1) * P],
-                        lhsT=cod[:, c0 : c0 + P].bitcast(FP8X4),
-                        lhsT_scale=sca[:, c0 : c0 + P],
-                        rhs=xc[:, r * P : (r + 1) * P].bitcast(FP8X4),
-                        rhs_scale=xs[:, r * P : (r + 1) * P],
-                        start=True,
-                        stop=True,
-                    )
-                ps_wj = ps[:].rearrange("p (j w) -> p w j", j=4)
-                if r < 2:
-                    nc.vector.tensor_tensor(
-                        out=enc_v[:, g, r * P : (r + 1) * P, :],
-                        in0=ps_wj,
-                        in1=bsum[:, g * 4 : (g + 1) * 4].unsqueeze(1).to_broadcast([P, P, 4]),
-                        op=ALU.add,
-                    )
-                else:
-                    nc.scalar.copy(out=dec_v[:, g, :, :], in_=ps_wj)
 
-        wfc = const.tile([P, 2048], U32, name="wfc", align_bytes=64)
-        wfs = const.tile([P, 2048], U8, name="wfs", align_bytes=64)
-        wf32 = wf[:].bitcast(F32).rearrange("p (r g x) -> p r g x", r=8, g=2)
-        for g in range(2):
-            wfg = const.tile([P, 4096], BF16, name="wfg%d" % g, align_bytes=64)
-            wfg32 = wfg[:].bitcast(F32)
-            for r0 in range(0, 8, 2):
-                pt = psum.tile([P, 512], F32, name="ptf", tag="bank")
-                for c in range(2):
-                    for h in range(2):
-                        i = c * 2 + h
-                        nc.tensor.transpose(
-                            out=pt[:, i * P : (i + 1) * P],
-                            in_=wf32[:, r0 + c, g, h * P : (h + 1) * P],
-                            identity=ident[:],
-                        )
-                evacuate(
-                    wfg32[:, r0 * 256 : (r0 + 2) * 256].rearrange(
-                        "q (c r h) -> q c r h", c=2, h=2
-                    ),
-                    pt[:].rearrange("q (c h r) -> q c r h", c=2, h=2),
-                )
-            nc.vector.quantize_mx(
-                out=wfc[:, g * 1024 : (g + 1) * 1024].bitcast(FP8X4),
-                scales=wfs[:, g * 1024 : (g + 1) * 1024],
-                in_=wfg[:],
-            )
-
-        for b in range(B):
-            hc, hs = [], []
-            for g in range(2):
-                comb = work.tile([P, 2048], F32, name="comb", tag="comb")
-                add_eng = nc.vector if (b == 0 and g == 0) else nc.gpsimd
-                add_eng.tensor_tensor(
-                    out=comb[:].rearrange("p (t u j) -> p t u j", t=T, u=U),
-                    in0=enc_v[:, g, b * T : (b + 1) * T, :].unsqueeze(2).to_broadcast([P, T, U, 4]),
-                    in1=dec_v[:, g, b * U : (b + 1) * U, :].unsqueeze(1).to_broadcast([P, T, U, 4]),
-                    op=ALU.add,
-                )
-                h = work.tile([P, 2048], BF16, name="h", tag="h", align_bytes=64)
-                nc.scalar.activation(out=h[:], in_=comb[:], func=ACT.Tanh)
-                hcg = codes.tile([P, 512], U32, name="hc", tag="hc", align_bytes=64)
-                hsg = codes.tile([P, 512], U8, name="hs", tag="hs", align_bytes=64)
-                nc.vector.quantize_mx(out=hcg[:].bitcast(FP8X4), scales=hsg[:], in_=h[:])
-                hc.append(hcg)
-                hs.append(hsg)
-
-            zb = zpool.tile([P, 4 * V], F32, name="zb", tag="zb")
-            zv = zb[:].rearrange("p (n v) -> p n v", n=4)
-            z0 = zv[:, :, 0]
-            negm = stat.tile([P, 4], F32, name="negm", tag="negm")
-            xx = stat.tile([P, 16], F32, name="xx", tag="xx")
-            for n in range(4):
-                ys = [psum.tile([P, 512], F32, name="y%d" % v, tag="bank") for v in range(2)]
-                for g in range(2):
-                    for v in range(2):
-                        c0 = g * 1024 + v * 512
+            def project(g):
+                for r in range(3):
+                    cod, sca = (wec, wes) if r < 2 else (wdc, wds)
+                    ps = psum.tile([P, 512], F32, name="ps", tag="bank")
+                    for j in range(4):
+                        c0 = (g * 4 + j) * P
                         nc.tensor.matmul_mx(
-                            out=ys[v][:],
-                            lhsT=hc[g][:, n * P : (n + 1) * P].bitcast(FP8X4),
-                            lhsT_scale=hs[g][:, n * P : (n + 1) * P],
-                            rhs=wfc[:, c0 : c0 + 512].bitcast(FP8X4),
-                            rhs_scale=wfs[:, c0 : c0 + 512],
-                            start=(g == 0),
-                            stop=(g == 1),
+                            out=ps[:, j * P : (j + 1) * P],
+                            lhsT=cod[:, c0 : c0 + P].bitcast(FP8X4),
+                            lhsT_scale=sca[:, c0 : c0 + P],
+                            rhs=xc[:, r * P : (r + 1) * P].bitcast(FP8X4),
+                            rhs_scale=xs[:, r * P : (r + 1) * P],
+                            start=True,
+                            stop=True,
                         )
-                for v in range(2):
-                    nc.vector.tensor_tensor(
-                        out=zv[:, n, v * 512 : (v + 1) * 512],
-                        in0=ys[v][:],
-                        in1=bfc[:, v * 512 : (v + 1) * 512],
-                        op=ALU.add,
-                    )
-                nc.vector.tensor_reduce(
-                    out=negm[:, n : n + 1], in_=zv[:, n, 1:V], axis=AX.X, op=ALU.max, negate=True
-                )
-                junk = work.tile([P, V], BF16, name="junk", tag="junk")
-                nc.scalar.activation(
-                    out=junk[:, 0 : V - 1],
-                    in_=zv[:, n, 1:V],
-                    func=ACT.Exp,
-                    bias=negm[:, n : n + 1],
-                    scale=1.0,
-                    accum_out=xx[:, n : n + 1],
+                    ps_wj = ps[:].rearrange("p (j w) -> p w j", j=4)
+                    if r < 2:
+                        nc.scalar.copy(out=enc_v[:, g, r * P : (r + 1) * P, :], in_=ps_wj)
+                    else:
+                        nc.vector.tensor_tensor(
+                            out=dec_v[:, g, :, :],
+                            in0=ps_wj,
+                            in1=bsum[:, g * 4 : (g + 1) * 4].unsqueeze(1).to_broadcast([P, P, 4]),
+                            op=ALU.add,
+                        )
+
+            wf32 = wf[:].bitcast(F32).rearrange("p (r g x) -> p r g x", r=8, g=2)
+
+            def fc_weights(r0, g, eng):
+                srcs = [wf32[:, r0 + c, g, h * P : (h + 1) * P] for c in range(2) for h in range(2)]
+                turn(srcs, wfg[g][:].bitcast(F32)[:, r0 * 256 : (r0 + 2) * 256], eng)
+
+            def fc_quant(g, half):
+                c0 = g * 1024 + half * 512
+                nc.vector.quantize_mx(
+                    out=wfc[:, c0 : c0 + 512].bitcast(FP8X4),
+                    scales=wfs[:, c0 : c0 + 512],
+                    in_=wfg[g][:, half * 2048 : (half + 1) * 2048],
                 )
 
-            mx = stat.tile([P, 4], F32, name="mx", tag="mx")
-            nc.vector.tensor_scalar(out=mx[:], in0=z0, scalar1=0.0, scalar2=None, op0=ALU.max)
-            na = stat.tile([P, 4], F32, name="na", tag="na")
-            nc.vector.scalar_tensor_tensor(
-                out=na[:], in0=mx[:], scalar=-2.0, in1=z0, op0=ALU.mult, op1=ALU.add
-            )
-            ev = stat.tile([P, 4], F32, name="ev", tag="ev")
-            nc.scalar.activation(out=ev[:], in_=na[:], func=ACT.Exp)
-            nc.vector.tensor_scalar(
-                out=xx[:, 8:12], in0=ev[:], scalar1=1.0, scalar2=None, op0=ALU.add
-            )
-            xv = xx[:].rearrange("p (a c) -> p a c", a=2)[:, :, 0:4]
-            xi = xx[:].bitcast(I32).rearrange("p (a c) -> p a c", a=2)[:, :, 0:4]
-            lg = stat.tile([P, 8], F32, name="lg", tag="lg")
-            lgv = lg[:].rearrange("p (a c) -> p a c", a=2)
-            nc.vector.tensor_scalar(
-                out=lgv, in0=xi, scalar1=K1, scalar2=K2, op0=ALU.mult, op1=ALU.add
-            )
-            for it in range(NEWTON):
-                en = stat.tile([P, 8], F32, name="en", tag="en")
-                nc.scalar.activation(out=en[:], in_=lg[:], func=ACT.Exp, scale=-1.0)
-                tn = stat.tile([P, 8], F32, name="tn", tag="tn")
-                nc.vector.tensor_tensor(
-                    out=tn[:].rearrange("p (a c) -> p a c", a=2),
-                    in0=en[:].rearrange("p (a c) -> p a c", a=2),
-                    in1=xv,
-                    op=ALU.mult,
-                )
-                nc.vector.scalar_tensor_tensor(
-                    out=lg[:], in0=lg[:], scalar=-1.0, in1=tn[:], op0=ALU.add, op1=ALU.add
-                )
-            aa = stat.tile([P, 4], F32, name="aa", tag="aa")
-            nc.vector.tensor_tensor(out=aa[:], in0=lg[:, 0:4], in1=negm[:], op=ALU.subtract)
-            nc.vector.tensor_tensor(out=z0, in0=z0, in1=aa[:], op=ALU.add)
-            bb = stat.tile([P, 4], F32, name="bb", tag="bb")
-            nc.vector.tensor_tensor(out=bb[:], in0=mx[:], in1=lg[:, 4:8], op=ALU.add)
-            negc = stat.tile([P, 4], F32, name="negc", tag="negc")
-            nc.vector.scalar_tensor_tensor(
-                out=negc[:], in0=aa[:], scalar=-1.0, in1=bb[:], op0=ALU.mult, op1=ALU.subtract
-            )
+            weights(we, weg, wec, wes, 0)
+            weights(wd, wdg, wdc, wds, 0)
+            ptb = psum.tile([P, 512], F32, name="ptb", tag="bank")
+            nc.tensor.transpose(out=ptb[:, 0:P], in_=braw[:].bitcast(F32), identity=ident[:])
+            nc.vector.tensor_copy(out=bT[:], in_=ptb[:, 0:8])
+            bT16 = bT[:].bitcast(BF16)
+            nc.vector.tensor_tensor(out=bsum[:], in0=bT16[:, 0:8], in1=bT16[:, 8:16], op=ALU.add)
+            weights(we, weg, wec, wes, 1)
+            project(0)
+            add(0, 0, nc.gpsimd, 0, 16)
+            add(0, 0, nc.gpsimd, 16, 32)
+            weights(wd, wdg, wdc, wds, 1)
+            fc_weights(0, 0, "S")
+            fc_weights(0, 1, "S")
+            project(1)
+            add(0, 1, nc.vector, 0, 16)
+            add(0, 1, nc.gpsimd, 16, 32)
+            fc_weights(2, 0, "V")
+            tanh(0, 0, 0, 16)
+            tanh(0, 1, 0, 16)
+            fc_weights(2, 1, "S")
+            fc_quant(0, 0)
+            quant(0, 0, 0, 16)
+            fc_quant(1, 0)
+            quant(0, 1, 0, 16)
+            add(1, 0, nc.gpsimd)
+            fc_weights(4, 0, "S")
+            fc_weights(4, 1, "S")
+            fc_weights(6, 0, "V")
+            fc_weights(6, 1, "S")
+            fc_quant(0, 1)
+            fc_quant(1, 1)
+            matmul(0)
+            tanh(0, 0, 16, 32)
+            tanh(0, 1, 16, 32)
+            add(1, 1, nc.gpsimd)
+            quant(0, 0, 16, 32)
+            quant(0, 1, 16, 32)
 
+        zpool = ctx.enter_context(tc.tile_pool(name="zpool", bufs=5))
+
+        def on(b, step):
+            if 0 <= b < B:
+                chain(b, step)
+
+        def tile_ok(i):
+            return 0 <= i < 4 * B
+
+        def esum(i):
+            if tile_ok(i):
+                exp_sum(i)
+
+        def badd(i, v):
+            if tile_ok(i):
+                bias_add(i, v)
+
+        def rmax(i):
+            if tile_ok(i):
+                row_max(i)
+
+        for u in range(0, B + 3):
+            fin = [4 * (u - 2) + n for n in range(4)] if 0 <= u - 2 < B else []
+            fin_g = [i for i in fin if FIN[i % 4] == "G"]
+            fin_s = [i for i in fin if FIN[i % 4] == "S"]
+            fin_v = [i for i in fin if FIN[i % 4] == "V"]
+            if u < B:
+                zbt[u] = zpool.tile([P, 4 * V], F32, name="zb", tag="zb")
+                negm[u] = stat.tile([P, 4], F32, name="negm", tag="negm")
+                xx[u] = stat.tile([P, 16], F32, name="xx", tag="xx")
+            c1, c2 = u - 1, u - 2
             for n in range(4):
-                if n % 2 == 0:
-                    nc.gpsimd.tensor_scalar(
-                        out=zv[:, n, :],
-                        in0=zv[:, n, :],
-                        scalar1=1.0,
-                        scalar2=negc[:, n : n + 1],
-                        op0=ALU.mult,
-                        op1=ALU.add,
-                    )
+                i = 4 * u + n
+                if n == 0:
+                    if u + 2 < B:
+                        add(u + 2, 0, nc.gpsimd)
+                    esum(i - 2)
+                    on(c1, "ab")
+                    if u + 1 < B:
+                        tanh(u + 1, 0)
+                    on(c1, "ev")
+                    badd(i, 0)
+                    on(c2, "lg")
+                    badd(i, 1)
+                    on(c2, "aa")
+                    rmax(i - 1)
+                    on(c2, "bb")
+                    on(c2, "z0")
+                    on(c2, "nc")
+                elif n == 1:
+                    for k in fin_g[:1]:
+                        finish(k)
+                    esum(i - 2)
+                    on(c1, "q")
+                    on(c1, "mx")
+                    if u + 1 < B:
+                        tanh(u + 1, 1)
+                    badd(i, 0)
+                    badd(i, 1)
+                    rmax(i - 1)
+                    if u + 1 < B:
+                        quant(u + 1, 0)
+                    for k in fin_v:
+                        finish(k)
+                elif n == 2:
+                    if u + 2 < B:
+                        add(u + 2, 1, nc.gpsimd)
+                    badd(i, 0)
+                    on(c1, "x0")
+                    on(c1, "e0")
+                    esum(i - 2)
+                    badd(i, 1)
+                    rmax(i - 1)
+                    on(c1, "t0")
+                    on(c1, "g1")
+                    for k in fin_s[:1]:
+                        finish(k)
+                    if u + 1 < B:
+                        quant(u + 1, 1)
+                    on(c1, "a1")
                 else:
-                    nc.scalar.activation(
-                        out=zv[:, n, :],
-                        in_=zv[:, n, :],
-                        func=ACT.Identity,
-                        bias=negc[:, n : n + 1],
-                        scale=1.0,
-                    )
-                r0 = (b * 4 + n) * P
-                nc.sync.dma_start(out=out_rows[r0 : r0 + P, :], in_=zv[:, n, :])
+                    for k in fin_g[1:]:
+                        finish(k)
+                    badd(i, 0)
+                    on(c1, "t1")
+                    esum(i - 2)
+                    on(c1, "g2")
+                    badd(i, 1)
+                    on(c1, "a2")
+                    rmax(i - 1)
+                    on(c1, "t2")
+                    for k in fin_s[1:]:
+                        finish(k)
+                if tile_ok(i + 1):
+                    matmul(i + 1)

@@ -34,7 +34,7 @@ def tile_jointnet_kernel(
         const = ctx.enter_context(tc.tile_pool(name="const", bufs=1))
         work = ctx.enter_context(tc.tile_pool(name="work", bufs=4))
         stat = ctx.enter_context(tc.tile_pool(name="stat", bufs=4))
-        psum = ctx.enter_context(tc.psum_pool(name="psum", bufs=8))
+        psum = ctx.enter_context(tc.psum_pool(name="psum", bufs=6))
 
         xc = const.tile([P, 384], U32, name="xc", align_bytes=64)
         xs = const.tile([P, 384], U8, name="xs", align_bytes=64)
@@ -56,8 +56,16 @@ def tile_jointnet_kernel(
         enc_v = encT[:].rearrange("p (g w j) -> p g w j", g=2, j=4)
         dec_v = decT[:].rearrange("p (g w j) -> p g w j", g=2, j=4)
 
-        comb, hid, hc, hs = {}, {}, {}, {}
+        comb, hid, hc, hs, dec_ps = {}, {}, {}, {}, {}
         ybank, zbt, negm, xx, st = {}, {}, {}, {}, {}
+
+        def dec_slice(b, g):
+            nc.vector.tensor_tensor(
+                out=dec_v[:, g, b * U : (b + 1) * U, :],
+                in0=dec_ps[g][:, b * U : (b + 1) * U, :],
+                in1=bsum[:, g * 4 : (g + 1) * 4].unsqueeze(1).to_broadcast([P, U, 4]),
+                op=ALU.add,
+            )
 
         def add(b, g, eng, t0=0, t1=T):
             if t0 == 0:
@@ -71,20 +79,22 @@ def tile_jointnet_kernel(
             )
 
         def tanh(b, g, t0=0, t1=T):
-            if t0 == 0:
-                hid[b, g] = work.tile([P, 2048], BF16, name="hid", tag="hid", align_bytes=64)
+            if g == 0 and t0 == 0:
+                hid[b] = work.tile([P, 4096], BF16, name="hid", tag="hid", align_bytes=64, bufs=2)
             nc.scalar.activation(
-                out=hid[b, g][:, t0 * 64 : t1 * 64], in_=comb[b, g][:, t0 * 64 : t1 * 64], func=ACT.Tanh
+                out=hid[b][:, g * 2048 + t0 * 64 : g * 2048 + t1 * 64],
+                in_=comb[b, g][:, t0 * 64 : t1 * 64],
+                func=ACT.Tanh,
             )
 
-        def quant(b, g, t0=0, t1=T):
-            if t0 == 0:
-                hc[b, g] = work.tile([P, 512], U32, name="hc", tag="hc", align_bytes=64)
-                hs[b, g] = work.tile([P, 512], U8, name="hs", tag="hs", align_bytes=64)
+        def quant(b, c0=0, c1=4096):
+            if c0 == 0:
+                hc[b] = work.tile([P, 1024], U32, name="hc", tag="hc", align_bytes=64, bufs=2)
+                hs[b] = work.tile([P, 1024], U8, name="hs", tag="hs", align_bytes=64, bufs=2)
             nc.vector.quantize_mx(
-                out=hc[b, g][:, t0 * 16 : t1 * 16].bitcast(FP8X4),
-                scales=hs[b, g][:, t0 * 16 : t1 * 16],
-                in_=hid[b, g][:, t0 * 64 : t1 * 64],
+                out=hc[b][:, c0 // 4 : c1 // 4].bitcast(FP8X4),
+                scales=hs[b][:, c0 // 4 : c1 // 4],
+                in_=hid[b][:, c0:c1],
             )
 
         def matmul(i):
@@ -96,8 +106,8 @@ def tile_jointnet_kernel(
                     c0 = g * 1024 + v * 512
                     nc.tensor.matmul_mx(
                         out=ybank[i, v][:],
-                        lhsT=hc[b, g][:, n * P : (n + 1) * P].bitcast(FP8X4),
-                        lhsT_scale=hs[b, g][:, n * P : (n + 1) * P],
+                        lhsT=hc[b][:, g * 512 + n * P : g * 512 + (n + 1) * P].bitcast(FP8X4),
+                        lhsT_scale=hs[b][:, g * 512 + n * P : g * 512 + (n + 1) * P],
                         rhs=wfc[:, c0 : c0 + 512].bitcast(FP8X4),
                         rhs_scale=wfs[:, c0 : c0 + 512],
                         start=(g == 0),
@@ -173,18 +183,18 @@ def tile_jointnet_kernel(
                 nc.vector.tensor_tensor(
                     out=two(small(b, "t0", 8)[:]), in0=two(st[b, "e0"][:]), in1=xv, op=ALU.mult
                 )
-            elif step in ("g1", "g2"):
-                src = "t0" if step == "g1" else "t1"
+            elif step in ("g1", "g2", "g3"):
+                src = "t%d" % (int(step[1]) - 1)
                 nc.scalar.activation(
                     out=small(b, step, 8)[:], in_=st[b, src][:], func=ACT.Exp, bias=one[:], scale=-1.0
                 )
-            elif step in ("a1", "a2"):
-                src = "t0" if step == "a1" else "t1"
+            elif step in ("a1", "a2", "a3"):
+                src = "t%d" % (int(step[1]) - 1)
                 nc.vector.tensor_tensor(
                     out=st[b, "lg"][:], in0=st[b, "lg"][:], in1=st[b, src][:], op=ALU.add
                 )
-            elif step in ("t1", "t2"):
-                src, fac = ("t0", "g1") if step == "t1" else ("t1", "g2")
+            elif step in ("t1", "t2", "t3"):
+                src, fac = "t%d" % (int(step[1]) - 1), "g" + step[1]
                 nc.vector.tensor_tensor(
                     out=small(b, step, 8)[:], in0=st[b, src][:], in1=st[b, fac][:], op=ALU.mult
                 )
@@ -192,8 +202,8 @@ def tile_jointnet_kernel(
                 nc.vector.scalar_tensor_tensor(
                     out=st[b, "lg"][:],
                     in0=st[b, "lg"][:],
-                    scalar=-3.0,
-                    in1=st[b, "t2"][:],
+                    scalar=-4.0,
+                    in1=st[b, "t3"][:],
                     op0=ALU.add,
                     op1=ALU.add,
                 )
@@ -305,31 +315,28 @@ def tile_jointnet_kernel(
                     in_=grp[:, g * 2048 : (g + 1) * 2048],
                 )
 
-            def project(g):
-                for r in range(3):
-                    cod, sca = (wec, wes) if r < 2 else (wdc, wds)
+            def project(g, r):
+                cod, sca = (wec, wes) if r < 2 else (wdc, wds)
+                if r < 2:
                     ps = psum.tile([P, 512], F32, name="ps", tag="bank")
-                    for j in range(4):
-                        c0 = (g * 4 + j) * P
-                        nc.tensor.matmul_mx(
-                            out=ps[:, j * P : (j + 1) * P],
-                            lhsT=cod[:, c0 : c0 + P].bitcast(FP8X4),
-                            lhsT_scale=sca[:, c0 : c0 + P],
-                            rhs=xc[:, r * P : (r + 1) * P].bitcast(FP8X4),
-                            rhs_scale=xs[:, r * P : (r + 1) * P],
-                            start=True,
-                            stop=True,
-                        )
-                    ps_wj = ps[:].rearrange("p (j w) -> p w j", j=4)
-                    if r < 2:
-                        nc.scalar.copy(out=enc_v[:, g, r * P : (r + 1) * P, :], in_=ps_wj)
-                    else:
-                        nc.vector.tensor_tensor(
-                            out=dec_v[:, g, :, :],
-                            in0=ps_wj,
-                            in1=bsum[:, g * 4 : (g + 1) * 4].unsqueeze(1).to_broadcast([P, P, 4]),
-                            op=ALU.add,
-                        )
+                else:
+                    ps = psum.tile([P, 512], F32, name="psd", tag="dec", bufs=2)
+                for j in range(4):
+                    c0 = (g * 4 + j) * P
+                    nc.tensor.matmul_mx(
+                        out=ps[:, j * P : (j + 1) * P],
+                        lhsT=cod[:, c0 : c0 + P].bitcast(FP8X4),
+                        lhsT_scale=sca[:, c0 : c0 + P],
+                        rhs=xc[:, r * P : (r + 1) * P].bitcast(FP8X4),
+                        rhs_scale=xs[:, r * P : (r + 1) * P],
+                        start=True,
+                        stop=True,
+                    )
+                ps_wj = ps[:].rearrange("p (j w) -> p w j", j=4)
+                if r < 2:
+                    nc.scalar.copy(out=enc_v[:, g, r * P : (r + 1) * P, :], in_=ps_wj)
+                else:
+                    dec_ps[g] = ps_wj
 
             wf32 = wf[:].bitcast(F32).rearrange("p (r g x) -> p r g x", r=8, g=2)
 
@@ -353,36 +360,39 @@ def tile_jointnet_kernel(
             bT16 = bT[:].bitcast(BF16)
             nc.vector.tensor_tensor(out=bsum[:], in0=bT16[:, 0:8], in1=bT16[:, 8:16], op=ALU.add)
             weights(we, weg, wec, wes, 1)
-            project(0)
-            add(0, 0, nc.gpsimd, 0, 16)
-            add(0, 0, nc.gpsimd, 16, 32)
+            project(0, 2)
+            project(0, 0)
             weights(wd, wdg, wdc, wds, 1)
             fc_weights(0, 0, "S")
             fc_weights(0, 1, "S")
-            project(1)
-            add(0, 1, nc.vector, 0, 16)
-            add(0, 1, nc.gpsimd, 16, 32)
-            fc_weights(2, 0, "V")
-            tanh(0, 0, 0, 16)
-            tanh(0, 1, 0, 16)
+            fc_weights(2, 0, "S")
+            dec_slice(0, 0)
+            add(0, 0, nc.vector)
+            project(1, 2)
+            project(1, 0)
             fc_weights(2, 1, "S")
             fc_quant(0, 0)
-            quant(0, 0, 0, 16)
-            fc_quant(1, 0)
-            quant(0, 1, 0, 16)
-            add(1, 0, nc.gpsimd)
+            tanh(0, 0)
+            dec_slice(0, 1)
+            add(0, 1, nc.vector)
             fc_weights(4, 0, "S")
-            fc_weights(4, 1, "S")
+            fc_quant(1, 0)
+            tanh(0, 1)
+            fc_weights(4, 1, "V")
             fc_weights(6, 0, "V")
-            fc_weights(6, 1, "S")
+            fc_weights(6, 1, "V")
+            dec_slice(1, 0)
+            add(1, 0, nc.vector)
             fc_quant(0, 1)
             fc_quant(1, 1)
+            quant(0)
             matmul(0)
-            tanh(0, 0, 16, 32)
-            tanh(0, 1, 16, 32)
+            dec_slice(1, 1)
+            dec_slice(2, 0)
             add(1, 1, nc.gpsimd)
-            quant(0, 0, 16, 32)
-            quant(0, 1, 16, 32)
+            add(2, 0, nc.gpsimd)
+            project(0, 1)
+            project(1, 1)
 
         zpool = ctx.enter_context(tc.tile_pool(name="zpool", bufs=5))
 
@@ -406,7 +416,8 @@ def tile_jointnet_kernel(
                 row_max(i)
 
         for u in range(0, B + 3):
-            fin = [4 * (u - 2) + n for n in range(4)] if 0 <= u - 2 < B else []
+            c1, c2 = u - 1, u - 2
+            fin = [4 * c2 + n for n in range(4)] if 0 <= c2 < B else []
             fin_g = [i for i in fin if FIN[i % 4] == "G"]
             fin_s = [i for i in fin if FIN[i % 4] == "S"]
             fin_v = [i for i in fin if FIN[i % 4] == "V"]
@@ -414,17 +425,27 @@ def tile_jointnet_kernel(
                 zbt[u] = zpool.tile([P, 4 * V], F32, name="zb", tag="zb")
                 negm[u] = stat.tile([P, 4], F32, name="negm", tag="negm")
                 xx[u] = stat.tile([P, 16], F32, name="xx", tag="xx")
-            c1, c2 = u - 1, u - 2
             for n in range(4):
                 i = 4 * u + n
                 if n == 0:
-                    if u + 2 < B:
-                        add(u + 2, 0, nc.gpsimd)
+                    badd(i, 0)
+                    on(c2, "t2")
                     esum(i - 2)
+                    on(c2, "g3")
                     on(c1, "ab")
                     if u + 1 < B:
                         tanh(u + 1, 0)
                     on(c1, "ev")
+                    badd(i, 1)
+                    on(c2, "a3")
+                    rmax(i - 1)
+                    on(c2, "t3")
+                elif n == 1:
+                    esum(i - 2)
+                    on(c1, "q")
+                    on(c1, "mx")
+                    if u + 1 < B:
+                        tanh(u + 1, 1)
                     badd(i, 0)
                     on(c2, "lg")
                     badd(i, 1)
@@ -432,25 +453,7 @@ def tile_jointnet_kernel(
                     rmax(i - 1)
                     on(c2, "bb")
                     on(c2, "z0")
-                    on(c2, "nc")
-                elif n == 1:
-                    for k in fin_g[:1]:
-                        finish(k)
-                    esum(i - 2)
-                    on(c1, "q")
-                    on(c1, "mx")
-                    if u + 1 < B:
-                        tanh(u + 1, 1)
-                    badd(i, 0)
-                    badd(i, 1)
-                    rmax(i - 1)
-                    if u + 1 < B:
-                        quant(u + 1, 0)
-                    for k in fin_v:
-                        finish(k)
                 elif n == 2:
-                    if u + 2 < B:
-                        add(u + 2, 1, nc.gpsimd)
                     badd(i, 0)
                     on(c1, "x0")
                     on(c1, "e0")
@@ -459,22 +462,32 @@ def tile_jointnet_kernel(
                     rmax(i - 1)
                     on(c1, "t0")
                     on(c1, "g1")
+                    if u + 1 < B:
+                        quant(u + 1)
+                    on(c2, "nc")
+                    for k in fin_v:
+                        finish(k)
+                    if u + 2 < B:
+                        dec_slice(u + 2, 1)
+                    if u + 3 < B:
+                        dec_slice(u + 3, 0)
+                    if u + 2 < B:
+                        add(u + 2, 1, nc.gpsimd)
+                    if u + 3 < B:
+                        add(u + 3, 0, nc.gpsimd)
+                    for k in fin_g:
+                        finish(k)
                     for k in fin_s[:1]:
                         finish(k)
-                    if u + 1 < B:
-                        quant(u + 1, 1)
-                    on(c1, "a1")
                 else:
-                    for k in fin_g[1:]:
-                        finish(k)
                     badd(i, 0)
+                    on(c1, "a1")
+                    badd(i, 1)
                     on(c1, "t1")
                     esum(i - 2)
                     on(c1, "g2")
-                    badd(i, 1)
-                    on(c1, "a2")
                     rmax(i - 1)
-                    on(c1, "t2")
+                    on(c1, "a2")
                     for k in fin_s[1:]:
                         finish(k)
                 if tile_ok(i + 1):

@@ -19,7 +19,8 @@ FLOPS = 2 * (256 * 512 * 1024 + 128 * 512 * 1024 + 4096 * 1024 * 1024)
 
 LN2 = 0.6931471805599453
 K1 = LN2 / 8388608.0
-C0 = (0.043 - 127.0) * 8388608.0
+STEPS = 4
+C0 = (0.043 - 127.0) * 8388608.0 - STEPS / K1
 
 FIN = ("G", "S", "G", "S")
 
@@ -53,6 +54,7 @@ def tile_jointnet_kernel(
         warm = const.tile([P, 8], F32, name="warm")
         warm2 = const.tile([P, 8], F32, name="warm2")
         one = const.tile([P, 1], F32, name="one")
+        shift = const.tile([P, 1], F32, name="shift")
         enc_v = encT[:].rearrange("p (g w j) -> p g w j", g=2, j=4)
         dec_v = decT[:].rearrange("p (g w j) -> p g w j", g=2, j=4)
 
@@ -60,21 +62,17 @@ def tile_jointnet_kernel(
         ybank, zbt, negm, xx, st = {}, {}, {}, {}, {}
 
         def dec_slice(b, g):
-            nc.vector.tensor_tensor(
-                out=dec_v[:, g, b * U : (b + 1) * U, :],
-                in0=dec_ps[g][:, b * U : (b + 1) * U, :],
-                in1=bsum[:, g * 4 : (g + 1) * 4].unsqueeze(1).to_broadcast([P, U, 4]),
-                op=ALU.add,
+            nc.vector.tensor_copy(
+                out=dec_v[:, g, b * U : (b + 1) * U, :], in_=dec_ps[g][:, b * U : (b + 1) * U, :]
             )
 
-        def add(b, g, eng, t0=0, t1=T):
-            if t0 == 0:
-                comb[b, g] = work.tile([P, 2048], F32, name="comb", tag="comb")
-            nt = t1 - t0
-            eng.tensor_tensor(
-                out=comb[b, g][:, t0 * 64 : t1 * 64].rearrange("p (t u j) -> p t u j", t=nt, u=U),
-                in0=enc_v[:, g, b * T + t0 : b * T + t1, :].unsqueeze(2).to_broadcast([P, nt, U, 4]),
-                in1=dec_v[:, g, b * U : (b + 1) * U, :].unsqueeze(1).to_broadcast([P, nt, U, 4]),
+        def add(b, g, eng):
+            comb[b, g] = work.tile([P, 2048], F32, name="comb", tag="comb")
+            dec = dec_ps[g] if eng == "V" else dec_v[:, g, :, :]
+            (nc.vector if eng == "V" else nc.gpsimd).tensor_tensor(
+                out=comb[b, g][:].rearrange("p (t u j) -> p t u j", t=T, u=U),
+                in0=enc_v[:, g, b * T : (b + 1) * T, :].unsqueeze(2).to_broadcast([P, T, U, 4]),
+                in1=dec[:, b * U : (b + 1) * U, :].unsqueeze(1).to_broadcast([P, T, U, 4]),
                 op=ALU.add,
             )
 
@@ -153,9 +151,19 @@ def tile_jointnet_kernel(
 
         def chain(b, step):
             z0 = zbt[b][:].rearrange("p (n v) -> p n v", n=4)[:, :, 0]
-            xv = two(xx[b][:])[:, :, 0:4]
+            if step == "ab":
+                st[b, "w"] = stat.tile([P, 40], F32, name="w", tag="w")
+                st[b, "tt"] = stat.tile([P, 8 * (STEPS + 1)], F32, name="tt", tag="tt")
+            wv = st[b, "w"][:].rearrange("p (k c) -> p k c", c=8)
+            tv = st[b, "tt"][:].rearrange("p (k c) -> p k c", c=8)
             if step == "ab":
                 nc.scalar.activation(out=small(b, "ab")[:], in_=z0, func=ACT.Abs)
+            elif step == "zc":
+                nc.scalar.activation(out=wv[:, 0, 0:4], in_=z0, func=ACT.Identity)
+            elif step == "mc":
+                nc.scalar.activation(out=wv[:, 1, 0:4], in_=negm[b][:], func=ACT.Identity, scale=-1.0)
+            elif step == "mx":
+                nc.scalar.activation(out=wv[:, 4, 0:4], in_=z0, func=ACT.Relu)
             elif step == "ev":
                 nc.scalar.activation(
                     out=small(b, "ev")[:], in_=st[b, "ab"][:], func=ACT.Exp, scale=-1.0
@@ -164,67 +172,54 @@ def tile_jointnet_kernel(
                 nc.scalar.activation(
                     out=xx[b][:, 8:12], in_=st[b, "ev"][:], func=ACT.Identity, bias=one[:], scale=1.0
                 )
-            elif step == "mx":
-                nc.scalar.activation(out=small(b, "mx")[:], in_=z0, func=ACT.Relu)
             elif step == "x0":
                 nc.vector.tensor_scalar(
-                    out=two(small(b, "lg", 8)[:]),
+                    out=two(tv[:, 0, :]),
                     in0=two(xx[b][:].bitcast(I32))[:, :, 0:4],
                     scalar1=C0,
                     scalar2=K1,
                     op0=ALU.add,
                     op1=ALU.mult,
                 )
-            elif step == "e0":
+            elif step == "g0":
                 nc.scalar.activation(
-                    out=small(b, "e0", 8)[:], in_=st[b, "lg"][:], func=ACT.Exp, scale=-1.0
+                    out=small(b, "g0", 8)[:], in_=tv[:, 0, :], func=ACT.Exp, bias=shift[:], scale=-1.0
                 )
             elif step == "t0":
-                nc.vector.tensor_tensor(
-                    out=two(small(b, "t0", 8)[:]), in0=two(st[b, "e0"][:]), in1=xv, op=ALU.mult
+                nc.gpsimd.tensor_tensor(
+                    out=two(tv[:, 1, :]),
+                    in0=two(st[b, "g0"][:]),
+                    in1=two(xx[b][:])[:, :, 0:4],
+                    op=ALU.mult,
                 )
-            elif step in ("g1", "g2", "g3"):
-                src = "t%d" % (int(step[1]) - 1)
+            elif step[0] == "g":
+                k = int(step[1])
                 nc.scalar.activation(
-                    out=small(b, step, 8)[:], in_=st[b, src][:], func=ACT.Exp, bias=one[:], scale=-1.0
+                    out=small(b, step, 8)[:], in_=tv[:, k, :], func=ACT.Exp, bias=one[:], scale=-1.0
                 )
-            elif step in ("a1", "a2", "a3"):
-                src = "t%d" % (int(step[1]) - 1)
-                nc.vector.tensor_tensor(
-                    out=st[b, "lg"][:], in0=st[b, "lg"][:], in1=st[b, src][:], op=ALU.add
-                )
-            elif step in ("t1", "t2", "t3"):
-                src, fac = "t%d" % (int(step[1]) - 1), "g" + step[1]
-                nc.vector.tensor_tensor(
-                    out=small(b, step, 8)[:], in0=st[b, src][:], in1=st[b, fac][:], op=ALU.mult
+            elif step[0] == "t":
+                k = int(step[1])
+                nc.gpsimd.tensor_tensor(
+                    out=tv[:, k + 1, :], in0=tv[:, k, :], in1=st[b, "g%d" % k][:], op=ALU.mult
                 )
             elif step == "lg":
-                nc.vector.scalar_tensor_tensor(
-                    out=st[b, "lg"][:],
-                    in0=st[b, "lg"][:],
-                    scalar=-4.0,
-                    in1=st[b, "t3"][:],
-                    op0=ALU.add,
-                    op1=ALU.add,
-                )
-            elif step == "aa":
-                nc.vector.tensor_tensor(
-                    out=small(b, "aa")[:], in0=st[b, "lg"][:, 0:4], in1=negm[b][:], op=ALU.subtract
-                )
-            elif step == "bb":
-                nc.vector.tensor_tensor(
-                    out=small(b, "bb")[:], in0=st[b, "mx"][:], in1=st[b, "lg"][:, 4:8], op=ALU.add
+                nc.vector.tensor_reduce(
+                    out=wv[:, 2:4, 0:4],
+                    in_=st[b, "tt"][:].rearrange("p (k a c) -> p a c k", a=2, c=4),
+                    axis=AX.X,
+                    op=ALU.add,
                 )
             elif step == "z0":
-                nc.vector.tensor_tensor(out=z0, in0=z0, in1=st[b, "aa"][:], op=ALU.add)
+                nc.vector.tensor_reduce(
+                    out=z0, in_=wv[:, 0:3, 0:4].rearrange("p k c -> p c k"), axis=AX.X, op=ALU.add
+                )
             elif step == "nc":
-                nc.vector.scalar_tensor_tensor(
+                nc.vector.tensor_reduce(
                     out=small(b, "negc")[:],
-                    in0=st[b, "aa"][:],
-                    scalar=-1.0,
-                    in1=st[b, "bb"][:],
-                    op0=ALU.mult,
-                    op1=ALU.subtract,
+                    in_=wv[:, 1:5, 0:4].rearrange("p k c -> p c k"),
+                    axis=AX.X,
+                    op=ALU.add,
+                    negate=True,
                 )
 
         def finish(i):
@@ -245,6 +240,7 @@ def tile_jointnet_kernel(
             make_identity(nc, ident[:])
             nc.vector.memset(warm[:], 0.0)
             nc.vector.memset(one[:], 1.0)
+            nc.vector.memset(shift[:], -1.0 * STEPS)
             nc.scalar.activation(out=warm2[:], in_=warm[:], func=ACT.Exp)
             braw = staging.tile([P, 256], BF16, name="braw")
             nc.vector.memset(braw[:], 0.0)
@@ -334,7 +330,12 @@ def tile_jointnet_kernel(
                     )
                 ps_wj = ps[:].rearrange("p (j w) -> p w j", j=4)
                 if r < 2:
-                    nc.scalar.copy(out=enc_v[:, g, r * P : (r + 1) * P, :], in_=ps_wj)
+                    nc.vector.tensor_tensor(
+                        out=enc_v[:, g, r * P : (r + 1) * P, :],
+                        in0=ps_wj,
+                        in1=bsum[:, g * 4 : (g + 1) * 4].unsqueeze(1).to_broadcast([P, P, 4]),
+                        op=ALU.add,
+                    )
                 else:
                     dec_ps[g] = ps_wj
 
@@ -366,31 +367,27 @@ def tile_jointnet_kernel(
             fc_weights(0, 0, "S")
             fc_weights(0, 1, "S")
             fc_weights(2, 0, "S")
-            dec_slice(0, 0)
-            add(0, 0, nc.vector)
+            add(0, 0, "V")
             project(1, 2)
             project(1, 0)
             fc_weights(2, 1, "S")
             fc_quant(0, 0)
             tanh(0, 0)
-            dec_slice(0, 1)
-            add(0, 1, nc.vector)
+            add(0, 1, "V")
             fc_weights(4, 0, "S")
             fc_quant(1, 0)
             tanh(0, 1)
             fc_weights(4, 1, "V")
             fc_weights(6, 0, "V")
             fc_weights(6, 1, "V")
-            dec_slice(1, 0)
-            add(1, 0, nc.vector)
             fc_quant(0, 1)
             fc_quant(1, 1)
             quant(0)
             matmul(0)
             dec_slice(1, 1)
-            dec_slice(2, 0)
-            add(1, 1, nc.gpsimd)
-            add(2, 0, nc.gpsimd)
+            dec_slice(2, 1)
+            add(1, 1, "G")
+            add(1, 0, "V")
             project(0, 1)
             project(1, 1)
 
@@ -415,80 +412,76 @@ def tile_jointnet_kernel(
             if tile_ok(i):
                 row_max(i)
 
-        for u in range(0, B + 3):
-            c1, c2 = u - 1, u - 2
-            fin = [4 * c2 + n for n in range(4)] if 0 <= c2 < B else []
-            fin_g = [i for i in fin if FIN[i % 4] == "G"]
-            fin_s = [i for i in fin if FIN[i % 4] == "S"]
-            fin_v = [i for i in fin if FIN[i % 4] == "V"]
+        def fin_on(b, eng):
+            if 0 <= b < B:
+                for n in range(4):
+                    if FIN[n] == eng:
+                        finish(4 * b + n)
+
+        def mm(i):
+            if tile_ok(i):
+                matmul(i)
+
+        for u in range(0, B + 2):
             if u < B:
                 zbt[u] = zpool.tile([P, 4 * V], F32, name="zb", tag="zb")
                 negm[u] = stat.tile([P, 4], F32, name="negm", tag="negm")
                 xx[u] = stat.tile([P, 16], F32, name="xx", tag="xx")
-            for n in range(4):
-                i = 4 * u + n
-                if n == 0:
-                    badd(i, 0)
-                    on(c2, "t2")
-                    esum(i - 2)
-                    on(c2, "g3")
-                    on(c1, "ab")
-                    if u + 1 < B:
-                        tanh(u + 1, 0)
-                    on(c1, "ev")
-                    badd(i, 1)
-                    on(c2, "a3")
-                    rmax(i - 1)
-                    on(c2, "t3")
-                elif n == 1:
-                    esum(i - 2)
-                    on(c1, "q")
-                    on(c1, "mx")
-                    if u + 1 < B:
-                        tanh(u + 1, 1)
-                    badd(i, 0)
-                    on(c2, "lg")
-                    badd(i, 1)
-                    on(c2, "aa")
-                    rmax(i - 1)
-                    on(c2, "bb")
-                    on(c2, "z0")
-                elif n == 2:
-                    badd(i, 0)
-                    on(c1, "x0")
-                    on(c1, "e0")
-                    esum(i - 2)
-                    badd(i, 1)
-                    rmax(i - 1)
-                    on(c1, "t0")
-                    on(c1, "g1")
-                    if u + 1 < B:
-                        quant(u + 1)
-                    on(c2, "nc")
-                    for k in fin_v:
-                        finish(k)
-                    if u + 2 < B:
-                        dec_slice(u + 2, 1)
-                    if u + 3 < B:
-                        dec_slice(u + 3, 0)
-                    if u + 2 < B:
-                        add(u + 2, 1, nc.gpsimd)
-                    if u + 3 < B:
-                        add(u + 3, 0, nc.gpsimd)
-                    for k in fin_g:
-                        finish(k)
-                    for k in fin_s[:1]:
-                        finish(k)
-                else:
-                    badd(i, 0)
-                    on(c1, "a1")
-                    badd(i, 1)
-                    on(c1, "t1")
-                    esum(i - 2)
-                    on(c1, "g2")
-                    rmax(i - 1)
-                    on(c1, "a2")
-                    for k in fin_s[1:]:
-                        finish(k)
-                if tile_ok(i + 1):
-                    matmul(i + 1)
+            i = 4 * u
+            badd(i, 0)
+            esum(i - 2)
+            on(u - 2, "g3")
+            on(u - 2, "t3")
+            badd(i, 1)
+            rmax(i - 1)
+            on(u - 2, "lg")
+            if u + 2 < B:
+                add(u + 2, 1, "G")
+            esum(i - 1)
+            mm(i + 1)
+
+            i = 4 * u + 1
+            badd(i, 0)
+            on(u - 2, "z0")
+            badd(i, 1)
+            on(u - 2, "nc")
+            rmax(i - 1)
+            if u + 2 < B:
+                add(u + 2, 0, "V")
+            for step in ("ab", "zc", "mc", "mx"):
+                on(u - 1, step)
+            if u + 1 < B:
+                tanh(u + 1, 0)
+            on(u - 1, "ev")
+            if u + 1 < B:
+                tanh(u + 1, 1)
+            on(u - 1, "q")
+            fin_on(u - 2, "S")
+            fin_on(u - 2, "G")
+            mm(i + 1)
+
+            i = 4 * u + 2
+            badd(i, 0)
+            badd(i, 1)
+            rmax(i - 1)
+            if u + 1 < B:
+                quant(u + 1)
+            on(u - 1, "x0")
+            fin_on(u - 2, "V")
+            if u + 3 < B:
+                dec_slice(u + 3, 1)
+            on(u - 1, "g0")
+            on(u - 1, "t0")
+            mm(i + 1)
+
+            i = 4 * u + 3
+            badd(i, 0)
+            esum(i - 3)
+            on(u - 1, "g1")
+            on(u - 1, "t1")
+            badd(i, 1)
+            esum(i - 2)
+            on(u - 1, "g2")
+            on(u - 1, "t2")
+            rmax(i - 1)
+            mm(i + 1)

@@ -66,18 +66,20 @@ def tile_jointnet_kernel(
                 out=dec_v[:, g, b * U : (b + 1) * U, :], in_=dec_ps[g][:, b * U : (b + 1) * U, :]
             )
 
-        def add(b, g, eng):
-            comb[b, g] = work.tile([P, 2048], F32, name="comb", tag="comb")
+        def add(b, g, eng, t0=0, t1=T):
+            if (b, g) not in comb:
+                comb[b, g] = work.tile([P, 2048], F32, name="comb", tag="comb")
+            nt = t1 - t0
             dec = dec_ps[g] if eng == "V" else dec_v[:, g, :, :]
             (nc.vector if eng == "V" else nc.gpsimd).tensor_tensor(
-                out=comb[b, g][:].rearrange("p (t u j) -> p t u j", t=T, u=U),
-                in0=enc_v[:, g, b * T : (b + 1) * T, :].unsqueeze(2).to_broadcast([P, T, U, 4]),
-                in1=dec[:, b * U : (b + 1) * U, :].unsqueeze(1).to_broadcast([P, T, U, 4]),
+                out=comb[b, g][:, t0 * 64 : t1 * 64].rearrange("p (t u j) -> p t u j", t=nt, u=U),
+                in0=enc_v[:, g, b * T + t0 : b * T + t1, :].unsqueeze(2).to_broadcast([P, nt, U, 4]),
+                in1=dec[:, b * U : (b + 1) * U, :].unsqueeze(1).to_broadcast([P, nt, U, 4]),
                 op=ALU.add,
             )
 
         def tanh(b, g, t0=0, t1=T):
-            if g == 0 and t0 == 0:
+            if b not in hid:
                 hid[b] = work.tile([P, 4096], BF16, name="hid", tag="hid", align_bytes=64, bufs=2)
             nc.scalar.activation(
                 out=hid[b][:, g * 2048 + t0 * 64 : g * 2048 + t1 * 64],
@@ -145,92 +147,93 @@ def tile_jointnet_kernel(
         def two(ap):
             return ap.rearrange("p (a c) -> p a c", a=2)
 
-        def small(b, name, width=4):
-            st[b, name] = stat.tile([P, width], F32, name=name, tag=name)
-            return st[b, name]
+        def small(grp, name, width=4):
+            st[grp, name] = stat.tile([P, width], F32, name=name, tag=name)
+            return st[grp, name]
 
-        def chain(b, step):
-            z0 = zbt[b][:].rearrange("p (n v) -> p n v", n=4)[:, :, 0]
+        def chain(grp, step):
+            b, n0, n1 = grp
+            c = n1 - n0
+            z0 = zbt[b][:].rearrange("p (n v) -> p n v", n=4)[:, n0:n1, 0]
             if step == "ab":
-                st[b, "w"] = stat.tile([P, 40], F32, name="w", tag="w")
-                st[b, "tt"] = stat.tile([P, 8 * (STEPS + 1)], F32, name="tt", tag="tt")
-            wv = st[b, "w"][:].rearrange("p (k c) -> p k c", c=8)
-            tv = st[b, "tt"][:].rearrange("p (k c) -> p k c", c=8)
+                st[grp, "w"] = stat.tile([P, 40], F32, name="w", tag="w")
+                st[grp, "tt"] = stat.tile([P, 8 * (STEPS + 1)], F32, name="tt", tag="tt")
+            wv = st[grp, "w"][:].rearrange("p (k c) -> p k c", c=8)[:, :, 0:c]
+            tv = st[grp, "tt"][:].rearrange("p (k a c) -> p k a c", a=2, c=4)[:, :, :, 0:c]
+            xv = two(xx[b][:])[:, :, n0:n1]
             if step == "ab":
-                nc.scalar.activation(out=small(b, "ab")[:], in_=z0, func=ACT.Abs)
+                nc.scalar.activation(out=small(grp, "ab")[:, 0:c], in_=z0, func=ACT.Abs)
             elif step == "zc":
-                nc.scalar.activation(out=wv[:, 0, 0:4], in_=z0, func=ACT.Identity)
+                nc.scalar.activation(out=wv[:, 0, :], in_=z0, func=ACT.Identity)
             elif step == "mc":
-                nc.scalar.activation(out=wv[:, 1, 0:4], in_=negm[b][:], func=ACT.Identity, scale=-1.0)
+                nc.scalar.activation(
+                    out=wv[:, 1, :], in_=negm[b][:, n0:n1], func=ACT.Identity, scale=-1.0
+                )
             elif step == "mx":
-                nc.scalar.activation(out=wv[:, 4, 0:4], in_=z0, func=ACT.Relu)
+                nc.scalar.activation(out=wv[:, 4, :], in_=z0, func=ACT.Relu)
             elif step == "ev":
                 nc.scalar.activation(
-                    out=small(b, "ev")[:], in_=st[b, "ab"][:], func=ACT.Exp, scale=-1.0
+                    out=small(grp, "ev")[:, 0:c], in_=st[grp, "ab"][:, 0:c], func=ACT.Exp, scale=-1.0
                 )
             elif step == "q":
                 nc.scalar.activation(
-                    out=xx[b][:, 8:12], in_=st[b, "ev"][:], func=ACT.Identity, bias=one[:], scale=1.0
+                    out=xx[b][:, 8 + n0 : 8 + n1],
+                    in_=st[grp, "ev"][:, 0:c],
+                    func=ACT.Identity,
+                    bias=one[:],
+                    scale=1.0,
                 )
             elif step == "x0":
                 nc.vector.tensor_scalar(
-                    out=two(tv[:, 0, :]),
-                    in0=two(xx[b][:].bitcast(I32))[:, :, 0:4],
+                    out=tv[:, 0, :, :],
+                    in0=two(xx[b][:].bitcast(I32))[:, :, n0:n1],
                     scalar1=C0,
                     scalar2=K1,
                     op0=ALU.add,
                     op1=ALU.mult,
                 )
-            elif step == "g0":
-                nc.scalar.activation(
-                    out=small(b, "g0", 8)[:], in_=tv[:, 0, :], func=ACT.Exp, bias=shift[:], scale=-1.0
-                )
-            elif step == "t0":
-                nc.gpsimd.tensor_tensor(
-                    out=two(tv[:, 1, :]),
-                    in0=two(st[b, "g0"][:]),
-                    in1=two(xx[b][:])[:, :, 0:4],
-                    op=ALU.mult,
-                )
             elif step[0] == "g":
                 k = int(step[1])
                 nc.scalar.activation(
-                    out=small(b, step, 8)[:], in_=tv[:, k, :], func=ACT.Exp, bias=one[:], scale=-1.0
+                    out=two(small(grp, step, 8)[:])[:, :, 0:c],
+                    in_=tv[:, k, :, :],
+                    func=ACT.Exp,
+                    bias=(shift if k == 0 else one)[:],
+                    scale=-1.0,
                 )
             elif step[0] == "t":
                 k = int(step[1])
-                nc.gpsimd.tensor_tensor(
-                    out=tv[:, k + 1, :], in0=tv[:, k, :], in1=st[b, "g%d" % k][:], op=ALU.mult
+                (nc.vector if grp == (B - 1, 2, 4) else nc.gpsimd).tensor_tensor(
+                    out=tv[:, k + 1, :, :],
+                    in0=two(st[grp, "g%d" % k][:])[:, :, 0:c],
+                    in1=xv if k == 0 else tv[:, k, :, :],
+                    op=ALU.mult,
                 )
             elif step == "lg":
                 nc.vector.tensor_reduce(
-                    out=wv[:, 2:4, 0:4],
-                    in_=st[b, "tt"][:].rearrange("p (k a c) -> p a c k", a=2, c=4),
-                    axis=AX.X,
-                    op=ALU.add,
+                    out=wv[:, 2:4, :], in_=tv.rearrange("p k a c -> p a c k"), axis=AX.X, op=ALU.add
                 )
             elif step == "z0":
                 nc.vector.tensor_reduce(
-                    out=z0, in_=wv[:, 0:3, 0:4].rearrange("p k c -> p c k"), axis=AX.X, op=ALU.add
+                    out=z0, in_=wv[:, 0:3, :].rearrange("p k c -> p c k"), axis=AX.X, op=ALU.add
                 )
             elif step == "nc":
                 nc.vector.tensor_reduce(
-                    out=small(b, "negc")[:],
-                    in_=wv[:, 1:5, 0:4].rearrange("p k c -> p c k"),
+                    out=small(grp, "negc")[:, 0:c],
+                    in_=wv[:, 1:5, :].rearrange("p k c -> p c k"),
                     axis=AX.X,
                     op=ALU.add,
                     negate=True,
                 )
 
-        def finish(i):
-            b, n = divmod(i, 4)
+        def finish(i, grp, eng):
             z = zrow(i)
-            c = st[b, "negc"][:, n : n + 1]
-            if FIN[n] == "G":
+            c = st[grp, "negc"][:, i % 4 - grp[1] : i % 4 - grp[1] + 1]
+            if eng == "G":
                 nc.gpsimd.tensor_scalar(
                     out=z, in0=z, scalar1=1.0, scalar2=c, op0=ALU.mult, op1=ALU.add
                 )
-            elif FIN[n] == "S":
+            elif eng == "S":
                 nc.scalar.activation(out=z, in_=z, func=ACT.Identity, bias=c, scale=1.0)
             else:
                 nc.vector.tensor_scalar(out=z, in0=z, scalar1=c, scalar2=None, op0=ALU.add)
@@ -292,7 +295,7 @@ def tile_jointnet_kernel(
                 return [src32[:, (first + i) * P : (first + i + 1) * P] for i in range(count)]
 
             xin32, xg32 = xin[:].bitcast(F32), xg[:].bitcast(F32)
-            turn(blocks(xin32, 0, 4), xg32[:, 0:512], "V")
+            turn(blocks(xin32, 0, 4), xg32[:, 0:512], "S")
             turn(blocks(xin32, 4, 2), xg32[:, 512:768], "S")
             nc.vector.quantize_mx(
                 out=xc[:, 0:256].bitcast(FP8X4), scales=xs[:, 0:256], in_=xg[:, 0:1024]
@@ -303,7 +306,7 @@ def tile_jointnet_kernel(
 
             def weights(raw, grp, cod, sca, g):
                 r32, g32 = raw[:].bitcast(F32), grp[:].bitcast(F32)
-                turn(blocks(r32, g * 8, 4), g32[:, g * 1024 : g * 1024 + 512], "V")
+                turn(blocks(r32, g * 8, 4), g32[:, g * 1024 : g * 1024 + 512], "S")
                 turn(blocks(r32, g * 8 + 4, 4), g32[:, g * 1024 + 512 : g * 1024 + 1024], "S")
                 nc.vector.quantize_mx(
                     out=cod[:, g * 512 : (g + 1) * 512].bitcast(FP8X4),
@@ -311,7 +314,9 @@ def tile_jointnet_kernel(
                     in_=grp[:, g * 2048 : (g + 1) * 2048],
                 )
 
-            def project(g, r):
+            proj = {}
+
+            def project(g, r, late=False):
                 cod, sca = (wec, wes) if r < 2 else (wdc, wds)
                 if r < 2:
                     ps = psum.tile([P, 512], F32, name="ps", tag="bank")
@@ -328,16 +333,19 @@ def tile_jointnet_kernel(
                         start=True,
                         stop=True,
                     )
-                ps_wj = ps[:].rearrange("p (j w) -> p w j", j=4)
-                if r < 2:
-                    nc.vector.tensor_tensor(
-                        out=enc_v[:, g, r * P : (r + 1) * P, :],
-                        in0=ps_wj,
-                        in1=bsum[:, g * 4 : (g + 1) * 4].unsqueeze(1).to_broadcast([P, P, 4]),
-                        op=ALU.add,
-                    )
-                else:
-                    dec_ps[g] = ps_wj
+                proj[g, r] = ps[:].rearrange("p (j w) -> p w j", j=4)
+                if r == 2:
+                    dec_ps[g] = proj[g, r]
+                elif not late:
+                    enc_out(g, r)
+
+            def enc_out(g, r):
+                nc.vector.tensor_tensor(
+                    out=enc_v[:, g, r * P : (r + 1) * P, :],
+                    in0=proj[g, r],
+                    in1=bsum[:, g * 4 : (g + 1) * 4].unsqueeze(1).to_broadcast([P, P, 4]),
+                    op=ALU.add,
+                )
 
             wf32 = wf[:].bitcast(F32).rearrange("p (r g x) -> p r g x", r=8, g=2)
 
@@ -363,39 +371,47 @@ def tile_jointnet_kernel(
             weights(we, weg, wec, wes, 1)
             project(0, 2)
             project(0, 0)
+            project(0, 1)
+            for g in range(2):
+                comb[0, g] = work.tile([P, 2048], F32, name="comb", tag="comb")
+            add(0, 0, "V", 0, 16)
             weights(wd, wdg, wdc, wds, 1)
+            dec_slice(1, 0)
+            add(1, 0, "G")
+            add(0, 0, "V", 16, 32)
             fc_weights(0, 0, "S")
             fc_weights(0, 1, "S")
             fc_weights(2, 0, "S")
-            add(0, 0, "V")
             project(1, 2)
             project(1, 0)
+            tanh(0, 0, 0, 16)
+            add(0, 1, "V", 0, 16)
+            add(0, 1, "V", 16, 32)
             fc_weights(2, 1, "S")
-            fc_quant(0, 0)
-            tanh(0, 0)
-            add(0, 1, "V")
+            tanh(0, 0, 16, 32)
             fc_weights(4, 0, "S")
-            fc_quant(1, 0)
-            tanh(0, 1)
+            tanh(0, 1, 0, 16)
+            tanh(0, 1, 16, 32)
             fc_weights(4, 1, "V")
             fc_weights(6, 0, "V")
             fc_weights(6, 1, "V")
+            fc_quant(0, 0)
+            fc_quant(1, 0)
             fc_quant(0, 1)
             fc_quant(1, 1)
+            project(1, 1, True)
             quant(0)
             matmul(0)
             dec_slice(1, 1)
             dec_slice(2, 1)
             add(1, 1, "G")
-            add(1, 0, "V")
-            project(0, 1)
-            project(1, 1)
+            enc_out(1, 1)
 
         zpool = ctx.enter_context(tc.tile_pool(name="zpool", bufs=5))
 
         def on(b, step):
-            if 0 <= b < B:
-                chain(b, step)
+            if 0 <= b < B - 1:
+                chain((b, 0, 4), step)
 
         def tile_ok(i):
             return 0 <= i < 4 * B
@@ -413,16 +429,16 @@ def tile_jointnet_kernel(
                 row_max(i)
 
         def fin_on(b, eng):
-            if 0 <= b < B:
+            if 0 <= b < B - 1:
                 for n in range(4):
                     if FIN[n] == eng:
-                        finish(4 * b + n)
+                        finish(4 * b + n, (b, 0, 4), eng)
 
         def mm(i):
             if tile_ok(i):
                 matmul(i)
 
-        for u in range(0, B + 2):
+        for u in range(0, B - 1):
             if u < B:
                 zbt[u] = zpool.tile([P, 4 * V], F32, name="zb", tag="zb")
                 negm[u] = stat.tile([P, 4], F32, name="negm", tag="negm")
@@ -485,3 +501,83 @@ def tile_jointnet_kernel(
             on(u - 1, "t2")
             rmax(i - 1)
             mm(i + 1)
+
+        u = B - 1
+        zbt[u] = zpool.tile([P, 4 * V], F32, name="zb", tag="zb")
+        negm[u] = stat.tile([P, 4], F32, name="negm", tag="negm")
+        xx[u] = stat.tile([P, 16], F32, name="xx", tag="xx")
+        ga, gb, gc, gd = (u - 2, 0, 4), (u - 1, 0, 4), (u, 0, 2), (u, 2, 4)
+        i = 4 * u
+
+        def steps(grp, names):
+            for name in names:
+                chain(grp, name)
+
+        prep = ("ab", "zc", "mc", "mx", "ev", "q")
+        badd(i, 0)
+        esum(i - 2)
+        steps(ga, ("g3", "t3"))
+        badd(i, 1)
+        rmax(i - 1)
+        esum(i - 1)
+        mm(i + 1)
+        steps(gb, prep)
+        badd(i + 1, 0)
+        chain(ga, "lg")
+        badd(i + 1, 1)
+        chain(ga, "z0")
+        chain(ga, "nc")
+        rmax(i)
+        mm(i + 2)
+        chain(gb, "x0")
+        finish(4 * (u - 2) + 0, ga, "G")
+        finish(4 * (u - 2) + 3, ga, "S")
+        steps(gb, ("g0", "t0"))
+        esum(i)
+        finish(4 * (u - 2) + 1, ga, "G")
+        steps(gb, ("g1", "t1"))
+        badd(i + 2, 0)
+        badd(i + 2, 1)
+        rmax(i + 1)
+        mm(i + 3)
+        finish(4 * (u - 2) + 2, ga, "G")
+        esum(i + 1)
+        steps(gb, ("g2", "t2"))
+        steps(gc, prep)
+        steps(gb, ("g3", "t3"))
+        badd(i + 3, 0)
+        badd(i + 3, 1)
+        rmax(i + 2)
+        chain(gc, "x0")
+        chain(gb, "lg")
+        steps(gc, ("g0", "t0"))
+        esum(i + 2)
+        steps(gd, ("ab", "zc", "mx", "ev", "q"))
+        rmax(i + 3)
+        chain(gb, "z0")
+        chain(gb, "nc")
+        steps(gc, ("g1", "t1"))
+        esum(i + 3)
+        finish(4 * (u - 1) + 0, gb, "V")
+        finish(4 * (u - 1) + 1, gb, "V")
+        steps(gc, ("g2", "t2"))
+        chain(gd, "x0")
+        steps(gd, ("g0", "mc"))
+        finish(4 * (u - 1) + 2, gb, "V")
+        chain(gd, "t0")
+        steps(gc, ("g3", "t3"))
+        chain(gd, "g1")
+        finish(4 * (u - 1) + 3, gb, "V")
+        chain(gd, "t1")
+        chain(gc, "lg")
+        chain(gd, "g2")
+        chain(gc, "z0")
+        chain(gc, "nc")
+        chain(gd, "t2")
+        chain(gd, "g3")
+        finish(i, gc, "V")
+        finish(i + 1, gc, "S")
+        chain(gd, "t3")
+        steps(gd, ("lg", "z0", "nc"))
+        finish(i + 2, gd, "V")
+        finish(i + 3, gd, "S")

@@ -22,7 +22,8 @@ K1 = LN2 / 8388608.0
 STEPS = 4
 C0 = (0.043 - 127.0) * 8388608.0 - STEPS / K1
 
-FIN = ("G", "S", "G", "S")
+OLD = 3
+HALVES = 16
 
 
 def tile_jointnet_kernel(
@@ -35,7 +36,7 @@ def tile_jointnet_kernel(
         const = ctx.enter_context(tc.tile_pool(name="const", bufs=1))
         work = ctx.enter_context(tc.tile_pool(name="work", bufs=4))
         stat = ctx.enter_context(tc.tile_pool(name="stat", bufs=4))
-        psum = ctx.enter_context(tc.psum_pool(name="psum", bufs=6))
+        psum = ctx.enter_context(tc.psum_pool(name="psum", bufs=4))
 
         xc = const.tile([P, 384], U32, name="xc", align_bytes=64)
         xs = const.tile([P, 384], U8, name="xs", align_bytes=64)
@@ -45,8 +46,8 @@ def tile_jointnet_kernel(
         wds = const.tile([P, 1024], U8, name="wds", align_bytes=64)
         wfc = const.tile([P, 2048], U32, name="wfc", align_bytes=64)
         wfs = const.tile([P, 2048], U8, name="wfs", align_bytes=64)
-        encT = const.tile([P, 2048], F32, name="encT")
-        decT = const.tile([P, 1024], F32, name="decT")
+        encT = const.tile([P, 384], F32, name="encT")
+        decT = const.tile([P, 256], F32, name="decT")
         bfc = const.tile([P, V], BF16, name="bfc")
         ident = const.tile([P, P], F32, name="ident")
         bT = const.tile([P, 8], F32, name="bT")
@@ -55,64 +56,128 @@ def tile_jointnet_kernel(
         warm2 = const.tile([P, 8], F32, name="warm2")
         one = const.tile([P, 1], F32, name="one")
         shift = const.tile([P, 1], F32, name="shift")
+        amat = const.tile([P, (HALVES - OLD) * 1024], BF16, name="amat")
+        pick = const.tile([P, 256], BF16, name="pick")
+        piece = [const.tile([P, 3072], BF16, name="piece%d" % q) for q in range(3)]
+        rest = const.tile([P, 3072], F32, name="rest")
         enc_v = encT[:].rearrange("p (g w j) -> p g w j", g=2, j=4)
         dec_v = decT[:].rearrange("p (g w j) -> p g w j", g=2, j=4)
 
         comb, hid, hc, hs, dec_ps = {}, {}, {}, {}, {}
-        ybank, zbt, negm, xx, st = {}, {}, {}, {}, {}
+        cbank, ybank, zbt, negm, xx, st = {}, {}, {}, {}, {}, {}
+        nat_ps = {}
 
-        def dec_slice(b, g):
-            nc.vector.tensor_copy(
-                out=dec_v[:, g, b * U : (b + 1) * U, :], in_=dec_ps[g][:, b * U : (b + 1) * U, :]
-            )
-
-        def add(b, g, eng, t0=0, t1=T):
-            if (b, g) not in comb:
-                comb[b, g] = work.tile([P, 2048], F32, name="comb", tag="comb")
-            nt = t1 - t0
+        def add(h, g, eng):
+            comb[h, g] = work.tile([P, 1024], F32, name="comb", tag="comb", bufs=2 * OLD)
+            b = h // 2
             dec = dec_ps[g] if eng == "V" else dec_v[:, g, :, :]
             (nc.vector if eng == "V" else nc.gpsimd).tensor_tensor(
-                out=comb[b, g][:, t0 * 64 : t1 * 64].rearrange("p (t u j) -> p t u j", t=nt, u=U),
-                in0=enc_v[:, g, b * T + t0 : b * T + t1, :].unsqueeze(2).to_broadcast([P, nt, U, 4]),
-                in1=dec[:, b * U : (b + 1) * U, :].unsqueeze(1).to_broadcast([P, nt, U, 4]),
+                out=comb[h, g][:].rearrange("p (t u j) -> p t u j", t=16, u=U),
+                in0=enc_v[:, g, h * 16 : (h + 1) * 16, :].unsqueeze(2).to_broadcast([P, 16, U, 4]),
+                in1=dec[:, b * U : (b + 1) * U, :].unsqueeze(1).to_broadcast([P, 16, U, 4]),
                 op=ALU.add,
             )
 
-        def tanh(b, g, t0=0, t1=T):
-            if b not in hid:
-                hid[b] = work.tile([P, 4096], BF16, name="hid", tag="hid", align_bytes=64, bufs=2)
+        def hid_tile(h):
+            if h not in hid:
+                hid[h] = work.tile([P, 2048], BF16, name="hid", tag="hid", align_bytes=64, bufs=3)
+            return hid[h]
+
+        def tanh_old(h, g):
             nc.scalar.activation(
-                out=hid[b][:, g * 2048 + t0 * 64 : g * 2048 + t1 * 64],
-                in_=comb[b, g][:, t0 * 64 : t1 * 64],
+                out=hid_tile(h)[:].rearrange("p (n g x) -> p n g x", n=2, g=2)[:, :, g, :],
+                in_=comb[h, g][:].rearrange("p (n x) -> p n x", n=2),
                 func=ACT.Tanh,
             )
 
-        def quant(b, c0=0, c1=4096):
-            if c0 == 0:
-                hc[b] = work.tile([P, 1024], U32, name="hc", tag="hc", align_bytes=64, bufs=2)
-                hs[b] = work.tile([P, 1024], U8, name="hs", tag="hs", align_bytes=64, bufs=2)
-            nc.vector.quantize_mx(
-                out=hc[b][:, c0 // 4 : c1 // 4].bitcast(FP8X4),
-                scales=hs[b][:, c0 // 4 : c1 // 4],
-                in_=hid[b][:, c0:c1],
+        def comb_mm(i):
+            h, n = divmod(i, 2)
+            for g in range(2):
+                cbank[i, g] = psum.tile([P, 512], F32, name="cb", tag="cb")
+                for j in range(4):
+                    c0 = (h - OLD) * 1024 + g * 512 + j * P
+                    nc.tensor.matmul(
+                        out=cbank[i, g][:, j * P : (j + 1) * P],
+                        lhsT=amat[:, c0 : c0 + P],
+                        rhs=pick[:, n * P : (n + 1) * P],
+                        start=True,
+                        stop=True,
+                    )
+
+        def tanh(i, g):
+            h, n = divmod(i, 2)
+            c0 = n * 1024 + g * 512
+            nc.scalar.activation(
+                out=hid_tile(h)[:, c0 : c0 + 512].rearrange("p (n j) -> p n j", j=4),
+                in_=cbank[i, g][:].rearrange("p (j n) -> p n j", j=4),
+                func=ACT.Tanh,
             )
 
+        def quant(h):
+            hc[h] = work.tile([P, 512], U32, name="hc", tag="hc", align_bytes=64, bufs=3)
+            hs[h] = work.tile([P, 512], U8, name="hs", tag="hs", align_bytes=64, bufs=3)
+            nc.vector.quantize_mx(out=hc[h][:].bitcast(FP8X4), scales=hs[h][:], in_=hid[h][:])
+
         def matmul(i):
-            b, n = divmod(i, 4)
+            h, n = divmod(i, 2)
             for v in range(2):
                 ybank[i, v] = psum.tile([P, 512], F32, name="y", tag="bank")
             for g in range(2):
+                s0 = n * 256 + g * P
                 for v in range(2):
                     c0 = g * 1024 + v * 512
                     nc.tensor.matmul_mx(
                         out=ybank[i, v][:],
-                        lhsT=hc[b][:, g * 512 + n * P : g * 512 + (n + 1) * P].bitcast(FP8X4),
-                        lhsT_scale=hs[b][:, g * 512 + n * P : g * 512 + (n + 1) * P],
+                        lhsT=hc[h][:, s0 : s0 + P].bitcast(FP8X4),
+                        lhsT_scale=hs[h][:, s0 : s0 + P],
                         rhs=wfc[:, c0 : c0 + 512].bitcast(FP8X4),
                         rhs_scale=wfs[:, c0 : c0 + 512],
                         start=(g == 0),
                         stop=(g == 1),
                     )
+
+        def natural(src, g):
+            cod, sca = (wec, wes) if src < 2 else (wdc, wds)
+            nat_ps[src, g] = psum.tile([P, 512], F32, name="nat", tag="bank" if src == 2 else "cb")
+            nc.tensor.matmul_mx(
+                out=nat_ps[src, g][:],
+                lhsT=xc[:, src * P : (src + 1) * P].bitcast(FP8X4),
+                lhsT_scale=xs[:, src * P : (src + 1) * P],
+                rhs=cod[:, g * 512 : (g + 1) * 512].bitcast(FP8X4),
+                rhs_scale=sca[:, g * 512 : (g + 1) * 512],
+                start=True,
+                stop=True,
+            )
+
+        def split_a(src, g):
+            cols = slice(src * 1024 + g * 512, src * 1024 + (g + 1) * 512)
+            nc.scalar.copy(out=piece[0][:, cols], in_=nat_ps[src, g][:])
+            nc.vector.tensor_tensor(
+                out=rest[:, cols], in0=nat_ps[src, g][:], in1=piece[0][:, cols], op=ALU.subtract
+            )
+
+        def split_b(src, g):
+            cols = slice(src * 1024 + g * 512, src * 1024 + (g + 1) * 512)
+            nc.gpsimd.tensor_scalar(
+                out=piece[1][:, cols], in0=rest[:, cols], scalar1=1.0, scalar2=0.0, op0=ALU.mult, op1=ALU.add
+            )
+            nc.gpsimd.tensor_tensor(
+                out=piece[2][:, cols], in0=rest[:, cols], in1=piece[1][:, cols], op=ALU.subtract
+            )
+
+        def move_rows(h):
+            b, s = divmod(h, 2)
+            a0 = (h - OLD) * 1024
+            e0, p0 = b // 4 * 1024, b % 4 * 32 + s * 16
+            for q in range(3):
+                nc.sync.dma_start(
+                    out=amat[16 * q : 16 * (q + 1), a0 : a0 + 1024],
+                    in_=piece[q][p0 : p0 + 16, e0 : e0 + 1024],
+                )
+                nc.sync.dma_start(
+                    out=amat[48 + 16 * q : 64 + 16 * q, a0 : a0 + 1024],
+                    in_=piece[q][b * U : (b + 1) * U, 2048:3072],
+                )
 
         def zrow(i):
             b, n = divmod(i, 4)
@@ -164,24 +229,27 @@ def tile_jointnet_kernel(
             if step == "ab":
                 nc.scalar.activation(out=small(grp, "ab")[:, 0:c], in_=z0, func=ACT.Abs)
             elif step == "zc":
-                nc.scalar.activation(out=wv[:, 0, :], in_=z0, func=ACT.Identity)
+                nc.gpsimd.tensor_copy(out=wv[:, 0, :], in_=z0)
             elif step == "mc":
-                nc.scalar.activation(
-                    out=wv[:, 1, :], in_=negm[b][:, n0:n1], func=ACT.Identity, scale=-1.0
+                nc.gpsimd.tensor_scalar(
+                    out=wv[:, 1, :], in0=negm[b][:, n0:n1], scalar1=-1.0, scalar2=0.0, op0=ALU.mult, op1=ALU.add
                 )
             elif step == "mx":
-                nc.scalar.activation(out=wv[:, 4, :], in_=z0, func=ACT.Relu)
+                nc.gpsimd.tensor_scalar(
+                    out=wv[:, 4, :], in0=z0, scalar1=1.0, scalar2=0.0, op0=ALU.mult, op1=ALU.max
+                )
             elif step == "ev":
                 nc.scalar.activation(
                     out=small(grp, "ev")[:, 0:c], in_=st[grp, "ab"][:, 0:c], func=ACT.Exp, scale=-1.0
                 )
             elif step == "q":
-                nc.scalar.activation(
+                nc.gpsimd.tensor_scalar(
                     out=xx[b][:, 8 + n0 : 8 + n1],
-                    in_=st[grp, "ev"][:, 0:c],
-                    func=ACT.Identity,
-                    bias=one[:],
-                    scale=1.0,
+                    in0=st[grp, "ev"][:, 0:c],
+                    scalar1=1.0,
+                    scalar2=1.0,
+                    op0=ALU.mult,
+                    op1=ALU.add,
                 )
             elif step == "x0":
                 nc.vector.tensor_scalar(
@@ -247,6 +315,9 @@ def tile_jointnet_kernel(
             nc.scalar.activation(out=warm2[:], in_=warm[:], func=ACT.Exp)
             braw = staging.tile([P, 256], BF16, name="braw")
             nc.vector.memset(braw[:], 0.0)
+            brow = staging.tile([P, 1024], BF16, name="brow")
+            bperm = staging.tile([P, 1024], BF16, name="bperm")
+            nc.vector.memset(brow[96:128, :], 0.0)
             xin = staging.tile([P, 1536], BF16, name="xin")
             we = staging.tile([P, 4096], BF16, name="we")
             wd = staging.tile([P, 4096], BF16, name="wd")
@@ -273,11 +344,33 @@ def tile_jointnet_kernel(
             nc.sync.dma_start(out=braw[4:8, :], in_=b_dec.rearrange("(c x) -> c x", c=4))
             nc.sync.dma_start(out=we_dst[:, 2:4, :], in_=we_src[:, 2:4, :])
             nc.sync.dma_start(out=wd_dst[:, 2:4, :], in_=wd_src[:, 2:4, :])
+            nc.sync.dma_start(out=brow[96:97, :], in_=b_enc.unsqueeze(0))
+            nc.sync.dma_start(out=brow[97:98, :], in_=b_dec.unsqueeze(0))
             wf_src = W_fc.rearrange("(r p) f -> p r f", p=P)
             wf_dst = wf[:].rearrange("p (r f) -> p r f", r=8)
             for r0 in range(0, 8, 2):
                 nc.sync.dma_start(out=wf_dst[:, r0 : r0 + 2, :], in_=wf_src[:, r0 : r0 + 2, :])
             nc.sync.dma_start(out=bfc[:], in_=b_fc.partition_broadcast(P))
+
+            by_t = staging.tile([P, 16], F32, name="by_t")
+            by_u = staging.tile([P, 16], F32, name="by_u")
+            both = staging.tile([P, 1], F32, name="both")
+            nc.vector.tensor_reduce(
+                out=by_t[:], in_=ident[:, 0:48].rearrange("p (q t) -> p t q", q=3), axis=AX.X, op=ALU.add
+            )
+            nc.vector.tensor_reduce(
+                out=by_u[:], in_=ident[:, 48:96].rearrange("p (q t) -> p t q", q=3), axis=AX.X, op=ALU.add
+            )
+            nc.vector.tensor_reduce(out=both[:], in_=ident[:, 96:98], axis=AX.X, op=ALU.add)
+            nc.vector.tensor_scalar(
+                out=by_t[:], in0=by_t[:], scalar1=both[:], scalar2=None, op0=ALU.add
+            )
+            nc.vector.tensor_tensor(
+                out=pick[:].rearrange("p (t u) -> p t u", t=16),
+                in0=by_t[:].unsqueeze(2).to_broadcast([P, 16, U]),
+                in1=by_u[:].unsqueeze(1).to_broadcast([P, 16, U]),
+                op=ALU.add,
+            )
 
             def turn(srcs, dst32, eng):
                 n = len(srcs) // 2
@@ -314,14 +407,9 @@ def tile_jointnet_kernel(
                     in_=grp[:, g * 2048 : (g + 1) * 2048],
                 )
 
-            proj = {}
-
-            def project(g, r, late=False):
+            def project(g, r):
                 cod, sca = (wec, wes) if r < 2 else (wdc, wds)
-                if r < 2:
-                    ps = psum.tile([P, 512], F32, name="ps", tag="bank")
-                else:
-                    ps = psum.tile([P, 512], F32, name="psd", tag="dec", bufs=2)
+                ps = psum.tile([P, 512], F32, name="ps", tag="bank" if r < 2 else "cb")
                 for j in range(4):
                     c0 = (g * 4 + j) * P
                     nc.tensor.matmul_mx(
@@ -333,19 +421,20 @@ def tile_jointnet_kernel(
                         start=True,
                         stop=True,
                     )
-                proj[g, r] = ps[:].rearrange("p (j w) -> p w j", j=4)
+                view = ps[:].rearrange("p (j w) -> p w j", j=4)
                 if r == 2:
-                    dec_ps[g] = proj[g, r]
-                elif not late:
-                    enc_out(g, r)
+                    dec_ps[g] = view
+                else:
+                    w = OLD * 16
+                    nc.vector.tensor_tensor(
+                        out=enc_v[:, g, :, :],
+                        in0=view[:, 0:w, :],
+                        in1=bsum[:, g * 4 : (g + 1) * 4].unsqueeze(1).to_broadcast([P, w, 4]),
+                        op=ALU.add,
+                    )
 
-            def enc_out(g, r):
-                nc.vector.tensor_tensor(
-                    out=enc_v[:, g, r * P : (r + 1) * P, :],
-                    in0=proj[g, r],
-                    in1=bsum[:, g * 4 : (g + 1) * 4].unsqueeze(1).to_broadcast([P, P, 4]),
-                    op=ALU.add,
-                )
+            def dec_copy(g):
+                nc.vector.tensor_copy(out=dec_v[:, g, :, :], in_=dec_ps[g][:, 0:32, :])
 
             wf32 = wf[:].bitcast(F32).rearrange("p (r g x) -> p r g x", r=8, g=2)
 
@@ -368,44 +457,60 @@ def tile_jointnet_kernel(
             nc.vector.tensor_copy(out=bT[:], in_=ptb[:, 0:8])
             bT16 = bT[:].bitcast(BF16)
             nc.vector.tensor_tensor(out=bsum[:], in0=bT16[:, 0:8], in1=bT16[:, 8:16], op=ALU.add)
-            weights(we, weg, wec, wes, 1)
             project(0, 2)
             project(0, 0)
-            project(0, 1)
-            for g in range(2):
-                comb[0, g] = work.tile([P, 2048], F32, name="comb", tag="comb")
-            add(0, 0, "V", 0, 16)
-            weights(wd, wdg, wdc, wds, 1)
-            dec_slice(1, 0)
+            dec_copy(0)
             add(1, 0, "G")
-            add(0, 0, "V", 16, 32)
-            fc_weights(0, 0, "S")
-            fc_weights(0, 1, "S")
-            fc_weights(2, 0, "S")
+            weights(we, weg, wec, wes, 1)
+            weights(wd, wdg, wdc, wds, 1)
             project(1, 2)
             project(1, 0)
-            tanh(0, 0, 0, 16)
-            add(0, 1, "V", 0, 16)
-            add(0, 1, "V", 16, 32)
+            natural(0, 0)
+            natural(2, 0)
+            natural(0, 1)
+            natural(2, 1)
+            add(0, 0, "V")
+            add(0, 1, "V")
+            split_a(0, 0)
+            split_a(2, 0)
+            split_b(0, 0)
+            split_b(2, 0)
+            split_a(0, 1)
+            split_a(2, 1)
+            split_b(0, 1)
+            split_b(2, 1)
+            nc.vector.tensor_copy(
+                out=bperm[96:128, :].rearrange("p (c e w) -> p c e w", c=4, e=2),
+                in_=brow[96:128, :].rearrange("p (c w e) -> p c e w", c=4, e=2),
+            )
+            nc.sync.dma_start(
+                out=amat[96:128, :].rearrange("p (h x) -> p h x", x=1024),
+                in_=bperm[96:128, :].unsqueeze(1).to_broadcast([32, HALVES - OLD, 1024]),
+            )
+            for h in range(OLD, 8):
+                move_rows(h)
+            fc_weights(0, 0, "S")
+            fc_weights(0, 1, "S")
+            dec_copy(1)
+            tanh_old(0, 0)
+            tanh_old(0, 1)
+            add(1, 1, "V")
+            add(2, 0, "G")
+            add(2, 1, "G")
+            fc_weights(2, 0, "V")
             fc_weights(2, 1, "S")
-            tanh(0, 0, 16, 32)
-            fc_weights(4, 0, "S")
-            tanh(0, 1, 0, 16)
-            tanh(0, 1, 16, 32)
-            fc_weights(4, 1, "V")
-            fc_weights(6, 0, "V")
-            fc_weights(6, 1, "V")
+            fc_weights(4, 0, "V")
             fc_quant(0, 0)
             fc_quant(1, 0)
+            fc_weights(4, 1, "S")
+            quant(0)
+            fc_weights(6, 0, "S")
+            fc_weights(6, 1, "V")
             fc_quant(0, 1)
             fc_quant(1, 1)
-            project(1, 1, True)
-            quant(0)
+            tanh_old(1, 0)
+            tanh_old(1, 1)
             matmul(0)
-            dec_slice(1, 1)
-            dec_slice(2, 1)
-            add(1, 1, "G")
-            enc_out(1, 1)
 
         zpool = ctx.enter_context(tc.tile_pool(name="zpool", bufs=5))
 
@@ -428,79 +533,97 @@ def tile_jointnet_kernel(
             if tile_ok(i):
                 row_max(i)
 
-        def fin_on(b, eng):
+        def fin(b, n):
             if 0 <= b < B - 1:
-                for n in range(4):
-                    if FIN[n] == eng:
-                        finish(4 * b + n, (b, 0, 4), eng)
+                finish(4 * b + n, (b, 0, 4), "G")
 
         def mm(i):
             if tile_ok(i):
                 matmul(i)
 
+        def hidden(i, g):
+            if i < 2 * OLD:
+                tanh_old(OLD - 1, 0 if i == 2 * OLD - 2 else 1) if g == 0 else None
+            elif tile_ok(i):
+                tanh(i, g)
+
+        def cmm(i):
+            if 2 * OLD <= i < 4 * B:
+                comb_mm(i)
+
         for u in range(0, B - 1):
-            if u < B:
-                zbt[u] = zpool.tile([P, 4 * V], F32, name="zb", tag="zb")
-                negm[u] = stat.tile([P, 4], F32, name="negm", tag="negm")
-                xx[u] = stat.tile([P, 16], F32, name="xx", tag="xx")
+            zbt[u] = zpool.tile([P, 4 * V], F32, name="zb", tag="zb")
+            negm[u] = stat.tile([P, 4], F32, name="negm", tag="negm")
+            xx[u] = stat.tile([P, 16], F32, name="xx", tag="xx")
             i = 4 * u
             badd(i, 0)
-            esum(i - 2)
-            on(u - 2, "g3")
-            on(u - 2, "t3")
             badd(i, 1)
             rmax(i - 1)
-            on(u - 2, "lg")
-            if u + 2 < B:
-                add(u + 2, 1, "G")
-            esum(i - 1)
+            quant(i // 2 + 1)
+            esum(i - 2)
+            hidden(i + 4, 0)
+            hidden(i + 4, 1)
+            on(u - 2, "t1")
+            on(u - 2, "g2")
+            fin(u - 3, 2)
             mm(i + 1)
+            cmm(i + 5)
 
             i = 4 * u + 1
             badd(i, 0)
-            on(u - 2, "z0")
             badd(i, 1)
-            on(u - 2, "nc")
             rmax(i - 1)
-            if u + 2 < B:
-                add(u + 2, 0, "V")
-            for step in ("ab", "zc", "mc", "mx"):
+            if u == 1:
+                natural(1, 0)
+                natural(1, 1)
+                split_a(1, 0)
+            esum(i - 2)
+            hidden(i + 4, 0)
+            for step in ("ab", "zc", "mc", "mx", "ev", "q"):
                 on(u - 1, step)
-            if u + 1 < B:
-                tanh(u + 1, 0)
-            on(u - 1, "ev")
-            if u + 1 < B:
-                tanh(u + 1, 1)
-            on(u - 1, "q")
-            fin_on(u - 2, "S")
-            fin_on(u - 2, "G")
+            hidden(i + 4, 1)
+            on(u - 2, "t2")
+            on(u - 2, "g3")
+            fin(u - 3, 3)
             mm(i + 1)
+            cmm(i + 5)
 
             i = 4 * u + 2
             badd(i, 0)
-            badd(i, 1)
-            rmax(i - 1)
-            if u + 1 < B:
-                quant(u + 1)
             on(u - 1, "x0")
-            fin_on(u - 2, "V")
-            if u + 3 < B:
-                dec_slice(u + 3, 1)
+            badd(i, 1)
+            on(u - 2, "t3")
+            rmax(i - 1)
+            on(u - 2, "lg")
+            quant(i // 2 + 1)
+            on(u - 2, "z0")
+            on(u - 2, "nc")
+            if u == 1:
+                split_a(1, 1)
+                split_b(1, 0)
+                split_b(1, 1)
+                for h in range(8, 16):
+                    move_rows(h)
+            esum(i - 2)
+            hidden(i + 4, 0)
+            hidden(i + 4, 1)
             on(u - 1, "g0")
-            on(u - 1, "t0")
+            fin(u - 2, 0)
             mm(i + 1)
+            cmm(i + 5)
 
             i = 4 * u + 3
             badd(i, 0)
-            esum(i - 3)
-            on(u - 1, "g1")
-            on(u - 1, "t1")
             badd(i, 1)
-            esum(i - 2)
-            on(u - 1, "g2")
-            on(u - 1, "t2")
             rmax(i - 1)
+            esum(i - 2)
+            hidden(i + 4, 0)
+            hidden(i + 4, 1)
+            on(u - 1, "t0")
+            on(u - 1, "g1")
+            fin(u - 2, 1)
             mm(i + 1)
+            cmm(i + 5)
 
         u = B - 1
         zbt[u] = zpool.tile([P, 4 * V], F32, name="zb", tag="zb")
@@ -516,10 +639,14 @@ def tile_jointnet_kernel(
         prep = ("ab", "zc", "mc", "mx", "ev", "q")
         badd(i, 0)
         esum(i - 2)
-        steps(ga, ("g3", "t3"))
+        steps(ga, ("t1", "g2", "t2"))
         badd(i, 1)
         rmax(i - 1)
+        fin(u - 3, 2)
+        quant(i // 2 + 1)
         esum(i - 1)
+        steps(ga, ("g3", "t3"))
+        fin(u - 3, 3)
         mm(i + 1)
         steps(gb, prep)
         badd(i + 1, 0)

@@ -22,8 +22,7 @@ K1 = LN2 / 8388608.0
 STEPS = 4
 C0 = (0.043 - 127.0) * 8388608.0 - STEPS / K1
 
-OLD = 3
-HALVES = 16
+ADDED = (0, 1, 7)
 
 
 def tile_jointnet_kernel(
@@ -46,8 +45,8 @@ def tile_jointnet_kernel(
         wds = const.tile([P, 1024], U8, name="wds", align_bytes=64)
         wfc = const.tile([P, 2048], U32, name="wfc", align_bytes=64)
         wfs = const.tile([P, 2048], U8, name="wfs", align_bytes=64)
-        encT = const.tile([P, 384], F32, name="encT")
-        decT = const.tile([P, 256], F32, name="decT")
+        encT = const.tile([P, 1024], F32, name="encT")
+        decT = const.tile([P, 512], F32, name="decT")
         bfc = const.tile([P, V], BF16, name="bfc")
         ident = const.tile([P, P], F32, name="ident")
         bT = const.tile([P, 8], F32, name="bT")
@@ -56,7 +55,7 @@ def tile_jointnet_kernel(
         warm2 = const.tile([P, 8], F32, name="warm2")
         one = const.tile([P, 1], F32, name="one")
         shift = const.tile([P, 1], F32, name="shift")
-        amat = const.tile([P, (HALVES - OLD) * 1024], BF16, name="amat")
+        amat = const.tile([P, 16 * 1024], BF16, name="amat")
         pick = const.tile([P, 256], BF16, name="pick")
         piece = [const.tile([P, 3072], BF16, name="piece%d" % q) for q in range(3)]
         rest = const.tile([P, 3072], F32, name="rest")
@@ -67,14 +66,17 @@ def tile_jointnet_kernel(
         cbank, ybank, zbt, negm, xx, st = {}, {}, {}, {}, {}, {}
         nat_ps = {}
 
-        def add(h, g, eng):
-            comb[h, g] = work.tile([P, 1024], F32, name="comb", tag="comb", bufs=2 * OLD)
-            b = h // 2
+        def add(h, g, eng, t0=0, t1=16):
+            if (h, g) not in comb:
+                comb[h, g] = work.tile([P, 1024], F32, name="comb", tag="comb", bufs=6)
+            b, nt = h // 2, t1 - t0
             dec = dec_ps[g] if eng == "V" else dec_v[:, g, :, :]
             (nc.vector if eng == "V" else nc.gpsimd).tensor_tensor(
-                out=comb[h, g][:].rearrange("p (t u j) -> p t u j", t=16, u=U),
-                in0=enc_v[:, g, h * 16 : (h + 1) * 16, :].unsqueeze(2).to_broadcast([P, 16, U, 4]),
-                in1=dec[:, b * U : (b + 1) * U, :].unsqueeze(1).to_broadcast([P, 16, U, 4]),
+                out=comb[h, g][:, t0 * 64 : t1 * 64].rearrange("p (t u j) -> p t u j", t=nt, u=U),
+                in0=enc_v[:, g, h * 16 + t0 : h * 16 + t1, :]
+                .unsqueeze(2)
+                .to_broadcast([P, nt, U, 4]),
+                in1=dec[:, b * U : (b + 1) * U, :].unsqueeze(1).to_broadcast([P, nt, U, 4]),
                 op=ALU.add,
             )
 
@@ -95,7 +97,7 @@ def tile_jointnet_kernel(
             for g in range(2):
                 cbank[i, g] = psum.tile([P, 512], F32, name="cb", tag="cb")
                 for j in range(4):
-                    c0 = (h - OLD) * 1024 + g * 512 + j * P
+                    c0 = h * 1024 + g * 512 + j * P
                     nc.tensor.matmul(
                         out=cbank[i, g][:, j * P : (j + 1) * P],
                         lhsT=amat[:, c0 : c0 + P],
@@ -165,18 +167,22 @@ def tile_jointnet_kernel(
                 out=piece[2][:, cols], in0=rest[:, cols], in1=piece[1][:, cols], op=ALU.subtract
             )
 
-        def move_rows(h):
-            b, s = divmod(h, 2)
-            a0 = (h - OLD) * 1024
-            e0, p0 = b // 4 * 1024, b % 4 * 32 + s * 16
+        def move_rows(b):
+            halves = [h for h in (2 * b, 2 * b + 1) if h not in ADDED]
+            n = len(halves)
+            a0 = halves[0] * 1024
             for q in range(3):
+                for h in halves:
+                    p0 = b % 4 * 32 + h % 2 * 16
+                    nc.sync.dma_start(
+                        out=amat[16 * q : 16 * (q + 1), h * 1024 : (h + 1) * 1024],
+                        in_=piece[q][p0 : p0 + 16, b // 4 * 1024 : (b // 4 + 1) * 1024],
+                    )
                 nc.sync.dma_start(
-                    out=amat[16 * q : 16 * (q + 1), a0 : a0 + 1024],
-                    in_=piece[q][p0 : p0 + 16, e0 : e0 + 1024],
-                )
-                nc.sync.dma_start(
-                    out=amat[48 + 16 * q : 64 + 16 * q, a0 : a0 + 1024],
-                    in_=piece[q][b * U : (b + 1) * U, 2048:3072],
+                    out=amat[48 + 16 * q : 64 + 16 * q, a0 : a0 + n * 1024].rearrange(
+                        "p (n x) -> p n x", n=n
+                    ),
+                    in_=piece[q][b * U : (b + 1) * U, 2048:3072].unsqueeze(1).to_broadcast([U, n, 1024]),
                 )
 
         def zrow(i):
@@ -229,14 +235,16 @@ def tile_jointnet_kernel(
             if step == "ab":
                 nc.scalar.activation(out=small(grp, "ab")[:, 0:c], in_=z0, func=ACT.Abs)
             elif step == "zc":
-                nc.gpsimd.tensor_copy(out=wv[:, 0, :], in_=z0)
+                nc.gpsimd.tensor_scalar(
+                    out=wv[:, 0, :], in0=z0, scalar1=1.0, scalar2=0.0, op0=ALU.mult, op1=ALU.add
+                )
             elif step == "mc":
                 nc.gpsimd.tensor_scalar(
                     out=wv[:, 1, :], in0=negm[b][:, n0:n1], scalar1=-1.0, scalar2=0.0, op0=ALU.mult, op1=ALU.add
                 )
             elif step == "mx":
                 nc.gpsimd.tensor_scalar(
-                    out=wv[:, 4, :], in0=z0, scalar1=1.0, scalar2=0.0, op0=ALU.mult, op1=ALU.max
+                    out=wv[:, 4, :], in0=z0, scalar1=3.0e38, scalar2=0.0, op0=ALU.min, op1=ALU.max
                 )
             elif step == "ev":
                 nc.scalar.activation(
@@ -425,16 +433,16 @@ def tile_jointnet_kernel(
                 if r == 2:
                     dec_ps[g] = view
                 else:
-                    w = OLD * 16
-                    nc.vector.tensor_tensor(
-                        out=enc_v[:, g, :, :],
-                        in0=view[:, 0:w, :],
-                        in1=bsum[:, g * 4 : (g + 1) * 4].unsqueeze(1).to_broadcast([P, w, 4]),
-                        op=ALU.add,
-                    )
+                    for w0, w1 in ((0, 32), (112, 128)):
+                        nc.vector.tensor_tensor(
+                            out=enc_v[:, g, w0:w1, :],
+                            in0=view[:, w0:w1, :],
+                            in1=bsum[:, g * 4 : (g + 1) * 4].unsqueeze(1).to_broadcast([P, w1 - w0, 4]),
+                            op=ALU.add,
+                        )
 
             def dec_copy(g):
-                nc.vector.tensor_copy(out=dec_v[:, g, :, :], in_=dec_ps[g][:, 0:32, :])
+                nc.vector.tensor_copy(out=dec_v[:, g, :, :], in_=dec_ps[g][:, 0:64, :])
 
             wf32 = wf[:].bitcast(F32).rearrange("p (r g x) -> p r g x", r=8, g=2)
 
@@ -452,6 +460,8 @@ def tile_jointnet_kernel(
 
             weights(we, weg, wec, wes, 0)
             weights(wd, wdg, wdc, wds, 0)
+            weights(we, weg, wec, wes, 1)
+            weights(wd, wdg, wdc, wds, 1)
             ptb = psum.tile([P, 512], F32, name="ptb", tag="bank")
             nc.tensor.transpose(out=ptb[:, 0:P], in_=braw[:].bitcast(F32), identity=ident[:])
             nc.vector.tensor_copy(out=bT[:], in_=ptb[:, 0:8])
@@ -461,8 +471,8 @@ def tile_jointnet_kernel(
             project(0, 0)
             dec_copy(0)
             add(1, 0, "G")
-            weights(we, weg, wec, wes, 1)
-            weights(wd, wdg, wdc, wds, 1)
+            fc_weights(0, 0, "S")
+            fc_weights(0, 1, "S")
             project(1, 2)
             project(1, 0)
             natural(0, 0)
@@ -470,47 +480,42 @@ def tile_jointnet_kernel(
             natural(0, 1)
             natural(2, 1)
             add(0, 0, "V")
+            for src, g in ((0, 0), (2, 0), (0, 1), (2, 1)):
+                split_a(src, g)
+                split_b(src, g)
             add(0, 1, "V")
-            split_a(0, 0)
-            split_a(2, 0)
-            split_b(0, 0)
-            split_b(2, 0)
-            split_a(0, 1)
-            split_a(2, 1)
-            split_b(0, 1)
-            split_b(2, 1)
             nc.vector.tensor_copy(
                 out=bperm[96:128, :].rearrange("p (c e w) -> p c e w", c=4, e=2),
                 in_=brow[96:128, :].rearrange("p (c w e) -> p c e w", c=4, e=2),
             )
-            nc.sync.dma_start(
-                out=amat[96:128, :].rearrange("p (h x) -> p h x", x=1024),
-                in_=bperm[96:128, :].unsqueeze(1).to_broadcast([32, HALVES - OLD, 1024]),
-            )
-            for h in range(OLD, 8):
-                move_rows(h)
-            fc_weights(0, 0, "S")
-            fc_weights(0, 1, "S")
-            dec_copy(1)
+            for h0, h1 in ((2, 4), (4, 16)):
+                nc.sync.dma_start(
+                    out=amat[96:128, h0 * 1024 : h1 * 1024].rearrange("p (h x) -> p h x", x=1024),
+                    in_=bperm[96:128, :].unsqueeze(1).to_broadcast([32, h1 - h0, 1024]),
+                )
+                if h0 == 2:
+                    move_rows(1)
+            for b in (2, 3):
+                move_rows(b)
+            fc_weights(2, 0, "S")
             tanh_old(0, 0)
             tanh_old(0, 1)
             add(1, 1, "V")
-            add(2, 0, "G")
-            add(2, 1, "G")
-            fc_weights(2, 0, "V")
+            dec_copy(1)
             fc_weights(2, 1, "S")
-            fc_weights(4, 0, "V")
             fc_quant(0, 0)
             fc_quant(1, 0)
-            fc_weights(4, 1, "S")
+            fc_weights(4, 0, "S")
             quant(0)
-            fc_weights(6, 0, "S")
-            fc_weights(6, 1, "V")
+            fc_weights(4, 1, "S")
+            fc_weights(6, 0, "V")
+            fc_weights(6, 1, "S")
             fc_quant(0, 1)
             fc_quant(1, 1)
             tanh_old(1, 0)
             tanh_old(1, 1)
             matmul(0)
+            comb_mm(4)
 
         zpool = ctx.enter_context(tc.tile_pool(name="zpool", bufs=5))
 
@@ -542,93 +547,114 @@ def tile_jointnet_kernel(
                 matmul(i)
 
         def hidden(i, g):
-            if i < 2 * OLD:
-                tanh_old(OLD - 1, 0 if i == 2 * OLD - 2 else 1) if g == 0 else None
-            elif tile_ok(i):
+            h, n = divmod(i, 2)
+            if h not in ADDED:
                 tanh(i, g)
+            elif n == 0:
+                tanh_old(h, g)
 
         def cmm(i):
-            if 2 * OLD <= i < 4 * B:
+            if tile_ok(i) and i // 2 not in ADDED:
                 comb_mm(i)
 
-        for u in range(0, B - 1):
+        gate = const.tile([P, 8], F32, name="gate")
+
+        def hold(i):
+            nc.gpsimd.tensor_scalar(
+                out=gate[:, 0:1], in0=zrow(i)[:, 0:1], scalar1=1.0, scalar2=0.0, op0=ALU.mult, op1=ALU.add
+            )
+
+        def new_entry(u):
             zbt[u] = zpool.tile([P, 4 * V], F32, name="zb", tag="zb")
             negm[u] = stat.tile([P, 4], F32, name="negm", tag="negm")
             xx[u] = stat.tile([P, 16], F32, name="xx", tag="xx")
+
+        for u in range(0, B - 1):
+            new_entry(u)
             i = 4 * u
-            badd(i, 0)
-            badd(i, 1)
-            rmax(i - 1)
             quant(i // 2 + 1)
-            esum(i - 2)
+            badd(i, 0)
+            rmax(i - 1)
+            badd(i, 1)
             hidden(i + 4, 0)
             hidden(i + 4, 1)
             on(u - 2, "t1")
             on(u - 2, "g2")
+            esum(i - 1)
+            hold(i)
             fin(u - 3, 2)
+            if u == 1:
+                add(7, 0, "G", 0, 8)
             mm(i + 1)
             cmm(i + 5)
 
             i = 4 * u + 1
             badd(i, 0)
-            badd(i, 1)
             rmax(i - 1)
+            badd(i, 1)
             if u == 1:
                 natural(1, 0)
                 natural(1, 1)
                 split_a(1, 0)
-            esum(i - 2)
             hidden(i + 4, 0)
+            hidden(i + 4, 1)
             for step in ("ab", "zc", "mc", "mx", "ev", "q"):
                 on(u - 1, step)
-            hidden(i + 4, 1)
             on(u - 2, "t2")
             on(u - 2, "g3")
+            esum(i - 1)
+            hold(i)
             fin(u - 3, 3)
+            on(u - 2, "t3")
+            if u == 1:
+                add(7, 0, "G", 8, 16)
             mm(i + 1)
             cmm(i + 5)
 
             i = 4 * u + 2
-            badd(i, 0)
+            quant(i // 2 + 1)
             on(u - 1, "x0")
-            badd(i, 1)
-            on(u - 2, "t3")
+            badd(i, 0)
             rmax(i - 1)
             on(u - 2, "lg")
-            quant(i // 2 + 1)
+            badd(i, 1)
             on(u - 2, "z0")
             on(u - 2, "nc")
             if u == 1:
                 split_a(1, 1)
                 split_b(1, 0)
                 split_b(1, 1)
-                for h in range(8, 16):
-                    move_rows(h)
-            esum(i - 2)
+                for b in range(4, 8):
+                    move_rows(b)
             hidden(i + 4, 0)
             hidden(i + 4, 1)
+            esum(i - 1)
             on(u - 1, "g0")
+            hold(i)
             fin(u - 2, 0)
+            if u == 1:
+                add(7, 1, "G", 0, 8)
             mm(i + 1)
             cmm(i + 5)
 
             i = 4 * u + 3
             badd(i, 0)
-            badd(i, 1)
             rmax(i - 1)
-            esum(i - 2)
+            badd(i, 1)
             hidden(i + 4, 0)
             hidden(i + 4, 1)
             on(u - 1, "t0")
             on(u - 1, "g1")
+            esum(i - 1)
+            hold(i)
             fin(u - 2, 1)
+            if u == 1:
+                add(7, 1, "G", 8, 16)
             mm(i + 1)
             cmm(i + 5)
 
         u = B - 1
-        zbt[u] = zpool.tile([P, 4 * V], F32, name="zb", tag="zb")
-        negm[u] = stat.tile([P, 4], F32, name="negm", tag="negm")
-        xx[u] = stat.tile([P, 16], F32, name="xx", tag="xx")
+        new_entry(u)
         ga, gb, gc, gd = (u - 2, 0, 4), (u - 1, 0, 4), (u, 0, 2), (u, 2, 4)
         i = 4 * u
 
@@ -637,62 +663,68 @@ def tile_jointnet_kernel(
                 chain(grp, name)
 
         prep = ("ab", "zc", "mc", "mx", "ev", "q")
-        badd(i, 0)
-        esum(i - 2)
-        steps(ga, ("t1", "g2", "t2"))
-        badd(i, 1)
-        rmax(i - 1)
-        fin(u - 3, 2)
         quant(i // 2 + 1)
+        badd(i, 0)
+        rmax(i - 1)
+        badd(i, 1)
+        steps(ga, ("t1", "g2", "t2", "g3", "t3"))
+        fin(u - 3, 2)
         esum(i - 1)
-        steps(ga, ("g3", "t3"))
-        fin(u - 3, 3)
-        mm(i + 1)
         steps(gb, prep)
+        mm(i + 1)
+
         badd(i + 1, 0)
         chain(ga, "lg")
-        badd(i + 1, 1)
-        chain(ga, "z0")
-        chain(ga, "nc")
         rmax(i)
-        mm(i + 2)
+        chain(ga, "z0")
+        badd(i + 1, 1)
+        chain(ga, "nc")
         chain(gb, "x0")
+        fin(u - 3, 3)
+        esum(i)
+        steps(gb, ("g0", "t0"))
         finish(4 * (u - 2) + 0, ga, "G")
         finish(4 * (u - 2) + 3, ga, "S")
-        steps(gb, ("g0", "t0"))
-        esum(i)
-        finish(4 * (u - 2) + 1, ga, "G")
         steps(gb, ("g1", "t1"))
+        mm(i + 2)
+
         badd(i + 2, 0)
-        badd(i + 2, 1)
         rmax(i + 1)
-        mm(i + 3)
-        finish(4 * (u - 2) + 2, ga, "G")
+        badd(i + 2, 1)
+        finish(4 * (u - 2) + 1, ga, "G")
+        chain(gb, "g2")
+        chain(gb, "t2")
         esum(i + 1)
-        steps(gb, ("g2", "t2"))
-        steps(gc, prep)
         steps(gb, ("g3", "t3"))
+        steps(gc, prep)
+        finish(4 * (u - 2) + 2, ga, "G")
+        mm(i + 3)
+
         badd(i + 3, 0)
-        badd(i + 3, 1)
         rmax(i + 2)
-        chain(gc, "x0")
         chain(gb, "lg")
+        badd(i + 3, 1)
+        chain(gb, "z0")
+        chain(gb, "nc")
+        chain(gc, "x0")
         steps(gc, ("g0", "t0"))
         esum(i + 2)
         steps(gd, ("ab", "zc", "mx", "ev", "q"))
+        finish(4 * (u - 1) + 0, gb, "G")
         rmax(i + 3)
-        chain(gb, "z0")
-        chain(gb, "nc")
-        steps(gc, ("g1", "t1"))
-        esum(i + 3)
-        finish(4 * (u - 1) + 0, gb, "V")
+        steps(gc, ("g1",))
         finish(4 * (u - 1) + 1, gb, "V")
-        steps(gc, ("g2", "t2"))
-        chain(gd, "x0")
-        steps(gd, ("g0", "mc"))
+        chain(gd, "mc")
+        esum(i + 3)
+        chain(gc, "t1")
+        chain(gc, "g2")
         finish(4 * (u - 1) + 2, gb, "V")
+        chain(gc, "t2")
+        chain(gd, "x0")
+        chain(gd, "g0")
+        chain(gc, "g3")
         chain(gd, "t0")
-        steps(gc, ("g3", "t3"))
+        chain(gc, "t3")
         chain(gd, "g1")
         finish(4 * (u - 1) + 3, gb, "V")
         chain(gd, "t1")
@@ -703,8 +735,8 @@ def tile_jointnet_kernel(
         chain(gd, "t2")
         chain(gd, "g3")
         finish(i, gc, "V")
-        finish(i + 1, gc, "S")
         chain(gd, "t3")
+        finish(i + 1, gc, "S")
         steps(gd, ("lg", "z0", "nc"))
         finish(i + 2, gd, "V")
         finish(i + 3, gd, "S")

@@ -7,7 +7,6 @@ F32 = mybir.dt.float32
 BF16 = mybir.dt.bfloat16
 U32 = mybir.dt.uint32
 U8 = mybir.dt.uint8
-I32 = mybir.dt.int32
 FP8X4 = mybir.dt.float8_e4m3fn_x4
 ALU = mybir.AluOpType
 ACT = mybir.ActivationFunctionType
@@ -20,9 +19,10 @@ FLOPS = 2 * (256 * 512 * 1024 + 128 * 512 * 1024 + 4096 * 1024 * 1024)
 LN2 = 0.6931471805599453
 K1 = LN2 / 8388608.0
 STEPS = 4
-C0 = (0.043 - 127.0) * 8388608.0 - STEPS / K1
+GUESS = (0.043 - 127.0) * LN2 - STEPS
 
-ADDED = (0, 1, 7)
+ADDED = (0, 1, 6)
+PLAIN = (2, 3)
 
 
 def tile_jointnet_kernel(
@@ -46,7 +46,7 @@ def tile_jointnet_kernel(
         wfc = const.tile([P, 2048], U32, name="wfc", align_bytes=64)
         wfs = const.tile([P, 2048], U8, name="wfs", align_bytes=64)
         encT = const.tile([P, 1024], F32, name="encT")
-        decT = const.tile([P, 512], F32, name="decT")
+        decT = const.tile([P, 128], F32, name="decT")
         bfc = const.tile([P, V], BF16, name="bfc")
         ident = const.tile([P, P], F32, name="ident")
         bT = const.tile([P, 8], F32, name="bT")
@@ -55,8 +55,12 @@ def tile_jointnet_kernel(
         warm2 = const.tile([P, 8], F32, name="warm2")
         one = const.tile([P, 1], F32, name="one")
         shift = const.tile([P, 1], F32, name="shift")
+        guess = const.tile([P, 1], F32, name="guess")
         amat = const.tile([P, 16 * 1024], BF16, name="amat")
         pick = const.tile([P, 256], BF16, name="pick")
+        amat32 = const.tile([P, 2 * 1024], F32, name="amat32")
+        pick32 = const.tile([P, 256], F32, name="pick32")
+        nat = const.tile([P, 2048], F32, name="nat")
         piece = [const.tile([P, 3072], BF16, name="piece%d" % q) for q in range(3)]
         rest = const.tile([P, 3072], F32, name="rest")
         enc_v = encT[:].rearrange("p (g w j) -> p g w j", g=2, j=4)
@@ -70,13 +74,13 @@ def tile_jointnet_kernel(
             if (h, g) not in comb:
                 comb[h, g] = work.tile([P, 1024], F32, name="comb", tag="comb", bufs=6)
             b, nt = h // 2, t1 - t0
-            dec = dec_ps[g] if eng == "V" else dec_v[:, g, :, :]
+            dec = dec_ps[g][:, b * U : (b + 1) * U, :] if eng == "V" else dec_v[:, g, :, :]
             (nc.vector if eng == "V" else nc.gpsimd).tensor_tensor(
                 out=comb[h, g][:, t0 * 64 : t1 * 64].rearrange("p (t u j) -> p t u j", t=nt, u=U),
                 in0=enc_v[:, g, h * 16 + t0 : h * 16 + t1, :]
                 .unsqueeze(2)
                 .to_broadcast([P, nt, U, 4]),
-                in1=dec[:, b * U : (b + 1) * U, :].unsqueeze(1).to_broadcast([P, nt, U, 4]),
+                in1=dec.unsqueeze(1).to_broadcast([P, nt, U, 4]),
                 op=ALU.add,
             )
 
@@ -94,14 +98,15 @@ def tile_jointnet_kernel(
 
         def comb_mm(i):
             h, n = divmod(i, 2)
+            rows, sel, h0 = (amat32, pick32, 2) if h in PLAIN else (amat, pick, 0)
             for g in range(2):
                 cbank[i, g] = psum.tile([P, 512], F32, name="cb", tag="cb")
                 for j in range(4):
-                    c0 = h * 1024 + g * 512 + j * P
+                    c0 = (h - h0) * 1024 + g * 512 + j * P
                     nc.tensor.matmul(
                         out=cbank[i, g][:, j * P : (j + 1) * P],
-                        lhsT=amat[:, c0 : c0 + P],
-                        rhs=pick[:, n * P : (n + 1) * P],
+                        lhsT=rows[:, c0 : c0 + P],
+                        rhs=sel[:, n * P : (n + 1) * P],
                         start=True,
                         stop=True,
                     )
@@ -151,9 +156,16 @@ def tile_jointnet_kernel(
                 stop=True,
             )
 
-        def split_a(src, g):
+        def nat_copy(src, g):
+            c0 = src // 2 * 1024 + g * 512
+            nc.scalar.copy(out=nat[:, c0 : c0 + 512], in_=nat_ps[src, g][:])
+
+        def split_hi(src, g):
             cols = slice(src * 1024 + g * 512, src * 1024 + (g + 1) * 512)
             nc.scalar.copy(out=piece[0][:, cols], in_=nat_ps[src, g][:])
+
+        def split_rest(src, g):
+            cols = slice(src * 1024 + g * 512, src * 1024 + (g + 1) * 512)
             nc.vector.tensor_tensor(
                 out=rest[:, cols], in0=nat_ps[src, g][:], in1=piece[0][:, cols], op=ALU.subtract
             )
@@ -185,6 +197,17 @@ def tile_jointnet_kernel(
                     in_=piece[q][b * U : (b + 1) * U, 2048:3072].unsqueeze(1).to_broadcast([U, n, 1024]),
                 )
 
+        def move_plain_rows():
+            for h in PLAIN:
+                nc.sync.dma_start(
+                    out=amat32[0:16, (h - 2) * 1024 : (h - 1) * 1024],
+                    in_=nat[16 * h : 16 * (h + 1), 0:1024],
+                )
+            nc.sync.dma_start(
+                out=amat32[16:32, :].rearrange("p (n x) -> p n x", n=2),
+                in_=nat[U : 2 * U, 1024:2048].unsqueeze(1).to_broadcast([U, 2, 1024]),
+            )
+
         def zrow(i):
             b, n = divmod(i, 4)
             return zbt[b][:].rearrange("p (n v) -> p n v", n=4)[:, n, :]
@@ -215,9 +238,6 @@ def tile_jointnet_kernel(
                 accum_out=xx[b][:, n : n + 1],
             )
 
-        def two(ap):
-            return ap.rearrange("p (a c) -> p a c", a=2)
-
         def small(grp, name, width=4):
             st[grp, name] = stat.tile([P, width], F32, name=name, tag=name)
             return st[grp, name]
@@ -227,76 +247,74 @@ def tile_jointnet_kernel(
             c = n1 - n0
             z0 = zbt[b][:].rearrange("p (n v) -> p n v", n=4)[:, n0:n1, 0]
             if step == "ab":
-                st[grp, "w"] = stat.tile([P, 40], F32, name="w", tag="w")
-                st[grp, "tt"] = stat.tile([P, 8 * (STEPS + 1)], F32, name="tt", tag="tt")
-            wv = st[grp, "w"][:].rearrange("p (k c) -> p k c", c=8)[:, :, 0:c]
-            tv = st[grp, "tt"][:].rearrange("p (k a c) -> p k a c", a=2, c=4)[:, :, :, 0:c]
-            xv = two(xx[b][:])[:, :, n0:n1]
+                small(grp, "w", 20)
+            wv = st[grp, "w"][:].rearrange("p (k c) -> p k c", c=4)[:, :, 0:c]
+            tv = xx[b][:].rearrange("p (k a c) -> p k a c", a=2, c=4)[:, :, :, n0:n1]
             if step == "ab":
                 nc.scalar.activation(out=small(grp, "ab")[:, 0:c], in_=z0, func=ACT.Abs)
             elif step == "zc":
-                nc.gpsimd.tensor_scalar(
-                    out=wv[:, 0, :], in0=z0, scalar1=1.0, scalar2=0.0, op0=ALU.mult, op1=ALU.add
-                )
+                nc.scalar.activation(out=wv[:, 0, :], in_=z0, func=ACT.Identity)
             elif step == "mc":
-                nc.gpsimd.tensor_scalar(
-                    out=wv[:, 1, :], in0=negm[b][:, n0:n1], scalar1=-1.0, scalar2=0.0, op0=ALU.mult, op1=ALU.add
+                nc.scalar.activation(
+                    out=wv[:, 1, :], in_=negm[b][:, n0:n1], func=ACT.Identity, scale=-1.0
                 )
             elif step == "mx":
-                nc.gpsimd.tensor_scalar(
-                    out=wv[:, 4, :], in0=z0, scalar1=3.0e38, scalar2=0.0, op0=ALU.min, op1=ALU.max
-                )
+                nc.scalar.activation(out=wv[:, 4, :], in_=z0, func=ACT.Relu)
             elif step == "ev":
                 nc.scalar.activation(
                     out=small(grp, "ev")[:, 0:c], in_=st[grp, "ab"][:, 0:c], func=ACT.Exp, scale=-1.0
                 )
             elif step == "q":
-                nc.gpsimd.tensor_scalar(
-                    out=xx[b][:, 8 + n0 : 8 + n1],
-                    in0=st[grp, "ev"][:, 0:c],
-                    scalar1=1.0,
-                    scalar2=1.0,
-                    op0=ALU.mult,
-                    op1=ALU.add,
+                nc.scalar.activation(
+                    out=tv[:, 0, 1, :],
+                    in_=st[grp, "ev"][:, 0:c],
+                    func=ACT.Identity,
+                    bias=one[:],
+                    scale=1.0,
                 )
             elif step == "x0":
-                nc.vector.tensor_scalar(
-                    out=tv[:, 0, :, :],
-                    in0=two(xx[b][:].bitcast(I32))[:, :, n0:n1],
-                    scalar1=C0,
-                    scalar2=K1,
-                    op0=ALU.add,
-                    op1=ALU.mult,
+                nc.scalar.activation(
+                    out=tv[:, 2 * STEPS + 2, :, :],
+                    in_=xx[b][:, 0:8].bitcast(U32).rearrange("p (a c) -> p a c", a=2)[:, :, n0:n1],
+                    func=ACT.Identity,
+                    bias=guess[:],
+                    scale=K1,
                 )
             elif step[0] == "g":
                 k = int(step[1])
                 nc.scalar.activation(
-                    out=two(small(grp, step, 8)[:])[:, :, 0:c],
-                    in_=tv[:, k, :, :],
+                    out=tv[:, 2 * k + 1, :, :],
+                    in_=tv[:, 2 * k if k else 2 * STEPS + 2, :, :],
                     func=ACT.Exp,
-                    bias=(shift if k == 0 else one)[:],
+                    bias=(one if k else shift)[:],
                     scale=-1.0,
                 )
             elif step[0] == "t":
                 k = int(step[1])
-                (nc.vector if grp == (B - 1, 2, 4) else nc.gpsimd).tensor_tensor(
-                    out=tv[:, k + 1, :, :],
-                    in0=two(st[grp, "g%d" % k][:])[:, :, 0:c],
-                    in1=xv if k == 0 else tv[:, k, :, :],
+                nc.vector.tensor_reduce(
+                    out=tv[:, 2 * k + 2, :, :],
+                    in_=tv[:, 2 * k : 2 * k + 2, :, :].rearrange("p k a c -> p a c k"),
+                    axis=AX.X,
                     op=ALU.mult,
                 )
             elif step == "lg":
                 nc.vector.tensor_reduce(
-                    out=wv[:, 2:4, :], in_=tv.rearrange("p k a c -> p a c k"), axis=AX.X, op=ALU.add
+                    out=wv[:, 2:4, :],
+                    in_=tv[:, 2 : 2 * STEPS + 3 : 2, :, :].rearrange("p k a c -> p a c k"),
+                    axis=AX.X,
+                    op=ALU.add,
                 )
             elif step == "z0":
                 nc.vector.tensor_reduce(
                     out=z0, in_=wv[:, 0:3, :].rearrange("p k c -> p c k"), axis=AX.X, op=ALU.add
                 )
-            elif step == "nc":
+            else:
+                lo, hi = (0, c) if step == "nc" else (0, 2) if step == "nc01" else (2, 4)
+                if lo == 0:
+                    small(grp, "negc")
                 nc.vector.tensor_reduce(
-                    out=small(grp, "negc")[:, 0:c],
-                    in_=wv[:, 1:5, :].rearrange("p k c -> p c k"),
+                    out=st[grp, "negc"][:, lo:hi],
+                    in_=wv[:, 1:5, lo:hi].rearrange("p k c -> p c k"),
                     axis=AX.X,
                     op=ALU.add,
                     negate=True,
@@ -316,16 +334,19 @@ def tile_jointnet_kernel(
             nc.sync.dma_start(out=out_rows[i * P : (i + 1) * P, :], in_=z)
 
         with tc.tile_pool(name="staging", bufs=1) as staging:
-            make_identity(nc, ident[:])
             nc.vector.memset(warm[:], 0.0)
+            brow = staging.tile([P, 1024], BF16, name="brow")
+            nc.vector.memset(brow[96:128, :], 0.0)
+            make_identity(nc, ident[:])
             nc.vector.memset(one[:], 1.0)
             nc.vector.memset(shift[:], -1.0 * STEPS)
+            nc.vector.memset(guess[:], GUESS)
             nc.scalar.activation(out=warm2[:], in_=warm[:], func=ACT.Exp)
+            nc.scalar.copy(out=amat32[:], in_=warm[:, 0:1].to_broadcast([P, 2048]))
             braw = staging.tile([P, 256], BF16, name="braw")
             nc.vector.memset(braw[:], 0.0)
-            brow = staging.tile([P, 1024], BF16, name="brow")
             bperm = staging.tile([P, 1024], BF16, name="bperm")
-            nc.vector.memset(brow[96:128, :], 0.0)
+            bperm32 = staging.tile([P, 1024], F32, name="bperm32")
             xin = staging.tile([P, 1536], BF16, name="xin")
             we = staging.tile([P, 4096], BF16, name="we")
             wd = staging.tile([P, 4096], BF16, name="wd")
@@ -360,25 +381,30 @@ def tile_jointnet_kernel(
                 nc.sync.dma_start(out=wf_dst[:, r0 : r0 + 2, :], in_=wf_src[:, r0 : r0 + 2, :])
             nc.sync.dma_start(out=bfc[:], in_=b_fc.partition_broadcast(P))
 
-            by_t = staging.tile([P, 16], F32, name="by_t")
-            by_u = staging.tile([P, 16], F32, name="by_u")
-            both = staging.tile([P, 1], F32, name="both")
-            nc.vector.tensor_reduce(
-                out=by_t[:], in_=ident[:, 0:48].rearrange("p (q t) -> p t q", q=3), axis=AX.X, op=ALU.add
-            )
-            nc.vector.tensor_reduce(
-                out=by_u[:], in_=ident[:, 48:96].rearrange("p (q t) -> p t q", q=3), axis=AX.X, op=ALU.add
-            )
-            nc.vector.tensor_reduce(out=both[:], in_=ident[:, 96:98], axis=AX.X, op=ALU.add)
-            nc.vector.tensor_scalar(
-                out=by_t[:], in0=by_t[:], scalar1=both[:], scalar2=None, op0=ALU.add
-            )
-            nc.vector.tensor_tensor(
-                out=pick[:].rearrange("p (t u) -> p t u", t=16),
-                in0=by_t[:].unsqueeze(2).to_broadcast([P, 16, U]),
-                in1=by_u[:].unsqueeze(1).to_broadcast([P, 16, U]),
-                op=ALU.add,
-            )
+            for sel, pieces in ((pick32, 1), (pick, 3)):
+                w = 16 * pieces
+                by_t = staging.tile([P, 16], F32, name="by_t%d" % pieces)
+                by_u = staging.tile([P, 16], F32, name="by_u%d" % pieces)
+                both = staging.tile([P, 1], F32, name="both%d" % pieces)
+                for dst, c0 in ((by_t, 0), (by_u, w)):
+                    nc.vector.tensor_reduce(
+                        out=dst[:],
+                        in_=ident[:, c0 : c0 + w].rearrange("p (q t) -> p t q", q=pieces),
+                        axis=AX.X,
+                        op=ALU.add,
+                    )
+                nc.vector.tensor_reduce(
+                    out=both[:], in_=ident[:, 2 * w : 2 * w + 2], axis=AX.X, op=ALU.add
+                )
+                nc.vector.tensor_scalar(
+                    out=by_t[:], in0=by_t[:], scalar1=both[:], scalar2=None, op0=ALU.add
+                )
+                nc.vector.tensor_tensor(
+                    out=sel[:].rearrange("p (t u) -> p t u", t=16),
+                    in0=by_t[:].unsqueeze(2).to_broadcast([P, 16, U]),
+                    in1=by_u[:].unsqueeze(1).to_broadcast([P, 16, U]),
+                    op=ALU.add,
+                )
 
             def turn(srcs, dst32, eng):
                 n = len(srcs) // 2
@@ -415,6 +441,8 @@ def tile_jointnet_kernel(
                     in_=grp[:, g * 2048 : (g + 1) * 2048],
                 )
 
+            enc_ps = {}
+
             def project(g, r):
                 cod, sca = (wec, wes) if r < 2 else (wdc, wds)
                 ps = psum.tile([P, 512], F32, name="ps", tag="bank" if r < 2 else "cb")
@@ -430,19 +458,19 @@ def tile_jointnet_kernel(
                         stop=True,
                     )
                 view = ps[:].rearrange("p (j w) -> p w j", j=4)
-                if r == 2:
-                    dec_ps[g] = view
-                else:
-                    for w0, w1 in ((0, 32), (112, 128)):
-                        nc.vector.tensor_tensor(
-                            out=enc_v[:, g, w0:w1, :],
-                            in0=view[:, w0:w1, :],
-                            in1=bsum[:, g * 4 : (g + 1) * 4].unsqueeze(1).to_broadcast([P, w1 - w0, 4]),
-                            op=ALU.add,
-                        )
+                (dec_ps if r == 2 else enc_ps)[g] = view
+
+            def enc_out(g):
+                for w0, w1 in ((0, 32), (96, 112)):
+                    nc.vector.tensor_tensor(
+                        out=enc_v[:, g, w0:w1, :],
+                        in0=enc_ps[g][:, w0:w1, :],
+                        in1=bsum[:, g * 4 : (g + 1) * 4].unsqueeze(1).to_broadcast([P, w1 - w0, 4]),
+                        op=ALU.add,
+                    )
 
             def dec_copy(g):
-                nc.vector.tensor_copy(out=dec_v[:, g, :, :], in_=dec_ps[g][:, 0:64, :])
+                nc.vector.tensor_copy(out=dec_v[:, g, :, :], in_=dec_ps[g][:, 3 * U : 4 * U, :])
 
             wf32 = wf[:].bitcast(F32).rearrange("p (r g x) -> p r g x", r=8, g=2)
 
@@ -458,6 +486,23 @@ def tile_jointnet_kernel(
                     in_=wfg[g][:, half * 2048 : (half + 1) * 2048],
                 )
 
+            for dst in (bperm, bperm32):
+                nc.gpsimd.tensor_scalar(
+                    out=dst[96:128, :].rearrange("p (c e w) -> p c e w", c=4, e=2),
+                    in0=brow[96:128, :].rearrange("p (c w e) -> p c e w", c=4, e=2),
+                    scalar1=1.0,
+                    scalar2=0.0,
+                    op0=ALU.mult,
+                    op1=ALU.add,
+                )
+            nc.sync.dma_start(
+                out=amat32[32:34, :].rearrange("p (h x) -> p h x", h=2),
+                in_=bperm32[96:98, :].unsqueeze(1).to_broadcast([2, 2, 1024]),
+            )
+            nc.sync.dma_start(
+                out=amat[96:128, 4096:].rearrange("p (h x) -> p h x", x=1024),
+                in_=bperm[96:128, :].unsqueeze(1).to_broadcast([32, 12, 1024]),
+            )
             weights(we, weg, wec, wes, 0)
             weights(wd, wdg, wdc, wds, 0)
             weights(we, weg, wec, wes, 1)
@@ -466,56 +511,49 @@ def tile_jointnet_kernel(
             nc.tensor.transpose(out=ptb[:, 0:P], in_=braw[:].bitcast(F32), identity=ident[:])
             nc.vector.tensor_copy(out=bT[:], in_=ptb[:, 0:8])
             bT16 = bT[:].bitcast(BF16)
-            nc.vector.tensor_tensor(out=bsum[:], in0=bT16[:, 0:8], in1=bT16[:, 8:16], op=ALU.add)
+            fc_weights(0, 0, "S")
             project(0, 2)
             project(0, 0)
-            dec_copy(0)
-            add(1, 0, "G")
-            fc_weights(0, 0, "S")
-            fc_weights(0, 1, "S")
-            project(1, 2)
-            project(1, 0)
             natural(0, 0)
             natural(2, 0)
+            fc_weights(0, 1, "S")
+            nc.vector.tensor_tensor(out=bsum[:], in0=bT16[:, 0:8], in1=bT16[:, 8:16], op=ALU.add)
+            enc_out(0)
+            dec_copy(0)
+            add(0, 0, "V")
+            nat_copy(0, 0)
+            nat_copy(2, 0)
+            project(1, 2)
+            project(1, 0)
             natural(0, 1)
             natural(2, 1)
-            add(0, 0, "V")
-            for src, g in ((0, 0), (2, 0), (0, 1), (2, 1)):
-                split_a(src, g)
-                split_b(src, g)
-            add(0, 1, "V")
-            nc.vector.tensor_copy(
-                out=bperm[96:128, :].rearrange("p (c e w) -> p c e w", c=4, e=2),
-                in_=brow[96:128, :].rearrange("p (c w e) -> p c e w", c=4, e=2),
-            )
-            for h0, h1 in ((2, 4), (4, 16)):
-                nc.sync.dma_start(
-                    out=amat[96:128, h0 * 1024 : h1 * 1024].rearrange("p (h x) -> p h x", x=1024),
-                    in_=bperm[96:128, :].unsqueeze(1).to_broadcast([32, h1 - h0, 1024]),
-                )
-                if h0 == 2:
-                    move_rows(1)
-            for b in (2, 3):
-                move_rows(b)
-            fc_weights(2, 0, "S")
-            tanh_old(0, 0)
-            tanh_old(0, 1)
-            add(1, 1, "V")
+            enc_out(1)
             dec_copy(1)
+            fc_weights(2, 0, "S")
+            add(0, 1, "V")
+            nat_copy(0, 1)
+            nat_copy(2, 1)
+            move_plain_rows()
             fc_weights(2, 1, "S")
+            add(1, 0, "V")
+            fc_weights(4, 0, "V")
+            tanh_old(0, 0)
+            fc_weights(4, 1, "S")
+            tanh_old(0, 1)
             fc_quant(0, 0)
             fc_quant(1, 0)
-            fc_weights(4, 0, "S")
-            quant(0)
-            fc_weights(4, 1, "S")
-            fc_weights(6, 0, "V")
+            add(1, 1, "V")
+            fc_weights(6, 0, "S")
             fc_weights(6, 1, "S")
+            tanh_old(1, 0)
+            quant(0)
             fc_quant(0, 1)
             fc_quant(1, 1)
-            tanh_old(1, 0)
-            tanh_old(1, 1)
-            matmul(0)
             comb_mm(4)
+            natural(0, 0)
+            natural(2, 0)
+            matmul(0)
+            tanh_old(1, 1)
 
         zpool = ctx.enter_context(tc.tile_pool(name="zpool", bufs=5))
 
@@ -559,97 +597,115 @@ def tile_jointnet_kernel(
 
         gate = const.tile([P, 8], F32, name="gate")
 
-        def hold(i):
+        def late_add(i, g, t0):
             nc.gpsimd.tensor_scalar(
                 out=gate[:, 0:1], in0=zrow(i)[:, 0:1], scalar1=1.0, scalar2=0.0, op0=ALU.mult, op1=ALU.add
             )
+            add(6, g, "G", t0, t0 + 8)
 
         def new_entry(u):
             zbt[u] = zpool.tile([P, 4 * V], F32, name="zb", tag="zb")
             negm[u] = stat.tile([P, 4], F32, name="negm", tag="negm")
-            xx[u] = stat.tile([P, 16], F32, name="xx", tag="xx")
+            xx[u] = stat.tile([P, 8 * (2 * STEPS + 3)], F32, name="xx", tag="xx")
 
         for u in range(0, B - 1):
             new_entry(u)
             i = 4 * u
             quant(i // 2 + 1)
             badd(i, 0)
+            if u == 0:
+                for src in (0, 2):
+                    split_hi(src, 0)
+                    split_rest(src, 0)
+                    split_b(src, 0)
+                natural(0, 1)
+                natural(2, 1)
+            on(u - 3, "nc23")
             rmax(i - 1)
-            badd(i, 1)
             hidden(i + 4, 0)
-            hidden(i + 4, 1)
-            on(u - 2, "t1")
             on(u - 2, "g2")
+            hidden(i + 4, 1)
+            on(u - 2, "t2")
+            badd(i, 1)
             esum(i - 1)
-            hold(i)
             fin(u - 3, 2)
+            fin(u - 3, 3)
             if u == 1:
-                add(7, 0, "G", 0, 8)
+                late_add(i, 0, 0)
+            if u == 2:
+                split_rest(1, 0)
+                split_b(1, 0)
+                natural(1, 1)
+                split_hi(1, 1)
             mm(i + 1)
             cmm(i + 5)
 
             i = 4 * u + 1
             badd(i, 0)
+            if u == 0:
+                for src in (0, 2):
+                    split_hi(src, 1)
+                    split_rest(src, 1)
+                    split_b(src, 1)
+                for b in (2, 3):
+                    move_rows(b)
             rmax(i - 1)
-            badd(i, 1)
-            if u == 1:
-                natural(1, 0)
-                natural(1, 1)
-                split_a(1, 0)
+            on(u - 1, "ab")
+            on(u - 1, "zc")
             hidden(i + 4, 0)
-            hidden(i + 4, 1)
-            for step in ("ab", "zc", "mc", "mx", "ev", "q"):
-                on(u - 1, step)
-            on(u - 2, "t2")
             on(u - 2, "g3")
-            esum(i - 1)
-            hold(i)
-            fin(u - 3, 3)
+            on(u - 1, "ev")
+            on(u - 1, "mc")
+            hidden(i + 4, 1)
+            on(u - 1, "q")
+            on(u - 1, "mx")
             on(u - 2, "t3")
+            badd(i, 1)
+            esum(i - 1)
+            on(u - 1, "x0")
             if u == 1:
-                add(7, 0, "G", 8, 16)
+                late_add(i, 1, 0)
+            if u == 2:
+                split_rest(1, 1)
+                split_b(1, 1)
+                for b in range(4, 8):
+                    move_rows(b)
             mm(i + 1)
             cmm(i + 5)
 
             i = 4 * u + 2
             quant(i // 2 + 1)
-            on(u - 1, "x0")
-            badd(i, 0)
-            rmax(i - 1)
             on(u - 2, "lg")
-            badd(i, 1)
+            badd(i, 0)
             on(u - 2, "z0")
-            on(u - 2, "nc")
-            if u == 1:
-                split_a(1, 1)
-                split_b(1, 0)
-                split_b(1, 1)
-                for b in range(4, 8):
-                    move_rows(b)
+            rmax(i - 1)
+            on(u - 2, "nc01")
             hidden(i + 4, 0)
-            hidden(i + 4, 1)
-            esum(i - 1)
             on(u - 1, "g0")
-            hold(i)
-            fin(u - 2, 0)
+            hidden(i + 4, 1)
+            on(u - 1, "t0")
+            badd(i, 1)
+            esum(i - 1)
             if u == 1:
-                add(7, 1, "G", 0, 8)
+                late_add(i, 0, 8)
             mm(i + 1)
             cmm(i + 5)
 
             i = 4 * u + 3
             badd(i, 0)
             rmax(i - 1)
-            badd(i, 1)
             hidden(i + 4, 0)
-            hidden(i + 4, 1)
-            on(u - 1, "t0")
             on(u - 1, "g1")
+            hidden(i + 4, 1)
+            on(u - 1, "t1")
+            badd(i, 1)
             esum(i - 1)
-            hold(i)
+            fin(u - 2, 0)
             fin(u - 2, 1)
             if u == 1:
-                add(7, 1, "G", 8, 16)
+                late_add(i, 1, 8)
+                natural(1, 0)
+                split_hi(1, 0)
             mm(i + 1)
             cmm(i + 5)
 
@@ -662,81 +718,87 @@ def tile_jointnet_kernel(
             for name in names:
                 chain(grp, name)
 
-        prep = ("ab", "zc", "mc", "mx", "ev", "q")
+        prep = ("ab", "zc", "ev", "mc", "q", "mx", "x0")
         quant(i // 2 + 1)
         badd(i, 0)
+        on(u - 3, "nc23")
+        chain(ga, "g2")
         rmax(i - 1)
+        chain(ga, "t2")
         badd(i, 1)
-        steps(ga, ("t1", "g2", "t2", "g3", "t3"))
-        fin(u - 3, 2)
+        chain(ga, "g3")
         esum(i - 1)
         steps(gb, prep)
+        fin(u - 3, 2)
+        fin(u - 3, 3)
         mm(i + 1)
 
         badd(i + 1, 0)
-        chain(ga, "lg")
+        chain(ga, "t3")
         rmax(i)
-        chain(ga, "z0")
+        chain(ga, "lg")
+        chain(gb, "g0")
         badd(i + 1, 1)
+        chain(ga, "z0")
         chain(ga, "nc")
-        chain(gb, "x0")
-        fin(u - 3, 3)
+        chain(gb, "t0")
         esum(i)
-        steps(gb, ("g0", "t0"))
+        chain(gb, "g1")
         finish(4 * (u - 2) + 0, ga, "G")
         finish(4 * (u - 2) + 3, ga, "S")
-        steps(gb, ("g1", "t1"))
         mm(i + 2)
 
         badd(i + 2, 0)
+        chain(gb, "t1")
         rmax(i + 1)
-        badd(i + 2, 1)
-        finish(4 * (u - 2) + 1, ga, "G")
         chain(gb, "g2")
+        badd(i + 2, 1)
         chain(gb, "t2")
+        finish(4 * (u - 2) + 1, ga, "G")
         esum(i + 1)
-        steps(gb, ("g3", "t3"))
+        chain(gb, "g3")
         steps(gc, prep)
         finish(4 * (u - 2) + 2, ga, "G")
         mm(i + 3)
 
         badd(i + 3, 0)
+        chain(gb, "t3")
         rmax(i + 2)
         chain(gb, "lg")
+        chain(gc, "g0")
         badd(i + 3, 1)
         chain(gb, "z0")
         chain(gb, "nc")
-        chain(gc, "x0")
-        steps(gc, ("g0", "t0"))
+        chain(gc, "t0")
         esum(i + 2)
-        steps(gd, ("ab", "zc", "mx", "ev", "q"))
+        chain(gc, "g1")
+        steps(gd, ("ab", "zc", "ev", "mx", "q"))
         finish(4 * (u - 1) + 0, gb, "G")
         rmax(i + 3)
-        steps(gc, ("g1",))
-        finish(4 * (u - 1) + 1, gb, "V")
-        chain(gd, "mc")
-        esum(i + 3)
         chain(gc, "t1")
+        finish(4 * (u - 1) + 1, gb, "V")
         chain(gc, "g2")
-        finish(4 * (u - 1) + 2, gb, "V")
-        chain(gc, "t2")
+        esum(i + 3)
         chain(gd, "x0")
-        chain(gd, "g0")
+        chain(gd, "mc")
+        chain(gc, "t2")
         chain(gc, "g3")
-        chain(gd, "t0")
+        chain(gd, "g0")
+        finish(4 * (u - 1) + 2, gb, "V")
         chain(gc, "t3")
+        chain(gd, "t0")
         chain(gd, "g1")
-        finish(4 * (u - 1) + 3, gb, "V")
-        chain(gd, "t1")
         chain(gc, "lg")
-        chain(gd, "g2")
         chain(gc, "z0")
         chain(gc, "nc")
+        chain(gd, "t1")
+        chain(gd, "g2")
+        finish(4 * (u - 1) + 3, gb, "G")
+        finish(i, gc, "V")
         chain(gd, "t2")
         chain(gd, "g3")
-        finish(i, gc, "V")
-        chain(gd, "t3")
         finish(i + 1, gc, "S")
+        chain(gd, "t3")
         steps(gd, ("lg", "z0", "nc"))
         finish(i + 2, gd, "V")
         finish(i + 3, gd, "S")

@@ -235,31 +235,31 @@ def tile_jointnet_kernel(
                 func=ACT.Exp,
                 bias=negm[b][:, n : n + 1],
                 scale=1.0,
-                accum_out=xx[b][:, n : n + 1],
+                accum_out=xx[b, n // 2 if b == B - 1 else 0][:, n : n + 1],
             )
 
         def small(grp, name, width=4):
             st[grp, name] = stat.tile([P, width], F32, name=name, tag=name)
             return st[grp, name]
 
+        FIRST, EXTRA, BLANK = 2 * STEPS + 2, 2 * STEPS + 4, 2 * STEPS + 6
+
         def chain(grp, step):
             b, n0, n1 = grp
             c = n1 - n0
             z0 = zbt[b][:].rearrange("p (n v) -> p n v", n=4)[:, n0:n1, 0]
-            if step == "ab":
-                small(grp, "w", 20)
-            wv = st[grp, "w"][:].rearrange("p (k c) -> p k c", c=4)[:, :, 0:c]
-            tv = xx[b][:].rearrange("p (k a c) -> p k a c", a=2, c=4)[:, :, :, n0:n1]
+            xt = xx[b, n0 // 2] if b == B - 1 else xx[b, 0]
+            tv = xt[:].rearrange("p (k a c) -> p k a c", a=2, c=4)[:, :, :, n0:n1]
             if step == "ab":
                 nc.scalar.activation(out=small(grp, "ab")[:, 0:c], in_=z0, func=ACT.Abs)
             elif step == "zc":
-                nc.scalar.activation(out=wv[:, 0, :], in_=z0, func=ACT.Identity)
+                nc.scalar.activation(out=tv[:, BLANK, 0, :], in_=z0, func=ACT.Identity)
             elif step == "mc":
                 nc.scalar.activation(
-                    out=wv[:, 1, :], in_=negm[b][:, n0:n1], func=ACT.Identity, scale=-1.0
+                    out=tv[:, EXTRA, 0, :], in_=negm[b][:, n0:n1], func=ACT.Identity, scale=-1.0
                 )
             elif step == "mx":
-                nc.scalar.activation(out=wv[:, 4, :], in_=z0, func=ACT.Relu)
+                nc.scalar.activation(out=tv[:, EXTRA, 1, :], in_=z0, func=ACT.Relu)
             elif step == "ev":
                 nc.scalar.activation(
                     out=small(grp, "ev")[:, 0:c], in_=st[grp, "ab"][:, 0:c], func=ACT.Exp, scale=-1.0
@@ -274,8 +274,8 @@ def tile_jointnet_kernel(
                 )
             elif step == "x0":
                 nc.scalar.activation(
-                    out=tv[:, 2 * STEPS + 2, :, :],
-                    in_=xx[b][:, 0:8].bitcast(U32).rearrange("p (a c) -> p a c", a=2)[:, :, n0:n1],
+                    out=tv[:, FIRST, :, :],
+                    in_=xt[:, 0:8].bitcast(U32).rearrange("p (a c) -> p a c", a=2)[:, :, n0:n1],
                     func=ACT.Identity,
                     bias=guess[:],
                     scale=K1,
@@ -284,38 +284,39 @@ def tile_jointnet_kernel(
                 k = int(step[1])
                 nc.scalar.activation(
                     out=tv[:, 2 * k + 1, :, :],
-                    in_=tv[:, 2 * k if k else 2 * STEPS + 2, :, :],
+                    in_=tv[:, 2 * k if k else FIRST, :, :],
                     func=ACT.Exp,
                     bias=(one if k else shift)[:],
                     scale=-1.0,
                 )
             elif step[0] == "t":
                 k = int(step[1])
+                if b < B - 2:
+                    nc.gpsimd.tensor_tensor(
+                        out=tv[:, 2 * k + 2, :, :],
+                        in0=tv[:, 2 * k, :, :],
+                        in1=tv[:, 2 * k + 1, :, :],
+                        op=ALU.mult,
+                    )
+                else:
+                    nc.vector.tensor_reduce(
+                        out=tv[:, 2 * k + 2, :, :],
+                        in_=tv[:, 2 * k : 2 * k + 2, :, :].rearrange("p k a c -> p a c k"),
+                        axis=AX.X,
+                        op=ALU.mult,
+                    )
+            elif step == "z0":
                 nc.vector.tensor_reduce(
-                    out=tv[:, 2 * k + 2, :, :],
-                    in_=tv[:, 2 * k : 2 * k + 2, :, :].rearrange("p k a c -> p a c k"),
-                    axis=AX.X,
-                    op=ALU.mult,
-                )
-            elif step == "lg":
-                nc.vector.tensor_reduce(
-                    out=wv[:, 2:4, :],
-                    in_=tv[:, 2 : 2 * STEPS + 3 : 2, :, :].rearrange("p k a c -> p a c k"),
+                    out=z0,
+                    in_=tv[:, 2 : BLANK + 1 : 2, 0, :].rearrange("p k c -> p c k"),
                     axis=AX.X,
                     op=ALU.add,
                 )
-            elif step == "z0":
-                nc.vector.tensor_reduce(
-                    out=z0, in_=wv[:, 0:3, :].rearrange("p k c -> p c k"), axis=AX.X, op=ALU.add
-                )
             else:
-                lo, hi = (0, c) if step == "nc" else (0, 2) if step == "nc01" else (2, 4)
-                if lo == 0:
-                    small(grp, "negc")
                 nc.vector.tensor_reduce(
-                    out=st[grp, "negc"][:, lo:hi],
-                    in_=wv[:, 1:5, lo:hi].rearrange("p k c -> p c k"),
-                    axis=AX.X,
+                    out=small(grp, "negc")[:, 0:c],
+                    in_=tv[:, 2 : EXTRA + 1 : 2, :, :].rearrange("p k a c -> p c k a"),
+                    axis=AX.XY,
                     op=ALU.add,
                     negate=True,
                 )
@@ -512,12 +513,14 @@ def tile_jointnet_kernel(
             nc.vector.tensor_copy(out=bT[:], in_=ptb[:, 0:8])
             bT16 = bT[:].bitcast(BF16)
             fc_weights(0, 0, "S")
+            fc_weights(0, 1, "S")
+            fc_weights(2, 0, "V")
+            nc.vector.tensor_tensor(out=bsum[:], in0=bT16[:, 0:8], in1=bT16[:, 8:16], op=ALU.add)
             project(0, 2)
             project(0, 0)
             natural(0, 0)
             natural(2, 0)
-            fc_weights(0, 1, "S")
-            nc.vector.tensor_tensor(out=bsum[:], in0=bT16[:, 0:8], in1=bT16[:, 8:16], op=ALU.add)
+            fc_weights(2, 1, "S")
             enc_out(0)
             dec_copy(0)
             add(0, 0, "V")
@@ -529,21 +532,19 @@ def tile_jointnet_kernel(
             natural(2, 1)
             enc_out(1)
             dec_copy(1)
-            fc_weights(2, 0, "S")
             add(0, 1, "V")
             nat_copy(0, 1)
             nat_copy(2, 1)
             move_plain_rows()
-            fc_weights(2, 1, "S")
+            fc_weights(4, 0, "S")
             add(1, 0, "V")
-            fc_weights(4, 0, "V")
-            tanh_old(0, 0)
             fc_weights(4, 1, "S")
+            tanh_old(0, 0)
+            fc_weights(6, 0, "S")
             tanh_old(0, 1)
             fc_quant(0, 0)
             fc_quant(1, 0)
             add(1, 1, "V")
-            fc_weights(6, 0, "S")
             fc_weights(6, 1, "S")
             tanh_old(1, 0)
             quant(0)
@@ -606,11 +607,13 @@ def tile_jointnet_kernel(
         def new_entry(u):
             zbt[u] = zpool.tile([P, 4 * V], F32, name="zb", tag="zb")
             negm[u] = stat.tile([P, 4], F32, name="negm", tag="negm")
-            xx[u] = stat.tile([P, 8 * (2 * STEPS + 3)], F32, name="xx", tag="xx")
+            for k in range(2 if u == B - 1 else 1):
+                xx[u, k] = stat.tile([P, 8 * (2 * STEPS + 7)], F32, name="xx", tag="xx")
 
         for u in range(0, B - 1):
             new_entry(u)
             i = 4 * u
+            on(u - 2, "nc")
             quant(i // 2 + 1)
             badd(i, 0)
             if u == 0:
@@ -620,23 +623,16 @@ def tile_jointnet_kernel(
                     split_b(src, 0)
                 natural(0, 1)
                 natural(2, 1)
-            on(u - 3, "nc23")
             rmax(i - 1)
             hidden(i + 4, 0)
-            on(u - 2, "g2")
             hidden(i + 4, 1)
-            on(u - 2, "t2")
             badd(i, 1)
             esum(i - 1)
-            fin(u - 3, 2)
-            fin(u - 3, 3)
+            fin(u - 2, 0)
+            fin(u - 2, 1)
             if u == 1:
                 late_add(i, 0, 0)
-            if u == 2:
-                split_rest(1, 0)
-                split_b(1, 0)
-                natural(1, 1)
-                split_hi(1, 1)
+                add(6, 0, "G", 8, 16)
             mm(i + 1)
             cmm(i + 5)
 
@@ -653,59 +649,61 @@ def tile_jointnet_kernel(
             on(u - 1, "ab")
             on(u - 1, "zc")
             hidden(i + 4, 0)
-            on(u - 2, "g3")
             on(u - 1, "ev")
             on(u - 1, "mc")
             hidden(i + 4, 1)
             on(u - 1, "q")
             on(u - 1, "mx")
-            on(u - 2, "t3")
             badd(i, 1)
             esum(i - 1)
             on(u - 1, "x0")
+            fin(u - 2, 2)
+            fin(u - 2, 3)
             if u == 1:
                 late_add(i, 1, 0)
-            if u == 2:
-                split_rest(1, 1)
-                split_b(1, 1)
-                for b in range(4, 8):
-                    move_rows(b)
+                add(6, 1, "G", 8, 16)
+                natural(1, 0)
+                split_hi(1, 0)
             mm(i + 1)
             cmm(i + 5)
 
             i = 4 * u + 2
             quant(i // 2 + 1)
-            on(u - 2, "lg")
             badd(i, 0)
-            on(u - 2, "z0")
             rmax(i - 1)
-            on(u - 2, "nc01")
-            hidden(i + 4, 0)
             on(u - 1, "g0")
-            hidden(i + 4, 1)
             on(u - 1, "t0")
+            hidden(i + 4, 0)
+            on(u - 1, "g1")
+            on(u - 1, "t1")
+            hidden(i + 4, 1)
+            on(u - 1, "g2")
+            on(u - 1, "t2")
             badd(i, 1)
             esum(i - 1)
             if u == 1:
-                late_add(i, 0, 8)
+                split_rest(1, 0)
+                split_b(1, 0)
+                natural(1, 1)
+                split_hi(1, 1)
             mm(i + 1)
             cmm(i + 5)
 
             i = 4 * u + 3
             badd(i, 0)
             rmax(i - 1)
+            on(u - 1, "g3")
+            on(u - 1, "t3")
             hidden(i + 4, 0)
-            on(u - 1, "g1")
             hidden(i + 4, 1)
-            on(u - 1, "t1")
             badd(i, 1)
+            on(u - 1, "z0")
             esum(i - 1)
-            fin(u - 2, 0)
-            fin(u - 2, 1)
             if u == 1:
-                late_add(i, 1, 8)
-                natural(1, 0)
-                split_hi(1, 0)
+                split_rest(1, 1)
+                split_b(1, 1)
+                for b in range(4, 8):
+                    move_rows(b)
             mm(i + 1)
             cmm(i + 5)
 
@@ -718,87 +716,72 @@ def tile_jointnet_kernel(
             for name in names:
                 chain(grp, name)
 
-        prep = ("ab", "zc", "ev", "mc", "q", "mx", "x0")
+        chain(ga, "nc")
+        rmax(i - 1)
         quant(i // 2 + 1)
         badd(i, 0)
-        on(u - 3, "nc23")
-        chain(ga, "g2")
-        rmax(i - 1)
-        chain(ga, "t2")
+        steps(gb, ("ab", "zc", "ev", "mx", "q"))
         badd(i, 1)
-        chain(ga, "g3")
         esum(i - 1)
-        steps(gb, prep)
-        fin(u - 3, 2)
-        fin(u - 3, 3)
+        steps(gb, ("mc", "x0", "g0"))
+        finish(4 * (u - 2) + 0, ga, "G")
+        finish(4 * (u - 2) + 1, ga, "G")
         mm(i + 1)
 
         badd(i + 1, 0)
-        chain(ga, "t3")
-        rmax(i)
-        chain(ga, "lg")
-        chain(gb, "g0")
-        badd(i + 1, 1)
-        chain(ga, "z0")
-        chain(ga, "nc")
         chain(gb, "t0")
-        esum(i)
+        finish(4 * (u - 2) + 2, ga, "G")
         chain(gb, "g1")
-        finish(4 * (u - 2) + 0, ga, "G")
+        badd(i + 1, 1)
+        chain(gb, "t1")
+        chain(gb, "g2")
         finish(4 * (u - 2) + 3, ga, "S")
+        rmax(i)
+        chain(gb, "t2")
+        chain(gb, "g3")
+        esum(i)
         mm(i + 2)
 
         badd(i + 2, 0)
-        chain(gb, "t1")
+        chain(gb, "t3")
         rmax(i + 1)
-        chain(gb, "g2")
+        chain(gb, "nc")
+        chain(gb, "z0")
         badd(i + 2, 1)
-        chain(gb, "t2")
-        finish(4 * (u - 2) + 1, ga, "G")
+        steps(gc, ("ab", "zc", "ev", "mx", "q"))
         esum(i + 1)
-        chain(gb, "g3")
-        steps(gc, prep)
-        finish(4 * (u - 2) + 2, ga, "G")
+        steps(gc, ("mc", "x0", "g0"))
+        finish(4 * (u - 1) + 0, gb, "G")
+        finish(4 * (u - 1) + 1, gb, "G")
         mm(i + 3)
 
         badd(i + 3, 0)
-        chain(gb, "t3")
         rmax(i + 2)
-        chain(gb, "lg")
-        chain(gc, "g0")
-        badd(i + 3, 1)
-        chain(gb, "z0")
-        chain(gb, "nc")
         chain(gc, "t0")
-        esum(i + 2)
         chain(gc, "g1")
-        steps(gd, ("ab", "zc", "ev", "mx", "q"))
-        finish(4 * (u - 1) + 0, gb, "G")
-        rmax(i + 3)
+        finish(4 * (u - 1) + 2, gb, "G")
+        badd(i + 3, 1)
         chain(gc, "t1")
-        finish(4 * (u - 1) + 1, gb, "V")
         chain(gc, "g2")
-        esum(i + 3)
-        chain(gd, "x0")
-        chain(gd, "mc")
+        esum(i + 2)
+        rmax(i + 3)
         chain(gc, "t2")
+        steps(gd, ("ab", "zc", "ev", "mx", "q"))
         chain(gc, "g3")
-        chain(gd, "g0")
-        finish(4 * (u - 1) + 2, gb, "V")
+        esum(i + 3)
+        steps(gd, ("x0", "g0", "mc"))
         chain(gc, "t3")
+        finish(4 * (u - 1) + 3, gb, "V")
+        chain(gc, "nc")
+        chain(gc, "z0")
         chain(gd, "t0")
         chain(gd, "g1")
-        chain(gc, "lg")
-        chain(gc, "z0")
-        chain(gc, "nc")
+        finish(i, gc, "V")
         chain(gd, "t1")
         chain(gd, "g2")
-        finish(4 * (u - 1) + 3, gb, "G")
-        finish(i, gc, "V")
+        finish(i + 1, gc, "S")
         chain(gd, "t2")
         chain(gd, "g3")
-        finish(i + 1, gc, "S")
-        chain(gd, "t3")
-        steps(gd, ("lg", "z0", "nc"))
+        steps(gd, ("t3", "nc", "z0"))
         finish(i + 2, gd, "V")
         finish(i + 3, gd, "S")

@@ -21,8 +21,7 @@ K1 = LN2 / 8388608.0
 STEPS = 4
 GUESS = (0.043 - 127.0) * LN2 - STEPS
 
-ADDED = (0, 1, 6)
-PLAIN = (2, 3)
+ADDED = 3
 
 
 def tile_jointnet_kernel(
@@ -45,8 +44,7 @@ def tile_jointnet_kernel(
         wds = const.tile([P, 1024], U8, name="wds", align_bytes=64)
         wfc = const.tile([P, 2048], U32, name="wfc", align_bytes=64)
         wfs = const.tile([P, 2048], U8, name="wfs", align_bytes=64)
-        encT = const.tile([P, 1024], F32, name="encT")
-        decT = const.tile([P, 128], F32, name="decT")
+        encT = const.tile([P, ADDED * 128], F32, name="encT")
         bfc = const.tile([P, V], BF16, name="bfc")
         ident = const.tile([P, P], F32, name="ident")
         bT = const.tile([P, 8], F32, name="bT")
@@ -58,29 +56,21 @@ def tile_jointnet_kernel(
         guess = const.tile([P, 1], F32, name="guess")
         amat = const.tile([P, 16 * 1024], BF16, name="amat")
         pick = const.tile([P, 256], BF16, name="pick")
-        amat32 = const.tile([P, 2 * 1024], F32, name="amat32")
-        pick32 = const.tile([P, 256], F32, name="pick32")
-        nat = const.tile([P, 2048], F32, name="nat")
         piece = [const.tile([P, 3072], BF16, name="piece%d" % q) for q in range(3)]
         rest = const.tile([P, 3072], F32, name="rest")
         enc_v = encT[:].rearrange("p (g w j) -> p g w j", g=2, j=4)
-        dec_v = decT[:].rearrange("p (g w j) -> p g w j", g=2, j=4)
 
         comb, hid, hc, hs, dec_ps = {}, {}, {}, {}, {}
         cbank, ybank, zbt, negm, xx, st = {}, {}, {}, {}, {}, {}
         nat_ps = {}
 
-        def add(h, g, eng, t0=0, t1=16):
-            if (h, g) not in comb:
-                comb[h, g] = work.tile([P, 1024], F32, name="comb", tag="comb", bufs=6)
-            b, nt = h // 2, t1 - t0
-            dec = dec_ps[g][:, b * U : (b + 1) * U, :] if eng == "V" else dec_v[:, g, :, :]
-            (nc.vector if eng == "V" else nc.gpsimd).tensor_tensor(
-                out=comb[h, g][:, t0 * 64 : t1 * 64].rearrange("p (t u j) -> p t u j", t=nt, u=U),
-                in0=enc_v[:, g, h * 16 + t0 : h * 16 + t1, :]
-                .unsqueeze(2)
-                .to_broadcast([P, nt, U, 4]),
-                in1=dec.unsqueeze(1).to_broadcast([P, nt, U, 4]),
+        def add(h, g):
+            comb[h, g] = work.tile([P, 1024], F32, name="comb", tag="comb", bufs=2 * ADDED)
+            b = h // 2
+            nc.vector.tensor_tensor(
+                out=comb[h, g][:].rearrange("p (t u j) -> p t u j", t=16, u=U),
+                in0=enc_v[:, g, h * 16 : (h + 1) * 16, :].unsqueeze(2).to_broadcast([P, 16, U, 4]),
+                in1=dec_ps[g][:, b * U : (b + 1) * U, :].unsqueeze(1).to_broadcast([P, 16, U, 4]),
                 op=ALU.add,
             )
 
@@ -98,15 +88,14 @@ def tile_jointnet_kernel(
 
         def comb_mm(i):
             h, n = divmod(i, 2)
-            rows, sel, h0 = (amat32, pick32, 2) if h in PLAIN else (amat, pick, 0)
             for g in range(2):
                 cbank[i, g] = psum.tile([P, 512], F32, name="cb", tag="cb")
                 for j in range(4):
-                    c0 = (h - h0) * 1024 + g * 512 + j * P
+                    c0 = h * 1024 + g * 512 + j * P
                     nc.tensor.matmul(
                         out=cbank[i, g][:, j * P : (j + 1) * P],
-                        lhsT=rows[:, c0 : c0 + P],
-                        rhs=sel[:, n * P : (n + 1) * P],
+                        lhsT=amat[:, c0 : c0 + P],
+                        rhs=pick[:, n * P : (n + 1) * P],
                         start=True,
                         stop=True,
                     )
@@ -156,10 +145,6 @@ def tile_jointnet_kernel(
                 stop=True,
             )
 
-        def nat_copy(src, g):
-            c0 = src // 2 * 1024 + g * 512
-            nc.scalar.copy(out=nat[:, c0 : c0 + 512], in_=nat_ps[src, g][:])
-
         def split_hi(src, g):
             cols = slice(src * 1024 + g * 512, src * 1024 + (g + 1) * 512)
             nc.scalar.copy(out=piece[0][:, cols], in_=nat_ps[src, g][:])
@@ -180,7 +165,7 @@ def tile_jointnet_kernel(
             )
 
         def move_rows(b):
-            halves = [h for h in (2 * b, 2 * b + 1) if h not in ADDED]
+            halves = [h for h in (2 * b, 2 * b + 1) if h >= ADDED]
             n = len(halves)
             a0 = halves[0] * 1024
             for q in range(3):
@@ -196,17 +181,6 @@ def tile_jointnet_kernel(
                     ),
                     in_=piece[q][b * U : (b + 1) * U, 2048:3072].unsqueeze(1).to_broadcast([U, n, 1024]),
                 )
-
-        def move_plain_rows():
-            for h in PLAIN:
-                nc.sync.dma_start(
-                    out=amat32[0:16, (h - 2) * 1024 : (h - 1) * 1024],
-                    in_=nat[16 * h : 16 * (h + 1), 0:1024],
-                )
-            nc.sync.dma_start(
-                out=amat32[16:32, :].rearrange("p (n x) -> p n x", n=2),
-                in_=nat[U : 2 * U, 1024:2048].unsqueeze(1).to_broadcast([U, 2, 1024]),
-            )
 
         def zrow(i):
             b, n = divmod(i, 4)
@@ -291,20 +265,12 @@ def tile_jointnet_kernel(
                 )
             elif step[0] == "t":
                 k = int(step[1])
-                if b < B - 2:
-                    nc.gpsimd.tensor_tensor(
-                        out=tv[:, 2 * k + 2, :, :],
-                        in0=tv[:, 2 * k, :, :],
-                        in1=tv[:, 2 * k + 1, :, :],
-                        op=ALU.mult,
-                    )
-                else:
-                    nc.vector.tensor_reduce(
-                        out=tv[:, 2 * k + 2, :, :],
-                        in_=tv[:, 2 * k : 2 * k + 2, :, :].rearrange("p k a c -> p a c k"),
-                        axis=AX.X,
-                        op=ALU.mult,
-                    )
+                nc.vector.tensor_reduce(
+                    out=tv[:, 2 * k + 2, :, :],
+                    in_=tv[:, 2 * k : 2 * k + 2, :, :].rearrange("p k a c -> p a c k"),
+                    axis=AX.X,
+                    op=ALU.mult,
+                )
             elif step == "z0":
                 nc.vector.tensor_reduce(
                     out=z0,
@@ -343,11 +309,9 @@ def tile_jointnet_kernel(
             nc.vector.memset(shift[:], -1.0 * STEPS)
             nc.vector.memset(guess[:], GUESS)
             nc.scalar.activation(out=warm2[:], in_=warm[:], func=ACT.Exp)
-            nc.scalar.copy(out=amat32[:], in_=warm[:, 0:1].to_broadcast([P, 2048]))
             braw = staging.tile([P, 256], BF16, name="braw")
             nc.vector.memset(braw[:], 0.0)
             bperm = staging.tile([P, 1024], BF16, name="bperm")
-            bperm32 = staging.tile([P, 1024], F32, name="bperm32")
             xin = staging.tile([P, 1536], BF16, name="xin")
             we = staging.tile([P, 4096], BF16, name="we")
             wd = staging.tile([P, 4096], BF16, name="wd")
@@ -382,30 +346,26 @@ def tile_jointnet_kernel(
                 nc.sync.dma_start(out=wf_dst[:, r0 : r0 + 2, :], in_=wf_src[:, r0 : r0 + 2, :])
             nc.sync.dma_start(out=bfc[:], in_=b_fc.partition_broadcast(P))
 
-            for sel, pieces in ((pick32, 1), (pick, 3)):
-                w = 16 * pieces
-                by_t = staging.tile([P, 16], F32, name="by_t%d" % pieces)
-                by_u = staging.tile([P, 16], F32, name="by_u%d" % pieces)
-                both = staging.tile([P, 1], F32, name="both%d" % pieces)
-                for dst, c0 in ((by_t, 0), (by_u, w)):
-                    nc.vector.tensor_reduce(
-                        out=dst[:],
-                        in_=ident[:, c0 : c0 + w].rearrange("p (q t) -> p t q", q=pieces),
-                        axis=AX.X,
-                        op=ALU.add,
-                    )
+            by_t = staging.tile([P, 16], F32, name="by_t")
+            by_u = staging.tile([P, 16], F32, name="by_u")
+            both = staging.tile([P, 1], F32, name="both")
+            for dst, c0 in ((by_t, 0), (by_u, 48)):
                 nc.vector.tensor_reduce(
-                    out=both[:], in_=ident[:, 2 * w : 2 * w + 2], axis=AX.X, op=ALU.add
-                )
-                nc.vector.tensor_scalar(
-                    out=by_t[:], in0=by_t[:], scalar1=both[:], scalar2=None, op0=ALU.add
-                )
-                nc.vector.tensor_tensor(
-                    out=sel[:].rearrange("p (t u) -> p t u", t=16),
-                    in0=by_t[:].unsqueeze(2).to_broadcast([P, 16, U]),
-                    in1=by_u[:].unsqueeze(1).to_broadcast([P, 16, U]),
+                    out=dst[:],
+                    in_=ident[:, c0 : c0 + 48].rearrange("p (q t) -> p t q", q=3),
+                    axis=AX.X,
                     op=ALU.add,
                 )
+            nc.vector.tensor_reduce(out=both[:], in_=ident[:, 96:98], axis=AX.X, op=ALU.add)
+            nc.vector.tensor_scalar(
+                out=by_t[:], in0=by_t[:], scalar1=both[:], scalar2=None, op0=ALU.add
+            )
+            nc.vector.tensor_tensor(
+                out=pick[:].rearrange("p (t u) -> p t u", t=16),
+                in0=by_t[:].unsqueeze(2).to_broadcast([P, 16, U]),
+                in1=by_u[:].unsqueeze(1).to_broadcast([P, 16, U]),
+                op=ALU.add,
+            )
 
             def turn(srcs, dst32, eng):
                 n = len(srcs) // 2
@@ -462,16 +422,13 @@ def tile_jointnet_kernel(
                 (dec_ps if r == 2 else enc_ps)[g] = view
 
             def enc_out(g):
-                for w0, w1 in ((0, 32), (96, 112)):
-                    nc.vector.tensor_tensor(
-                        out=enc_v[:, g, w0:w1, :],
-                        in0=enc_ps[g][:, w0:w1, :],
-                        in1=bsum[:, g * 4 : (g + 1) * 4].unsqueeze(1).to_broadcast([P, w1 - w0, 4]),
-                        op=ALU.add,
-                    )
-
-            def dec_copy(g):
-                nc.vector.tensor_copy(out=dec_v[:, g, :, :], in_=dec_ps[g][:, 3 * U : 4 * U, :])
+                w = ADDED * 16
+                nc.vector.tensor_tensor(
+                    out=enc_v[:, g, :, :],
+                    in0=enc_ps[g][:, 0:w, :],
+                    in1=bsum[:, g * 4 : (g + 1) * 4].unsqueeze(1).to_broadcast([P, w, 4]),
+                    op=ALU.add,
+                )
 
             wf32 = wf[:].bitcast(F32).rearrange("p (r g x) -> p r g x", r=8, g=2)
 
@@ -487,22 +444,17 @@ def tile_jointnet_kernel(
                     in_=wfg[g][:, half * 2048 : (half + 1) * 2048],
                 )
 
-            for dst in (bperm, bperm32):
-                nc.gpsimd.tensor_scalar(
-                    out=dst[96:128, :].rearrange("p (c e w) -> p c e w", c=4, e=2),
-                    in0=brow[96:128, :].rearrange("p (c w e) -> p c e w", c=4, e=2),
-                    scalar1=1.0,
-                    scalar2=0.0,
-                    op0=ALU.mult,
-                    op1=ALU.add,
-                )
-            nc.sync.dma_start(
-                out=amat32[32:34, :].rearrange("p (h x) -> p h x", h=2),
-                in_=bperm32[96:98, :].unsqueeze(1).to_broadcast([2, 2, 1024]),
+            nc.gpsimd.tensor_scalar(
+                out=bperm[96:128, :].rearrange("p (c e w) -> p c e w", c=4, e=2),
+                in0=brow[96:128, :].rearrange("p (c w e) -> p c e w", c=4, e=2),
+                scalar1=1.0,
+                scalar2=0.0,
+                op0=ALU.mult,
+                op1=ALU.add,
             )
             nc.sync.dma_start(
-                out=amat[96:128, 4096:].rearrange("p (h x) -> p h x", x=1024),
-                in_=bperm[96:128, :].unsqueeze(1).to_broadcast([32, 12, 1024]),
+                out=amat[96:128, ADDED * 1024 :].rearrange("p (h x) -> p h x", x=1024),
+                in_=bperm[96:128, :].unsqueeze(1).to_broadcast([32, 16 - ADDED, 1024]),
             )
             weights(we, weg, wec, wes, 0)
             weights(wd, wdg, wdc, wds, 0)
@@ -516,45 +468,51 @@ def tile_jointnet_kernel(
             fc_weights(0, 1, "S")
             fc_weights(2, 0, "V")
             nc.vector.tensor_tensor(out=bsum[:], in0=bT16[:, 0:8], in1=bT16[:, 8:16], op=ALU.add)
-            project(0, 2)
-            project(0, 0)
             natural(0, 0)
             natural(2, 0)
+            project(0, 2)
+            project(0, 0)
+            split_hi(0, 0)
+            split_hi(2, 0)
             fc_weights(2, 1, "S")
             enc_out(0)
-            dec_copy(0)
-            add(0, 0, "V")
-            nat_copy(0, 0)
-            nat_copy(2, 0)
-            project(1, 2)
-            project(1, 0)
+            split_rest(0, 0)
+            split_b(0, 0)
+            split_rest(2, 0)
+            split_b(2, 0)
+            add(0, 0)
             natural(0, 1)
             natural(2, 1)
-            enc_out(1)
-            dec_copy(1)
-            add(0, 1, "V")
-            nat_copy(0, 1)
-            nat_copy(2, 1)
-            move_plain_rows()
+            project(1, 2)
+            project(1, 0)
             fc_weights(4, 0, "S")
-            add(1, 0, "V")
-            fc_weights(4, 1, "S")
-            tanh_old(0, 0)
-            fc_weights(6, 0, "S")
-            tanh_old(0, 1)
+            split_hi(0, 1)
+            split_hi(2, 1)
             fc_quant(0, 0)
             fc_quant(1, 0)
-            add(1, 1, "V")
+            enc_out(1)
+            split_rest(0, 1)
+            split_b(0, 1)
+            split_rest(2, 1)
+            split_b(2, 1)
+            add(0, 1)
+            fc_weights(4, 1, "S")
+            for b in (1, 2, 3):
+                move_rows(b)
+            tanh_old(0, 0)
+            fc_weights(6, 0, "S")
+            add(1, 0)
+            tanh_old(0, 1)
             fc_weights(6, 1, "S")
-            tanh_old(1, 0)
+            add(1, 1)
             quant(0)
             fc_quant(0, 1)
             fc_quant(1, 1)
-            comb_mm(4)
-            natural(0, 0)
-            natural(2, 0)
-            matmul(0)
+            tanh_old(1, 0)
             tanh_old(1, 1)
+            matmul(0)
+            add(2, 0)
+            add(2, 1)
 
         zpool = ctx.enter_context(tc.tile_pool(name="zpool", bufs=5))
 
@@ -587,22 +545,21 @@ def tile_jointnet_kernel(
 
         def hidden(i, g):
             h, n = divmod(i, 2)
-            if h not in ADDED:
+            if h >= ADDED:
                 tanh(i, g)
             elif n == 0:
                 tanh_old(h, g)
 
         def cmm(i):
-            if tile_ok(i) and i // 2 not in ADDED:
+            if tile_ok(i) and i // 2 >= ADDED:
                 comb_mm(i)
 
         gate = const.tile([P, 8], F32, name="gate")
 
-        def late_add(i, g, t0):
+        def hold(i):
             nc.gpsimd.tensor_scalar(
                 out=gate[:, 0:1], in0=zrow(i)[:, 0:1], scalar1=1.0, scalar2=0.0, op0=ALU.mult, op1=ALU.add
             )
-            add(6, g, "G", t0, t0 + 8)
 
         def new_entry(u):
             zbt[u] = zpool.tile([P, 4 * V], F32, name="zb", tag="zb")
@@ -613,75 +570,55 @@ def tile_jointnet_kernel(
         for u in range(0, B - 1):
             new_entry(u)
             i = 4 * u
-            on(u - 2, "nc")
             quant(i // 2 + 1)
-            badd(i, 0)
-            if u == 0:
-                for src in (0, 2):
-                    split_hi(src, 0)
-                    split_rest(src, 0)
-                    split_b(src, 0)
-                natural(0, 1)
-                natural(2, 1)
             rmax(i - 1)
-            hidden(i + 4, 0)
-            hidden(i + 4, 1)
+            badd(i, 0)
             badd(i, 1)
+            if u > 2:
+                hold(i)
+                fin(u - 3, 3)
+            hidden(i + 4, 0)
+            on(u - 2, "g2")
+            on(u - 2, "t2")
+            hidden(i + 4, 1)
             esum(i - 1)
-            fin(u - 2, 0)
-            fin(u - 2, 1)
-            if u == 1:
-                late_add(i, 0, 0)
-                add(6, 0, "G", 8, 16)
             mm(i + 1)
             cmm(i + 5)
 
             i = 4 * u + 1
             badd(i, 0)
-            if u == 0:
-                for src in (0, 2):
-                    split_hi(src, 1)
-                    split_rest(src, 1)
-                    split_b(src, 1)
-                for b in (2, 3):
-                    move_rows(b)
             rmax(i - 1)
+            badd(i, 1)
+            hidden(i + 4, 0)
+            on(u - 2, "g3")
+            on(u - 2, "t3")
+            hidden(i + 4, 1)
             on(u - 1, "ab")
             on(u - 1, "zc")
-            hidden(i + 4, 0)
-            on(u - 1, "ev")
-            on(u - 1, "mc")
-            hidden(i + 4, 1)
-            on(u - 1, "q")
-            on(u - 1, "mx")
-            badd(i, 1)
             esum(i - 1)
-            on(u - 1, "x0")
-            fin(u - 2, 2)
-            fin(u - 2, 3)
-            if u == 1:
-                late_add(i, 1, 0)
-                add(6, 1, "G", 8, 16)
+            for step in ("ev", "mc", "q", "mx", "x0"):
+                on(u - 1, step)
+            if u == 0:
                 natural(1, 0)
                 split_hi(1, 0)
             mm(i + 1)
             cmm(i + 5)
 
             i = 4 * u + 2
+            on(u - 2, "nc")
             quant(i // 2 + 1)
-            badd(i, 0)
+            on(u - 2, "z0")
             rmax(i - 1)
+            badd(i, 0)
+            badd(i, 1)
+            hidden(i + 4, 0)
             on(u - 1, "g0")
             on(u - 1, "t0")
-            hidden(i + 4, 0)
-            on(u - 1, "g1")
-            on(u - 1, "t1")
             hidden(i + 4, 1)
-            on(u - 1, "g2")
-            on(u - 1, "t2")
-            badd(i, 1)
             esum(i - 1)
-            if u == 1:
+            fin(u - 2, 0)
+            fin(u - 2, 1)
+            if u == 0:
                 split_rest(1, 0)
                 split_b(1, 0)
                 natural(1, 1)
@@ -692,14 +629,14 @@ def tile_jointnet_kernel(
             i = 4 * u + 3
             badd(i, 0)
             rmax(i - 1)
-            on(u - 1, "g3")
-            on(u - 1, "t3")
-            hidden(i + 4, 0)
-            hidden(i + 4, 1)
             badd(i, 1)
-            on(u - 1, "z0")
+            hidden(i + 4, 0)
+            on(u - 1, "g1")
+            on(u - 1, "t1")
+            hidden(i + 4, 1)
             esum(i - 1)
-            if u == 1:
+            fin(u - 2, 2)
+            if u == 0:
                 split_rest(1, 1)
                 split_b(1, 1)
                 for b in range(4, 8):
@@ -716,43 +653,50 @@ def tile_jointnet_kernel(
             for name in names:
                 chain(grp, name)
 
-        chain(ga, "nc")
-        rmax(i - 1)
         quant(i // 2 + 1)
+        chain(ga, "g2")
+        rmax(i - 1)
+        chain(ga, "t2")
         badd(i, 0)
         steps(gb, ("ab", "zc", "ev", "mx", "q"))
+        hold(i)
+        fin(u - 3, 3)
+        chain(ga, "g3")
         badd(i, 1)
+        chain(ga, "t3")
         esum(i - 1)
         steps(gb, ("mc", "x0", "g0"))
-        finish(4 * (u - 2) + 0, ga, "G")
-        finish(4 * (u - 2) + 1, ga, "G")
         mm(i + 1)
 
         badd(i + 1, 0)
+        chain(ga, "nc")
+        chain(ga, "z0")
+        finish(4 * (u - 2) + 0, ga, "G")
         chain(gb, "t0")
-        finish(4 * (u - 2) + 2, ga, "G")
         chain(gb, "g1")
-        badd(i + 1, 1)
+        rmax(i)
+        finish(4 * (u - 2) + 3, ga, "S")
         chain(gb, "t1")
         chain(gb, "g2")
-        finish(4 * (u - 2) + 3, ga, "S")
-        rmax(i)
+        badd(i + 1, 1)
+        finish(4 * (u - 2) + 1, ga, "G")
         chain(gb, "t2")
-        chain(gb, "g3")
         esum(i)
+        chain(gb, "g3")
         mm(i + 2)
 
         badd(i + 2, 0)
-        chain(gb, "t3")
+        finish(4 * (u - 2) + 2, ga, "G")
         rmax(i + 1)
+        chain(gb, "t3")
+        badd(i + 2, 1)
         chain(gb, "nc")
         chain(gb, "z0")
-        badd(i + 2, 1)
         steps(gc, ("ab", "zc", "ev", "mx", "q"))
         esum(i + 1)
         steps(gc, ("mc", "x0", "g0"))
         finish(4 * (u - 1) + 0, gb, "G")
-        finish(4 * (u - 1) + 1, gb, "G")
+        finish(4 * (u - 1) + 1, gb, "S")
         mm(i + 3)
 
         badd(i + 3, 0)
@@ -764,6 +708,7 @@ def tile_jointnet_kernel(
         chain(gc, "t1")
         chain(gc, "g2")
         esum(i + 2)
+        finish(4 * (u - 1) + 3, gb, "V")
         rmax(i + 3)
         chain(gc, "t2")
         steps(gd, ("ab", "zc", "ev", "mx", "q"))
@@ -771,7 +716,6 @@ def tile_jointnet_kernel(
         esum(i + 3)
         steps(gd, ("x0", "g0", "mc"))
         chain(gc, "t3")
-        finish(4 * (u - 1) + 3, gb, "V")
         chain(gc, "nc")
         chain(gc, "z0")
         chain(gd, "t0")
@@ -779,7 +723,7 @@ def tile_jointnet_kernel(
         finish(i, gc, "V")
         chain(gd, "t1")
         chain(gd, "g2")
-        finish(i + 1, gc, "S")
+        finish(i + 1, gc, "V")
         chain(gd, "t2")
         chain(gd, "g3")
         steps(gd, ("t3", "nc", "z0"))

@@ -45,6 +45,7 @@ def tile_jointnet_kernel(
         wfc = const.tile([P, 2048], U32, name="wfc", align_bytes=64)
         wfs = const.tile([P, 2048], U8, name="wfs", align_bytes=64)
         encT = const.tile([P, ADDED * 128], F32, name="encT")
+        decT = const.tile([P, 128], F32, name="decT")
         bfc = const.tile([P, V], BF16, name="bfc")
         ident = const.tile([P, P], F32, name="ident")
         bT = const.tile([P, 8], F32, name="bT")
@@ -59,20 +60,31 @@ def tile_jointnet_kernel(
         piece = [const.tile([P, 3072], BF16, name="piece%d" % q) for q in range(3)]
         rest = const.tile([P, 3072], F32, name="rest")
         enc_v = encT[:].rearrange("p (g w j) -> p g w j", g=2, j=4)
+        dec_v = decT[:].rearrange("p (g w j) -> p g w j", g=2, j=4)
 
         comb, hid, hc, hs, dec_ps = {}, {}, {}, {}, {}
         cbank, ybank, zbt, negm, xx, st = {}, {}, {}, {}, {}, {}
         nat_ps = {}
 
-        def add(h, g):
-            comb[h, g] = work.tile([P, 1024], F32, name="comb", tag="comb", bufs=2 * ADDED)
-            b = h // 2
-            nc.vector.tensor_tensor(
-                out=comb[h, g][:].rearrange("p (t u j) -> p t u j", t=16, u=U),
-                in0=enc_v[:, g, h * 16 : (h + 1) * 16, :].unsqueeze(2).to_broadcast([P, 16, U, 4]),
-                in1=dec_ps[g][:, b * U : (b + 1) * U, :].unsqueeze(1).to_broadcast([P, 16, U, 4]),
+        def add(h, g, eng="V", t0=0, t1=16):
+            if (h, g) not in comb:
+                comb[h, g] = work.tile([P, 1024], F32, name="comb", tag="comb", bufs=2 * ADDED)
+            b, nt = h // 2, t1 - t0
+            dec = dec_ps[g][:, b * U : (b + 1) * U, :] if eng == "V" else dec_v[:, g, :, :]
+            (nc.vector if eng == "V" else nc.gpsimd).tensor_tensor(
+                out=comb[h, g][:, t0 * 64 : t1 * 64].rearrange("p (t u j) -> p t u j", t=nt, u=U),
+                in0=enc_v[:, g, h * 16 + t0 : h * 16 + t1, :]
+                .unsqueeze(2)
+                .to_broadcast([P, nt, U, 4]),
+                in1=dec.unsqueeze(1).to_broadcast([P, nt, U, 4]),
                 op=ALU.add,
             )
+
+        def add_late(h, g):
+            b = h // 2
+            nc.scalar.copy(out=dec_v[:, g, :, :], in_=dec_ps[g][:, b * U : (b + 1) * U, :])
+            for t0 in (0, 8):
+                add(h, g, "G", t0, t0 + 8)
 
         def hid_tile(h):
             if h not in hid:
@@ -287,8 +299,8 @@ def tile_jointnet_kernel(
                     negate=True,
                 )
 
-        def finish(i, grp, eng):
-            z = zrow(i)
+        def finish(i, grp, eng, v0=0, v1=V):
+            z = zrow(i)[:, v0:v1]
             c = st[grp, "negc"][:, i % 4 - grp[1] : i % 4 - grp[1] + 1]
             if eng == "G":
                 nc.gpsimd.tensor_scalar(
@@ -298,7 +310,7 @@ def tile_jointnet_kernel(
                 nc.scalar.activation(out=z, in_=z, func=ACT.Identity, bias=c, scale=1.0)
             else:
                 nc.vector.tensor_scalar(out=z, in0=z, scalar1=c, scalar2=None, op0=ALU.add)
-            nc.sync.dma_start(out=out_rows[i * P : (i + 1) * P, :], in_=z)
+            nc.sync.dma_start(out=out_rows[i * P : (i + 1) * P, v0:v1], in_=z)
 
         with tc.tile_pool(name="staging", bufs=1) as staging:
             nc.vector.memset(warm[:], 0.0)
@@ -323,26 +335,27 @@ def tile_jointnet_kernel(
                 staging.tile([P, 4096], BF16, name="wfg%d" % g, align_bytes=64) for g in range(2)
             ]
 
+            we_src = W_enc.rearrange("(c p e) k -> p c (e k)", c=4, p=P, e=2)
+            wd_src = W_dec.rearrange("(c p e) k -> p c (e k)", c=4, p=P, e=2)
+            we_dst = we[:].rearrange("p (c x) -> p c x", c=4)
+            wd_dst = wd[:].rearrange("p (c x) -> p c x", c=4)
+            wf_src = W_fc.rearrange("(r p) f -> p r f", p=P)
+            wf_dst = wf[:].rearrange("p (r f) -> p r f", r=8)
             nc.sync.dma_start(
                 out=xin[:, 0:1024].rearrange("p (r k) -> p r k", r=2),
                 in_=encoder_output.flatten_outer_dims().rearrange("(r p) k -> p r k", p=P),
             )
             nc.sync.dma_start(out=xin[:, 1024:1536], in_=decoder_output.flatten_outer_dims())
-            we_src = W_enc.rearrange("(c p e) k -> p c (e k)", c=4, p=P, e=2)
-            wd_src = W_dec.rearrange("(c p e) k -> p c (e k)", c=4, p=P, e=2)
-            we_dst = we[:].rearrange("p (c x) -> p c x", c=4)
-            wd_dst = wd[:].rearrange("p (c x) -> p c x", c=4)
             nc.sync.dma_start(out=we_dst[:, 0:2, :], in_=we_src[:, 0:2, :])
             nc.sync.dma_start(out=wd_dst[:, 0:2, :], in_=wd_src[:, 0:2, :])
             nc.sync.dma_start(out=braw[0:4, :], in_=b_enc.rearrange("(c x) -> c x", c=4))
             nc.sync.dma_start(out=braw[4:8, :], in_=b_dec.rearrange("(c x) -> c x", c=4))
             nc.sync.dma_start(out=we_dst[:, 2:4, :], in_=we_src[:, 2:4, :])
             nc.sync.dma_start(out=wd_dst[:, 2:4, :], in_=wd_src[:, 2:4, :])
+            nc.sync.dma_start(out=wf_dst[:, 0:2, :], in_=wf_src[:, 0:2, :])
             nc.sync.dma_start(out=brow[96:97, :], in_=b_enc.unsqueeze(0))
             nc.sync.dma_start(out=brow[97:98, :], in_=b_dec.unsqueeze(0))
-            wf_src = W_fc.rearrange("(r p) f -> p r f", p=P)
-            wf_dst = wf[:].rearrange("p (r f) -> p r f", r=8)
-            for r0 in range(0, 8, 2):
+            for r0 in range(2, 8, 2):
                 nc.sync.dma_start(out=wf_dst[:, r0 : r0 + 2, :], in_=wf_src[:, r0 : r0 + 2, :])
             nc.sync.dma_start(out=bfc[:], in_=b_fc.partition_broadcast(P))
 
@@ -392,10 +405,10 @@ def tile_jointnet_kernel(
                 out=xc[:, 256:384].bitcast(FP8X4), scales=xs[:, 256:384], in_=xg[:, 1024:1536]
             )
 
-            def weights(raw, grp, cod, sca, g):
+            def weights(raw, grp, cod, sca, g, eng):
                 r32, g32 = raw[:].bitcast(F32), grp[:].bitcast(F32)
                 turn(blocks(r32, g * 8, 4), g32[:, g * 1024 : g * 1024 + 512], "S")
-                turn(blocks(r32, g * 8 + 4, 4), g32[:, g * 1024 + 512 : g * 1024 + 1024], "S")
+                turn(blocks(r32, g * 8 + 4, 4), g32[:, g * 1024 + 512 : g * 1024 + 1024], eng)
                 nc.vector.quantize_mx(
                     out=cod[:, g * 512 : (g + 1) * 512].bitcast(FP8X4),
                     scales=sca[:, g * 512 : (g + 1) * 512],
@@ -444,59 +457,56 @@ def tile_jointnet_kernel(
                     in_=wfg[g][:, half * 2048 : (half + 1) * 2048],
                 )
 
-            nc.gpsimd.tensor_scalar(
-                out=bperm[96:128, :].rearrange("p (c e w) -> p c e w", c=4, e=2),
-                in0=brow[96:128, :].rearrange("p (c w e) -> p c e w", c=4, e=2),
-                scalar1=1.0,
-                scalar2=0.0,
-                op0=ALU.mult,
-                op1=ALU.add,
-            )
-            nc.sync.dma_start(
-                out=amat[96:128, ADDED * 1024 :].rearrange("p (h x) -> p h x", x=1024),
-                in_=bperm[96:128, :].unsqueeze(1).to_broadcast([32, 16 - ADDED, 1024]),
-            )
-            weights(we, weg, wec, wes, 0)
-            weights(wd, wdg, wdc, wds, 0)
-            weights(we, weg, wec, wes, 1)
-            weights(wd, wdg, wdc, wds, 1)
+            weights(we, weg, wec, wes, 0, "S")
+            weights(wd, wdg, wdc, wds, 0, "S")
+            weights(we, weg, wec, wes, 1, "S")
+            weights(wd, wdg, wdc, wds, 1, "S")
             ptb = psum.tile([P, 512], F32, name="ptb", tag="bank")
             nc.tensor.transpose(out=ptb[:, 0:P], in_=braw[:].bitcast(F32), identity=ident[:])
             nc.vector.tensor_copy(out=bT[:], in_=ptb[:, 0:8])
             bT16 = bT[:].bitcast(BF16)
             fc_weights(0, 0, "S")
-            fc_weights(0, 1, "S")
-            fc_weights(2, 0, "V")
-            nc.vector.tensor_tensor(out=bsum[:], in0=bT16[:, 0:8], in1=bT16[:, 8:16], op=ALU.add)
-            natural(0, 0)
-            natural(2, 0)
             project(0, 2)
             project(0, 0)
+            nc.vector.tensor_tensor(out=bsum[:], in0=bT16[:, 0:8], in1=bT16[:, 8:16], op=ALU.add)
+            fc_weights(2, 0, "S")
+            natural(0, 0)
+            natural(2, 0)
+            fc_weights(0, 1, "S")
+            nc.vector.tensor_copy(
+                out=bperm[96:128, :].rearrange("p (c e w) -> p c e w", c=4, e=2),
+                in_=brow[96:128, :].rearrange("p (c w e) -> p c e w", c=4, e=2),
+            )
+            nc.sync.dma_start(
+                out=amat[96:128, ADDED * 1024 :].rearrange("p (h x) -> p h x", x=1024),
+                in_=bperm[96:128, :].unsqueeze(1).to_broadcast([32, 16 - ADDED, 1024]),
+            )
+            enc_out(0)
+            add_late(2, 0)
+            add(0, 0)
             split_hi(0, 0)
             split_hi(2, 0)
+            fc_quant(0, 0)
+            project(1, 2)
+            project(1, 0)
             fc_weights(2, 1, "S")
-            enc_out(0)
             split_rest(0, 0)
             split_b(0, 0)
             split_rest(2, 0)
             split_b(2, 0)
-            add(0, 0)
             natural(0, 1)
-            natural(2, 1)
-            project(1, 2)
-            project(1, 0)
             fc_weights(4, 0, "S")
+            natural(2, 1)
+            enc_out(1)
+            add(0, 1)
             split_hi(0, 1)
             split_hi(2, 1)
-            fc_quant(0, 0)
             fc_quant(1, 0)
-            enc_out(1)
+            fc_weights(4, 1, "S")
             split_rest(0, 1)
             split_b(0, 1)
             split_rest(2, 1)
             split_b(2, 1)
-            add(0, 1)
-            fc_weights(4, 1, "S")
             for b in (1, 2, 3):
                 move_rows(b)
             tanh_old(0, 0)
@@ -511,7 +521,6 @@ def tile_jointnet_kernel(
             tanh_old(1, 0)
             tanh_old(1, 1)
             matmul(0)
-            add(2, 0)
             add(2, 1)
 
         zpool = ctx.enter_context(tc.tile_pool(name="zpool", bufs=5))
@@ -588,10 +597,10 @@ def tile_jointnet_kernel(
             i = 4 * u + 1
             badd(i, 0)
             rmax(i - 1)
-            badd(i, 1)
             hidden(i + 4, 0)
             on(u - 2, "g3")
             on(u - 2, "t3")
+            badd(i, 1)
             hidden(i + 4, 1)
             on(u - 1, "ab")
             on(u - 1, "zc")
@@ -610,10 +619,10 @@ def tile_jointnet_kernel(
             on(u - 2, "z0")
             rmax(i - 1)
             badd(i, 0)
-            badd(i, 1)
             hidden(i + 4, 0)
             on(u - 1, "g0")
             on(u - 1, "t0")
+            badd(i, 1)
             hidden(i + 4, 1)
             esum(i - 1)
             fin(u - 2, 0)
@@ -629,10 +638,10 @@ def tile_jointnet_kernel(
             i = 4 * u + 3
             badd(i, 0)
             rmax(i - 1)
-            badd(i, 1)
             hidden(i + 4, 0)
             on(u - 1, "g1")
             on(u - 1, "t1")
+            badd(i, 1)
             hidden(i + 4, 1)
             esum(i - 1)
             fin(u - 2, 2)
@@ -663,9 +672,9 @@ def tile_jointnet_kernel(
         fin(u - 3, 3)
         chain(ga, "g3")
         badd(i, 1)
-        chain(ga, "t3")
         esum(i - 1)
-        steps(gb, ("mc", "x0", "g0"))
+        chain(ga, "t3")
+        steps(gb, ("x0", "g0", "mc"))
         mm(i + 1)
 
         badd(i + 1, 0)
@@ -674,8 +683,8 @@ def tile_jointnet_kernel(
         finish(4 * (u - 2) + 0, ga, "G")
         chain(gb, "t0")
         chain(gb, "g1")
-        rmax(i)
         finish(4 * (u - 2) + 3, ga, "S")
+        rmax(i)
         chain(gb, "t1")
         chain(gb, "g2")
         badd(i + 1, 1)
@@ -694,38 +703,38 @@ def tile_jointnet_kernel(
         chain(gb, "z0")
         steps(gc, ("ab", "zc", "ev", "mx", "q"))
         esum(i + 1)
-        steps(gc, ("mc", "x0", "g0"))
+        steps(gc, ("x0", "g0", "mc"))
         finish(4 * (u - 1) + 0, gb, "G")
-        finish(4 * (u - 1) + 1, gb, "S")
+        finish(4 * (u - 1) + 1, gb, "G")
         mm(i + 3)
 
         badd(i + 3, 0)
         rmax(i + 2)
         chain(gc, "t0")
-        chain(gc, "g1")
         finish(4 * (u - 1) + 2, gb, "G")
         badd(i + 3, 1)
+        esum(i + 2)
+        chain(gc, "g1")
+        steps(gd, ("ab", "zc", "ev", "mx", "q"))
+        finish(4 * (u - 1) + 3, gb, "G")
+        rmax(i + 3)
         chain(gc, "t1")
         chain(gc, "g2")
-        esum(i + 2)
-        finish(4 * (u - 1) + 3, gb, "V")
-        rmax(i + 3)
-        chain(gc, "t2")
-        steps(gd, ("ab", "zc", "ev", "mx", "q"))
-        chain(gc, "g3")
         esum(i + 3)
+        chain(gc, "t2")
+        chain(gc, "g3")
         steps(gd, ("x0", "g0", "mc"))
         chain(gc, "t3")
-        chain(gc, "nc")
-        chain(gc, "z0")
         chain(gd, "t0")
         chain(gd, "g1")
+        chain(gc, "nc")
+        chain(gc, "z0")
         finish(i, gc, "V")
         chain(gd, "t1")
         chain(gd, "g2")
         finish(i + 1, gc, "V")
-        chain(gd, "t2")
-        chain(gd, "g3")
-        steps(gd, ("t3", "nc", "z0"))
+        for step in ("t2", "g3", "t3", "nc", "z0"):
+            chain(gd, step)
         finish(i + 2, gd, "V")
-        finish(i + 3, gd, "S")
+        finish(i + 3, gd, "S", 0, 512)
+        finish(i + 3, gd, "V", 512, V)

@@ -235,6 +235,7 @@ def tile_jointnet_kernel(
             c = n1 - n0
             z0 = zbt[b][:].rearrange("p (n v) -> p n v", n=4)[:, n0:n1, 0]
             xt = xx[b, n0 // 2] if b == B - 1 else xx[b, 0]
+            first = FIRST if grp == (B - 1, 2, 4) else 2
             tv = xt[:].rearrange("p (k a c) -> p k a c", a=2, c=4)[:, :, :, n0:n1]
             if step == "ab":
                 nc.scalar.activation(out=small(grp, "ab")[:, 0:c], in_=z0, func=ACT.Abs)
@@ -266,6 +267,8 @@ def tile_jointnet_kernel(
                     bias=guess[:],
                     scale=K1,
                 )
+            elif step == "ln":
+                nc.scalar.activation(out=tv[:, FIRST, :, :], in_=tv[:, 0, :, :], func=ACT.Ln)
             elif step[0] == "g":
                 k = int(step[1])
                 nc.scalar.activation(
@@ -286,14 +289,14 @@ def tile_jointnet_kernel(
             elif step == "z0":
                 nc.vector.tensor_reduce(
                     out=z0,
-                    in_=tv[:, 2 : BLANK + 1 : 2, 0, :].rearrange("p k c -> p c k"),
+                    in_=tv[:, first : BLANK + 1 : 2, 0, :].rearrange("p k c -> p c k"),
                     axis=AX.X,
                     op=ALU.add,
                 )
             else:
                 nc.vector.tensor_reduce(
                     out=small(grp, "negc")[:, 0:c],
-                    in_=tv[:, 2 : EXTRA + 1 : 2, :, :].rearrange("p k a c -> p c k a"),
+                    in_=tv[:, first : EXTRA + 1 : 2, :, :].rearrange("p k a c -> p c k a"),
                     axis=AX.XY,
                     op=ALU.add,
                     negate=True,
@@ -515,13 +518,13 @@ def tile_jointnet_kernel(
             tanh_old(0, 1)
             fc_weights(6, 1, "S")
             add(1, 1)
+            add(2, 1)
             quant(0)
             fc_quant(0, 1)
             fc_quant(1, 1)
             tanh_old(1, 0)
             tanh_old(1, 1)
             matmul(0)
-            add(2, 1)
 
         zpool = ctx.enter_context(tc.tile_pool(name="zpool", bufs=5))
 
@@ -712,29 +715,25 @@ def tile_jointnet_kernel(
         rmax(i + 2)
         chain(gc, "t0")
         finish(4 * (u - 1) + 2, gb, "G")
-        badd(i + 3, 1)
-        esum(i + 2)
-        chain(gc, "g1")
         steps(gd, ("ab", "zc", "ev", "mx", "q"))
+        chain(gc, "g1")
+        badd(i + 3, 1)
+        chain(gc, "t1")
+        esum(i + 2)
+        chain(gc, "g2")
         finish(4 * (u - 1) + 3, gb, "G")
         rmax(i + 3)
-        chain(gc, "t1")
-        chain(gc, "g2")
-        esum(i + 3)
         chain(gc, "t2")
         chain(gc, "g3")
-        steps(gd, ("x0", "g0", "mc"))
+        esum(i + 3)
+        steps(gd, ("mc", "ln"))
         chain(gc, "t3")
-        chain(gd, "t0")
-        chain(gd, "g1")
         chain(gc, "nc")
         chain(gc, "z0")
         finish(i, gc, "V")
-        chain(gd, "t1")
-        chain(gd, "g2")
         finish(i + 1, gc, "V")
-        for step in ("t2", "g3", "t3", "nc", "z0"):
-            chain(gd, step)
+        chain(gd, "nc")
+        chain(gd, "z0")
         finish(i + 2, gd, "V")
         finish(i + 3, gd, "S", 0, 512)
         finish(i + 3, gd, "V", 512, V)

@@ -167,11 +167,19 @@ def tile_jointnet_kernel(
                 out=rest[:, cols], in0=nat_ps[src, g][:], in1=piece[0][:, cols], op=ALU.subtract
             )
 
-        def split_b(src, g):
+        def split_b(src, g, mid="G"):
             cols = slice(src * 1024 + g * 512, src * 1024 + (g + 1) * 512)
-            nc.gpsimd.tensor_scalar(
-                out=piece[1][:, cols], in0=rest[:, cols], scalar1=1.0, scalar2=0.0, op0=ALU.mult, op1=ALU.add
-            )
+            if mid == "S":
+                nc.scalar.copy(out=piece[1][:, cols], in_=rest[:, cols])
+            else:
+                nc.gpsimd.tensor_scalar(
+                    out=piece[1][:, cols],
+                    in0=rest[:, cols],
+                    scalar1=1.0,
+                    scalar2=0.0,
+                    op0=ALU.mult,
+                    op1=ALU.add,
+                )
             nc.gpsimd.tensor_tensor(
                 out=piece[2][:, cols], in0=rest[:, cols], in1=piece[1][:, cols], op=ALU.subtract
             )
@@ -280,12 +288,20 @@ def tile_jointnet_kernel(
                 )
             elif step[0] == "t":
                 k = int(step[1])
-                nc.vector.tensor_reduce(
-                    out=tv[:, 2 * k + 2, :, :],
-                    in_=tv[:, 2 * k : 2 * k + 2, :, :].rearrange("p k a c -> p a c k"),
-                    axis=AX.X,
-                    op=ALU.mult,
-                )
+                if b < 5:
+                    nc.gpsimd.tensor_tensor(
+                        out=tv[:, 2 * k + 2, :, :],
+                        in0=tv[:, 2 * k, :, :],
+                        in1=tv[:, 2 * k + 1, :, :],
+                        op=ALU.mult,
+                    )
+                else:
+                    nc.vector.tensor_reduce(
+                        out=tv[:, 2 * k + 2, :, :],
+                        in_=tv[:, 2 * k : 2 * k + 2, :, :].rearrange("p k a c -> p a c k"),
+                        axis=AX.X,
+                        op=ALU.mult,
+                    )
             elif step == "z0":
                 nc.vector.tensor_reduce(
                     out=z0,
@@ -494,9 +510,9 @@ def tile_jointnet_kernel(
             project(1, 0)
             fc_weights(2, 1, "S")
             split_rest(0, 0)
-            split_b(0, 0)
+            split_b(0, 0, "S")
             split_rest(2, 0)
-            split_b(2, 0)
+            split_b(2, 0, "S")
             natural(0, 1)
             fc_weights(4, 0, "S")
             natural(2, 1)
@@ -586,13 +602,13 @@ def tile_jointnet_kernel(
             rmax(i - 1)
             badd(i, 0)
             badd(i, 1)
+            hidden(i + 4, 0)
+            hidden(i + 4, 1)
+            on(u - 2, "g2")
             if u > 2:
                 hold(i)
                 fin(u - 3, 3)
-            hidden(i + 4, 0)
-            on(u - 2, "g2")
             on(u - 2, "t2")
-            hidden(i + 4, 1)
             esum(i - 1)
             mm(i + 1)
             cmm(i + 5)
@@ -601,10 +617,10 @@ def tile_jointnet_kernel(
             badd(i, 0)
             rmax(i - 1)
             hidden(i + 4, 0)
-            on(u - 2, "g3")
-            on(u - 2, "t3")
             badd(i, 1)
             hidden(i + 4, 1)
+            on(u - 2, "g3")
+            on(u - 2, "t3")
             on(u - 1, "ab")
             on(u - 1, "zc")
             esum(i - 1)
@@ -617,19 +633,19 @@ def tile_jointnet_kernel(
             cmm(i + 5)
 
             i = 4 * u + 2
-            on(u - 2, "nc")
             quant(i // 2 + 1)
+            on(u - 2, "nc")
             on(u - 2, "z0")
             rmax(i - 1)
             badd(i, 0)
             hidden(i + 4, 0)
             on(u - 1, "g0")
-            on(u - 1, "t0")
             badd(i, 1)
             hidden(i + 4, 1)
             esum(i - 1)
             fin(u - 2, 0)
             fin(u - 2, 1)
+            on(u - 1, "t0")
             if u == 0:
                 split_rest(1, 0)
                 split_b(1, 0)
@@ -642,12 +658,12 @@ def tile_jointnet_kernel(
             badd(i, 0)
             rmax(i - 1)
             hidden(i + 4, 0)
-            on(u - 1, "g1")
-            on(u - 1, "t1")
             badd(i, 1)
             hidden(i + 4, 1)
+            on(u - 1, "g1")
             esum(i - 1)
             fin(u - 2, 2)
+            on(u - 1, "t1")
             if u == 0:
                 split_rest(1, 1)
                 split_b(1, 1)

@@ -63,7 +63,7 @@ def tile_jointnet_kernel(
         dec_v = decT[:].rearrange("p (g w j) -> p g w j", g=2, j=4)
 
         comb, hid, hc, hs, dec_ps = {}, {}, {}, {}, {}
-        cbank, ybank, zbt, negm, xx, st = {}, {}, {}, {}, {}, {}
+        cbank, ybank, zbt, xx, st = {}, {}, {}, {}, {}
         nat_ps = {}
 
         def add(h, g, eng="V", t0=0, t1=16):
@@ -214,10 +214,14 @@ def tile_jointnet_kernel(
                 op=ALU.add,
             )
 
+        def stats(i):
+            b, n = divmod(i, 4)
+            return xx[b, n // 2 if b == B - 1 else 0]
+
         def row_max(i):
             b, n = divmod(i, 4)
             nc.vector.tensor_reduce(
-                out=negm[b][:, n : n + 1], in_=zrow(i)[:, 1:V], axis=AX.X, op=ALU.max, negate=True
+                out=stats(i)[:, n : n + 1], in_=zrow(i)[:, 1:V], axis=AX.X, op=ALU.max, negate=True
             )
 
         def exp_sum(i):
@@ -227,41 +231,39 @@ def tile_jointnet_kernel(
                 out=junk[:, 0 : V - 1],
                 in_=zrow(i)[:, 1:V],
                 func=ACT.Exp,
-                bias=negm[b][:, n : n + 1],
+                bias=stats(i)[:, n : n + 1],
                 scale=1.0,
-                accum_out=xx[b, n // 2 if b == B - 1 else 0][:, n : n + 1],
+                accum_out=stats(i)[:, 8 * (2 * STEPS + 6) + n : 8 * (2 * STEPS + 6) + n + 1],
             )
 
         def small(grp, name, width=4):
             st[grp, name] = stat.tile([P, width], F32, name=name, tag=name)
             return st[grp, name]
 
-        FIRST, EXTRA, BLANK = 2 * STEPS + 2, 2 * STEPS + 4, 2 * STEPS + 6
+        FIRST, BLANK, ARG = 2 * STEPS + 2, 2 * STEPS + 4, 2 * STEPS + 6
 
         def chain(grp, step):
             b, n0, n1 = grp
             c = n1 - n0
             z0 = zbt[b][:].rearrange("p (n v) -> p n v", n=4)[:, n0:n1, 0]
             xt = xx[b, n0 // 2] if b == B - 1 else xx[b, 0]
-            first = FIRST if grp == (B - 1, 2, 4) else 2
             tv = xt[:].rearrange("p (k a c) -> p k a c", a=2, c=4)[:, :, :, n0:n1]
+            by = FIRST if grp == (B - 1, 2, 4) else 2
             if step == "ab":
                 nc.scalar.activation(out=small(grp, "ab")[:, 0:c], in_=z0, func=ACT.Abs)
             elif step == "zc":
-                nc.scalar.activation(out=tv[:, BLANK, 0, :], in_=z0, func=ACT.Identity)
-            elif step == "mc":
                 nc.scalar.activation(
-                    out=tv[:, EXTRA, 0, :], in_=negm[b][:, n0:n1], func=ACT.Identity, scale=-1.0
+                    out=tv[:, BLANK if by == 2 else 2 * by, 0, :], in_=z0, func=ACT.Identity
                 )
             elif step == "mx":
-                nc.scalar.activation(out=tv[:, EXTRA, 1, :], in_=z0, func=ACT.Relu)
+                nc.scalar.activation(out=tv[:, 0, 1, :], in_=z0, func=ACT.Relu)
             elif step == "ev":
                 nc.scalar.activation(
                     out=small(grp, "ev")[:, 0:c], in_=st[grp, "ab"][:, 0:c], func=ACT.Exp, scale=-1.0
                 )
             elif step == "q":
                 nc.scalar.activation(
-                    out=tv[:, 0, 1, :],
+                    out=tv[:, ARG, 1, :],
                     in_=st[grp, "ev"][:, 0:c],
                     func=ACT.Identity,
                     bias=one[:],
@@ -270,17 +272,19 @@ def tile_jointnet_kernel(
             elif step == "x0":
                 nc.scalar.activation(
                     out=tv[:, FIRST, :, :],
-                    in_=xt[:, 0:8].bitcast(U32).rearrange("p (a c) -> p a c", a=2)[:, :, n0:n1],
+                    in_=xt[:, 8 * ARG : 8 * ARG + 8]
+                    .bitcast(U32)
+                    .rearrange("p (a c) -> p a c", a=2)[:, :, n0:n1],
                     func=ACT.Identity,
                     bias=guess[:],
                     scale=K1,
                 )
             elif step == "ln":
-                nc.scalar.activation(out=tv[:, FIRST, :, :], in_=tv[:, 0, :, :], func=ACT.Ln)
+                nc.scalar.activation(out=tv[:, FIRST, :, :], in_=tv[:, ARG, :, :], func=ACT.Ln)
             elif step[0] == "g":
                 k = int(step[1])
                 nc.scalar.activation(
-                    out=tv[:, 2 * k + 1, :, :],
+                    out=tv[:, 2 * k + 1 if k else ARG + 1, :, :],
                     in_=tv[:, 2 * k if k else FIRST, :, :],
                     func=ACT.Exp,
                     bias=(one if k else shift)[:],
@@ -288,34 +292,35 @@ def tile_jointnet_kernel(
                 )
             elif step[0] == "t":
                 k = int(step[1])
+                k0 = 2 * k if k else ARG
                 if b < 5:
                     nc.gpsimd.tensor_tensor(
                         out=tv[:, 2 * k + 2, :, :],
-                        in0=tv[:, 2 * k, :, :],
-                        in1=tv[:, 2 * k + 1, :, :],
+                        in0=tv[:, k0, :, :],
+                        in1=tv[:, k0 + 1, :, :],
                         op=ALU.mult,
                     )
                 else:
                     nc.vector.tensor_reduce(
                         out=tv[:, 2 * k + 2, :, :],
-                        in_=tv[:, 2 * k : 2 * k + 2, :, :].rearrange("p k a c -> p a c k"),
+                        in_=tv[:, k0 : k0 + 2, :, :].rearrange("p k a c -> p a c k"),
                         axis=AX.X,
                         op=ALU.mult,
                     )
             elif step == "z0":
                 nc.vector.tensor_reduce(
                     out=z0,
-                    in_=tv[:, first : BLANK + 1 : 2, 0, :].rearrange("p k c -> p c k"),
+                    in_=tv[:, 0 : (BLANK if by == 2 else 2 * by) + 1 : by, 0, :].rearrange("p k c -> p c k"),
                     axis=AX.X,
-                    op=ALU.add,
+                    op=ALU.subtract,
+                    negate=True,
                 )
             else:
                 nc.vector.tensor_reduce(
                     out=small(grp, "negc")[:, 0:c],
-                    in_=tv[:, first : EXTRA + 1 : 2, :, :].rearrange("p k a c -> p c k a"),
+                    in_=tv[:, 0 : FIRST + 1 : by, :, :].rearrange("p k a c -> p c k a"),
                     axis=AX.XY,
-                    op=ALU.add,
-                    negate=True,
+                    op=ALU.subtract,
                 )
 
         def finish(i, grp, eng, v0=0, v1=V):
@@ -591,9 +596,8 @@ def tile_jointnet_kernel(
 
         def new_entry(u):
             zbt[u] = zpool.tile([P, 4 * V], F32, name="zb", tag="zb")
-            negm[u] = stat.tile([P, 4], F32, name="negm", tag="negm")
             for k in range(2 if u == B - 1 else 1):
-                xx[u, k] = stat.tile([P, 8 * (2 * STEPS + 7)], F32, name="xx", tag="xx")
+                xx[u, k] = stat.tile([P, 8 * (4 * STEPS + 5)], F32, name="xx", tag="xx")
 
         for u in range(0, B - 1):
             new_entry(u)
@@ -616,16 +620,17 @@ def tile_jointnet_kernel(
             i = 4 * u + 1
             badd(i, 0)
             rmax(i - 1)
-            hidden(i + 4, 0)
             badd(i, 1)
+            hidden(i + 4, 0)
             hidden(i + 4, 1)
             on(u - 2, "g3")
             on(u - 2, "t3")
             on(u - 1, "ab")
             on(u - 1, "zc")
+            on(u - 1, "mx")
+            on(u - 1, "ev")
             esum(i - 1)
-            for step in ("ev", "mc", "q", "mx", "x0"):
-                on(u - 1, step)
+            on(u - 1, "q")
             if u == 0:
                 natural(1, 0)
                 split_hi(1, 0)
@@ -634,6 +639,7 @@ def tile_jointnet_kernel(
 
             i = 4 * u + 2
             quant(i // 2 + 1)
+            on(u - 1, "x0")
             on(u - 2, "nc")
             on(u - 2, "z0")
             rmax(i - 1)
@@ -693,7 +699,7 @@ def tile_jointnet_kernel(
         badd(i, 1)
         esum(i - 1)
         chain(ga, "t3")
-        steps(gb, ("x0", "g0", "mc"))
+        steps(gb, ("x0", "g0"))
         mm(i + 1)
 
         badd(i + 1, 0)
@@ -722,7 +728,7 @@ def tile_jointnet_kernel(
         chain(gb, "z0")
         steps(gc, ("ab", "zc", "ev", "mx", "q"))
         esum(i + 1)
-        steps(gc, ("x0", "g0", "mc"))
+        steps(gc, ("x0", "g0"))
         finish(4 * (u - 1) + 0, gb, "G")
         finish(4 * (u - 1) + 1, gb, "G")
         mm(i + 3)
@@ -742,7 +748,7 @@ def tile_jointnet_kernel(
         chain(gc, "t2")
         chain(gc, "g3")
         esum(i + 3)
-        steps(gd, ("mc", "ln"))
+        steps(gd, ("ln",))
         chain(gc, "t3")
         chain(gc, "nc")
         chain(gc, "z0")

from contextlib import ExitStack

import concourse.mybir as mybir
from concourse.masks import make_identity

F32 = mybir.dt.float32
BF16 = mybir.dt.bfloat16
U32 = mybir.dt.uint32
U8 = mybir.dt.uint8
FP8X4 = mybir.dt.float8_e4m3fn_x4
ALU = mybir.AluOpType
ACT = mybir.ActivationFunctionType
AX = mybir.AxisListType

P = 128
B, T, U, V = 8, 32, 16, 1024
FLOPS = 2 * (256 * 512 * 1024 + 128 * 512 * 1024 + 4096 * 1024 * 1024)

LN2 = 0.6931471805599453
K1 = LN2 / 8388608.0
STEPS = 4
GUESS = (0.043 - 127.0) * LN2 - STEPS

ADDED = 3


def tile_jointnet_kernel(
    tc, encoder_output, decoder_output, W_enc, b_enc, W_dec, b_dec, W_fc, b_fc, out
):
    nc = tc.nc
    out_rows = out.flatten_outer_dims()
    with ExitStack() as ctx:
        ctx.enter_context(tc.manual_schedule())
        const = ctx.enter_context(tc.tile_pool(name="const", bufs=1))
        work = ctx.enter_context(tc.tile_pool(name="work", bufs=4))
        stat = ctx.enter_context(tc.tile_pool(name="stat", bufs=4))
        psum = ctx.enter_context(tc.psum_pool(name="psum", bufs=4))

        xc = const.tile([P, 384], U32, name="xc", align_bytes=64)
        xs = const.tile([P, 384], U8, name="xs", align_bytes=64)
        wec = const.tile([P, 1024], U32, name="wec", align_bytes=64)
        wes = const.tile([P, 1024], U8, name="wes", align_bytes=64)
        wdc = const.tile([P, 1024], U32, name="wdc", align_bytes=64)
        wds = const.tile([P, 1024], U8, name="wds", align_bytes=64)
        wfc = const.tile([P, 2048], U32, name="wfc", align_bytes=64)
        wfs = const.tile([P, 2048], U8, name="wfs", align_bytes=64)
        encT = const.tile([P, ADDED * 128], F32, name="encT")
        decT = const.tile([P, 128], F32, name="decT")
        bfc = const.tile([P, V], BF16, name="bfc")
        ident = const.tile([P, P], F32, name="ident")
        bT = const.tile([P, 8], F32, name="bT")
        bsum = const.tile([P, 8], F32, name="bsum")
        warm = const.tile([P, 8], F32, name="warm")
        warm2 = const.tile([P, 8], F32, name="warm2")
        one = const.tile([P, 1], F32, name="one")
        shift = const.tile([P, 1], F32, name="shift")
        guess = const.tile([P, 1], F32, name="guess")
        amat = const.tile([P, 16 * 1024], BF16, name="amat")
        pick = const.tile([P, 256], BF16, name="pick")
        piece = [const.tile([P, 3072], BF16, name="piece%d" % q) for q in range(3)]
        rest = const.tile([P, 3072], F32, name="rest")
        enc_v = encT[:].rearrange("p (g w j) -> p g w j", g=2, j=4)
        dec_v = decT[:].rearrange("p (g w j) -> p g w j", g=2, j=4)

        comb, hid, hc, hs, dec_ps = {}, {}, {}, {}, {}
        cbank, ybank, zbt, xx, st = {}, {}, {}, {}, {}
        nat_ps = {}

        def add(h, g, eng="V", t0=0, t1=16):
            if (h, g) not in comb:
                comb[h, g] = work.tile([P, 1024], F32, name="comb", tag="comb", bufs=2 * ADDED)
            b, nt = h // 2, t1 - t0
            dec = dec_ps[g][:, b * U : (b + 1) * U, :] if eng == "V" else dec_v[:, g, :, :]
            (nc.vector if eng == "V" else nc.gpsimd).tensor_tensor(
                out=comb[h, g][:, t0 * 64 : t1 * 64].rearrange("p (t u j) -> p t u j", t=nt, u=U),
                in0=enc_v[:, g, h * 16 + t0 : h * 16 + t1, :]
                .unsqueeze(2)
                .to_broadcast([P, nt, U, 4]),
                in1=dec.unsqueeze(1).to_broadcast([P, nt, U, 4]),
                op=ALU.add,
            )

        def add_late(h, g):
            b = h // 2
            nc.scalar.copy(out=dec_v[:, g, :, :], in_=dec_ps[g][:, b * U : (b + 1) * U, :])
            for t0 in (0, 8):
                add(h, g, "G", t0, t0 + 8)

        def hid_tile(h):
            if h not in hid:
                hid[h] = work.tile([P, 2048], BF16, name="hid", tag="hid", align_bytes=64, bufs=3)
            return hid[h]

        def tanh_old(h, g):
            nc.scalar.activation(
                out=hid_tile(h)[:].rearrange("p (n g x) -> p n g x", n=2, g=2)[:, :, g, :],
                in_=comb[h, g][:].rearrange("p (n x) -> p n x", n=2),
                func=ACT.Tanh,
            )

        def comb_mm(i):
            h, n = divmod(i, 2)
            for g in range(2):
                cbank[i, g] = psum.tile([P, 512], F32, name="cb", tag="cb")
                for j in range(4):
                    c0 = h * 1024 + g * 512 + j * P
                    nc.tensor.matmul(
                        out=cbank[i, g][:, j * P : (j + 1) * P],
                        lhsT=amat[:, c0 : c0 + P],
                        rhs=pick[:, n * P : (n + 1) * P],
                        start=True,
                        stop=True,
                    )

        def tanh(i, g):
            h, n = divmod(i, 2)
            c0 = n * 1024 + g * 512
            nc.scalar.activation(
                out=hid_tile(h)[:, c0 : c0 + 512].rearrange("p (n j) -> p n j", j=4),
                in_=cbank[i, g][:].rearrange("p (j n) -> p n j", j=4),
                func=ACT.Tanh,
            )

        def quant(h):
            hc[h] = work.tile([P, 512], U32, name="hc", tag="hc", align_bytes=64, bufs=3)
            hs[h] = work.tile([P, 512], U8, name="hs", tag="hs", align_bytes=64, bufs=3)
            nc.vector.quantize_mx(out=hc[h][:].bitcast(FP8X4), scales=hs[h][:], in_=hid[h][:])

        def matmul(i):
            h, n = divmod(i, 2)
            for v in range(2):
                ybank[i, v] = psum.tile([P, 512], F32, name="y", tag="bank")
            for g in range(2):
                s0 = n * 256 + g * P
                for v in range(2):
                    c0 = g * 1024 + v * 512
                    nc.tensor.matmul_mx(
                        out=ybank[i, v][:],
                        lhsT=hc[h][:, s0 : s0 + P].bitcast(FP8X4),
                        lhsT_scale=hs[h][:, s0 : s0 + P],
                        rhs=wfc[:, c0 : c0 + 512].bitcast(FP8X4),
                        rhs_scale=wfs[:, c0 : c0 + 512],
                        start=(g == 0),
                        stop=(g == 1),
                    )

        def natural(src, g):
            cod, sca = (wec, wes) if src < 2 else (wdc, wds)
            nat_ps[src, g] = psum.tile([P, 512], F32, name="nat", tag="bank" if src == 2 else "cb")
            nc.tensor.matmul_mx(
                out=nat_ps[src, g][:],
                lhsT=xc[:, src * P : (src + 1) * P].bitcast(FP8X4),
                lhsT_scale=xs[:, src * P : (src + 1) * P],
                rhs=cod[:, g * 512 : (g + 1) * 512].bitcast(FP8X4),
                rhs_scale=sca[:, g * 512 : (g + 1) * 512],
                start=True,
                stop=True,
            )

        def split_hi(src, g):
            cols = slice(src * 1024 + g * 512, src * 1024 + (g + 1) * 512)
            nc.scalar.copy(out=piece[0][:, cols], in_=nat_ps[src, g][:])

        def split_rest(src, g):
            cols = slice(src * 1024 + g * 512, src * 1024 + (g + 1) * 512)
            nc.vector.tensor_tensor(
                out=rest[:, cols], in0=nat_ps[src, g][:], in1=piece[0][:, cols], op=ALU.subtract
            )

        def split_b(src, g, mid="G"):
            cols = slice(src * 1024 + g * 512, src * 1024 + (g + 1) * 512)
            if mid == "S":
                nc.scalar.copy(out=piece[1][:, cols], in_=rest[:, cols])
            else:
                nc.gpsimd.tensor_scalar(
                    out=piece[1][:, cols],
                    in0=rest[:, cols],
                    scalar1=1.0,
                    scalar2=0.0,
                    op0=ALU.mult,
                    op1=ALU.add,
                )
            nc.gpsimd.tensor_tensor(
                out=piece[2][:, cols], in0=rest[:, cols], in1=piece[1][:, cols], op=ALU.subtract
            )

        def move_rows(b):
            halves = [h for h in (2 * b, 2 * b + 1) if h >= ADDED]
            n = len(halves)
            a0 = halves[0] * 1024
            for q in range(3):
                for h in halves:
                    p0 = b % 4 * 32 + h % 2 * 16
                    nc.sync.dma_start(
                        out=amat[16 * q : 16 * (q + 1), h * 1024 : (h + 1) * 1024],
                        in_=piece[q][p0 : p0 + 16, b // 4 * 1024 : (b // 4 + 1) * 1024],
                    )
                nc.sync.dma_start(
                    out=amat[48 + 16 * q : 64 + 16 * q, a0 : a0 + n * 1024].rearrange(
                        "p (n x) -> p n x", n=n
                    ),
                    in_=piece[q][b * U : (b + 1) * U, 2048:3072].unsqueeze(1).to_broadcast([U, n, 1024]),
                )

        def zrow(i):
            b, n = divmod(i, 4)
            return zbt[b][:].rearrange("p (n v) -> p n v", n=4)[:, n, :]

        def bias_add(i, v):
            nc.vector.tensor_tensor(
                out=zrow(i)[:, v * 512 : (v + 1) * 512],
                in0=ybank[i, v][:],
                in1=bfc[:, v * 512 : (v + 1) * 512],
                op=ALU.add,
            )

        def stats(i):
            b, n = divmod(i, 4)
            return xx[b, n // 2 if b == B - 1 else 0]

        def row_max(i):
            b, n = divmod(i, 4)
            nc.vector.tensor_reduce(
                out=stats(i)[:, n : n + 1], in_=zrow(i)[:, 1:V], axis=AX.X, op=ALU.max, negate=True
            )

        def exp_sum(i):
            b, n = divmod(i, 4)
            junk = work.tile([P, V], BF16, name="junk", tag="junk", bufs=2)
            nc.scalar.activation(
                out=junk[:, 0 : V - 1],
                in_=zrow(i)[:, 1:V],
                func=ACT.Exp,
                bias=stats(i)[:, n : n + 1],
                scale=1.0,
                accum_out=stats(i)[:, 8 * (2 * STEPS + 6) + n : 8 * (2 * STEPS + 6) + n + 1],
            )

        def small(grp, name, width=4):
            st[grp, name] = stat.tile([P, width], F32, name=name, tag=name)
            return st[grp, name]

        FIRST, BLANK, ARG = 2 * STEPS + 2, 2 * STEPS + 4, 2 * STEPS + 6

        def chain(grp, step):
            b, n0, n1 = grp
            c = n1 - n0
            z0 = zbt[b][:].rearrange("p (n v) -> p n v", n=4)[:, n0:n1, 0]
            xt = xx[b, n0 // 2] if b == B - 1 else xx[b, 0]
            tv = xt[:].rearrange("p (k a c) -> p k a c", a=2, c=4)[:, :, :, n0:n1]
            by = FIRST if grp == (B - 1, 2, 4) else 2
            if step == "ab":
                nc.scalar.activation(out=small(grp, "ab")[:, 0:c], in_=z0, func=ACT.Abs)
            elif step == "zc":
                nc.scalar.activation(
                    out=tv[:, BLANK if by == 2 else 2 * by, 0, :], in_=z0, func=ACT.Identity
                )
            elif step == "mx":
                nc.scalar.activation(out=tv[:, 0, 1, :], in_=z0, func=ACT.Relu)
            elif step == "ev":
                nc.scalar.activation(
                    out=small(grp, "ev")[:, 0:c], in_=st[grp, "ab"][:, 0:c], func=ACT.Exp, scale=-1.0
                )
            elif step == "q":
                nc.scalar.activation(
                    out=tv[:, ARG, 1, :],
                    in_=st[grp, "ev"][:, 0:c],
                    func=ACT.Identity,
                    bias=one[:],
                    scale=1.0,
                )
            elif step == "x0":
                nc.scalar.activation(
                    out=tv[:, FIRST, :, :],
                    in_=xt[:, 8 * ARG : 8 * ARG + 8]
                    .bitcast(U32)
                    .rearrange("p (a c) -> p a c", a=2)[:, :, n0:n1],
                    func=ACT.Identity,
                    bias=guess[:],
                    scale=K1,
                )
            elif step == "ln":
                nc.scalar.activation(out=tv[:, FIRST, :, :], in_=tv[:, ARG, :, :], func=ACT.Ln)
            elif step[0] == "g":
                k = int(step[1])
                nc.scalar.activation(
                    out=tv[:, 2 * k + 1 if k else ARG + 1, :, :],
                    in_=tv[:, 2 * k if k else FIRST, :, :],
                    func=ACT.Exp,
                    bias=(one if k else shift)[:],
                    scale=-1.0,
                )
            elif step[0] == "t":
                k = int(step[1])
                k0 = 2 * k if k else ARG
                if b < 5:
                    nc.gpsimd.tensor_tensor(
                        out=tv[:, 2 * k + 2, :, :],
                        in0=tv[:, k0, :, :],
                        in1=tv[:, k0 + 1, :, :],
                        op=ALU.mult,
                    )
                else:
                    nc.vector.tensor_reduce(
                        out=tv[:, 2 * k + 2, :, :],
                        in_=tv[:, k0 : k0 + 2, :, :].rearrange("p k a c -> p a c k"),
                        axis=AX.X,
                        op=ALU.mult,
                    )
            elif step == "z0":
                nc.vector.tensor_reduce(
                    out=z0,
                    in_=tv[:, 0 : (BLANK if by == 2 else 2 * by) + 1 : by, 0, :].rearrange("p k c -> p c k"),
                    axis=AX.X,
                    op=ALU.subtract,
                    negate=True,
                )
            else:
                nc.vector.tensor_reduce(
                    out=small(grp, "negc")[:, 0:c],
                    in_=tv[:, 0 : FIRST + 1 : by, :, :].rearrange("p k a c -> p c k a"),
                    axis=AX.XY,
                    op=ALU.subtract,
                )

        def finish(i, grp, eng, v0=0, v1=V):
            z = zrow(i)[:, v0:v1]
            c = st[grp, "negc"][:, i % 4 - grp[1] : i % 4 - grp[1] + 1]
            if eng == "G":
                nc.gpsimd.tensor_scalar(
                    out=z, in0=z, scalar1=1.0, scalar2=c, op0=ALU.mult, op1=ALU.add
                )
            elif eng == "S":
                nc.scalar.activation(out=z, in_=z, func=ACT.Identity, bias=c, scale=1.0)
            else:
                nc.vector.tensor_scalar(out=z, in0=z, scalar1=c, scalar2=None, op0=ALU.add)
            nc.sync.dma_start(out=out_rows[i * P : (i + 1) * P, v0:v1], in_=z)

        with tc.tile_pool(name="staging", bufs=1) as staging:
            nc.vector.memset(warm[:], 0.0)
            brow = staging.tile([P, 1024], BF16, name="brow")
            nc.vector.memset(brow[96:128, :], 0.0)
            make_identity(nc, ident[:])
            nc.vector.memset(one[:], 1.0)
            nc.vector.memset(shift[:], -1.0 * STEPS)
            nc.vector.memset(guess[:], GUESS)
            nc.scalar.activation(out=warm2[:], in_=warm[:], func=ACT.Exp)
            braw = staging.tile([P, 256], BF16, name="braw")
            nc.vector.memset(braw[:], 0.0)
            bperm = staging.tile([P, 1024], BF16, name="bperm")
            xin = staging.tile([P, 1536], BF16, name="xin")
            we = staging.tile([P, 4096], BF16, name="we")
            wd = staging.tile([P, 4096], BF16, name="wd")
            wf = staging.tile([P, 8192], BF16, name="wf")
            xg = staging.tile([P, 1536], BF16, name="xg", align_bytes=64)
            weg = staging.tile([P, 4096], BF16, name="weg", align_bytes=64)
            wdg = staging.tile([P, 4096], BF16, name="wdg", align_bytes=64)
            wfg = [
                staging.tile([P, 4096], BF16, name="wfg%d" % g, align_bytes=64) for g in range(2)
            ]

            we_src = W_enc.rearrange("(c p e) k -> p c (e k)", c=4, p=P, e=2)
            wd_src = W_dec.rearrange("(c p e) k -> p c (e k)", c=4, p=P, e=2)
            we_dst = we[:].rearrange("p (c x) -> p c x", c=4)
            wd_dst = wd[:].rearrange("p (c x) -> p c x", c=4)
            wf_src = W_fc.rearrange("(r p) f -> p r f", p=P)
            wf_dst = wf[:].rearrange("p (r f) -> p r f", r=8)
            nc.sync.dma_start(
                out=xin[:, 0:1024].rearrange("p (r k) -> p r k", r=2),
                in_=encoder_output.flatten_outer_dims().rearrange("(r p) k -> p r k", p=P),
            )
            nc.sync.dma_start(out=xin[:, 1024:1536], in_=decoder_output.flatten_outer_dims())
            nc.sync.dma_start(out=we_dst[:, 0:2, :], in_=we_src[:, 0:2, :])
            nc.sync.dma_start(out=wd_dst[:, 0:2, :], in_=wd_src[:, 0:2, :])
            nc.sync.dma_start(out=braw[0:4, :], in_=b_enc.rearrange("(c x) -> c x", c=4))
            nc.sync.dma_start(out=braw[4:8, :], in_=b_dec.rearrange("(c x) -> c x", c=4))
            nc.sync.dma_start(out=we_dst[:, 2:4, :], in_=we_src[:, 2:4, :])
            nc.sync.dma_start(out=wd_dst[:, 2:4, :], in_=wd_src[:, 2:4, :])
            nc.sync.dma_start(out=wf_dst[:, 0:2, :], in_=wf_src[:, 0:2, :])
            nc.sync.dma_start(out=brow[96:97, :], in_=b_enc.unsqueeze(0))
            nc.sync.dma_start(out=brow[97:98, :], in_=b_dec.unsqueeze(0))
            for r0 in range(2, 8, 2):
                nc.sync.dma_start(out=wf_dst[:, r0 : r0 + 2, :], in_=wf_src[:, r0 : r0 + 2, :])
            nc.sync.dma_start(out=bfc[:], in_=b_fc.partition_broadcast(P))

            by_t = staging.tile([P, 16], F32, name="by_t")
            by_u = staging.tile([P, 16], F32, name="by_u")
            both = staging.tile([P, 1], F32, name="both")
            for dst, c0 in ((by_t, 0), (by_u, 48)):
                nc.vector.tensor_reduce(
                    out=dst[:],
                    in_=ident[:, c0 : c0 + 48].rearrange("p (q t) -> p t q", q=3),
                    axis=AX.X,
                    op=ALU.add,
                )
            nc.vector.tensor_reduce(out=both[:], in_=ident[:, 96:98], axis=AX.X, op=ALU.add)
            nc.vector.tensor_scalar(
                out=by_t[:], in0=by_t[:], scalar1=both[:], scalar2=None, op0=ALU.add
            )
            nc.vector.tensor_tensor(
                out=pick[:].rearrange("p (t u) -> p t u", t=16),
                in0=by_t[:].unsqueeze(2).to_broadcast([P, 16, U]),
                in1=by_u[:].unsqueeze(1).to_broadcast([P, 16, U]),
                op=ALU.add,
            )

            def turn(srcs, dst32, eng):
                n = len(srcs) // 2
                pt = psum.tile([P, 512], F32, name="pt", tag="bank")
                for i, s in enumerate(srcs):
                    nc.tensor.transpose(out=pt[:, i * P : (i + 1) * P], in_=s, identity=ident[:])
                dst = dst32.rearrange("q (c r h) -> q c r h", c=n, h=2)
                src = pt[:, 0 : n * 256].rearrange("q (c h r) -> q c r h", c=n, h=2)
                if eng == "V":
                    nc.vector.tensor_copy(out=dst, in_=src)
                else:
                    nc.scalar.copy(out=dst, in_=src)

            def blocks(src32, first, count):
                return [src32[:, (first + i) * P : (first + i + 1) * P] for i in range(count)]

            xin32, xg32 = xin[:].bitcast(F32), xg[:].bitcast(F32)
            turn(blocks(xin32, 0, 4), xg32[:, 0:512], "S")
            turn(blocks(xin32, 4, 2), xg32[:, 512:768], "S")
            nc.vector.quantize_mx(
                out=xc[:, 0:256].bitcast(FP8X4), scales=xs[:, 0:256], in_=xg[:, 0:1024]
            )
            nc.vector.quantize_mx(
                out=xc[:, 256:384].bitcast(FP8X4), scales=xs[:, 256:384], in_=xg[:, 1024:1536]
            )

            def weights(raw, grp, cod, sca, g, eng):
                r32, g32 = raw[:].bitcast(F32), grp[:].bitcast(F32)
                turn(blocks(r32, g * 8, 4), g32[:, g * 1024 : g * 1024 + 512], "S")
                turn(blocks(r32, g * 8 + 4, 4), g32[:, g * 1024 + 512 : g * 1024 + 1024], eng)
                nc.vector.quantize_mx(
                    out=cod[:, g * 512 : (g + 1) * 512].bitcast(FP8X4),
                    scales=sca[:, g * 512 : (g + 1) * 512],
                    in_=grp[:, g * 2048 : (g + 1) * 2048],
                )

            enc_ps = {}

            def project(g, r):
                cod, sca = (wec, wes) if r < 2 else (wdc, wds)
                ps = psum.tile([P, 512], F32, name="ps", tag="bank" if r < 2 else "cb")
                for j in range(4):
                    c0 = (g * 4 + j) * P
                    nc.tensor.matmul_mx(
                        out=ps[:, j * P : (j + 1) * P],
                        lhsT=cod[:, c0 : c0 + P].bitcast(FP8X4),
                        lhsT_scale=sca[:, c0 : c0 + P],
                        rhs=xc[:, r * P : (r + 1) * P].bitcast(FP8X4),
                        rhs_scale=xs[:, r * P : (r + 1) * P],
                        start=True,
                        stop=True,
                    )
                view = ps[:].rearrange("p (j w) -> p w j", j=4)
                (dec_ps if r == 2 else enc_ps)[g] = view

            def enc_out(g):
                w = ADDED * 16
                nc.vector.tensor_tensor(
                    out=enc_v[:, g, :, :],
                    in0=enc_ps[g][:, 0:w, :],
                    in1=bsum[:, g * 4 : (g + 1) * 4].unsqueeze(1).to_broadcast([P, w, 4]),
                    op=ALU.add,
                )

            wf32 = wf[:].bitcast(F32).rearrange("p (r g x) -> p r g x", r=8, g=2)

            def fc_weights(r0, g, eng):
                srcs = [wf32[:, r0 + c, g, h * P : (h + 1) * P] for c in range(2) for h in range(2)]
                turn(srcs, wfg[g][:].bitcast(F32)[:, r0 * 256 : (r0 + 2) * 256], eng)

            def fc_quant(g, half):
                c0 = g * 1024 + half * 512
                nc.vector.quantize_mx(
                    out=wfc[:, c0 : c0 + 512].bitcast(FP8X4),
                    scales=wfs[:, c0 : c0 + 512],
                    in_=wfg[g][:, half * 2048 : (half + 1) * 2048],
                )

            weights(we, weg, wec, wes, 0, "S")
            weights(wd, wdg, wdc, wds, 0, "S")
            weights(we, weg, wec, wes, 1, "S")
            weights(wd, wdg, wdc, wds, 1, "S")
            ptb = psum.tile([P, 512], F32, name="ptb", tag="bank")
            nc.tensor.transpose(out=ptb[:, 0:P], in_=braw[:].bitcast(F32), identity=ident[:])
            nc.vector.tensor_copy(out=bT[:], in_=ptb[:, 0:8])
            bT16 = bT[:].bitcast(BF16)
            fc_weights(0, 0, "S")
            project(0, 2)
            project(0, 0)
            nc.vector.tensor_tensor(out=bsum[:], in0=bT16[:, 0:8], in1=bT16[:, 8:16], op=ALU.add)
            fc_weights(2, 0, "S")
            natural(0, 0)
            natural(2, 0)
            fc_weights(0, 1, "S")
            nc.vector.tensor_copy(
                out=bperm[96:128, :].rearrange("p (c e w) -> p c e w", c=4, e=2),
                in_=brow[96:128, :].rearrange("p (c w e) -> p c e w", c=4, e=2),
            )
            nc.sync.dma_start(
                out=amat[96:128, ADDED * 1024 :].rearrange("p (h x) -> p h x", x=1024),
                in_=bperm[96:128, :].unsqueeze(1).to_broadcast([32, 16 - ADDED, 1024]),
            )
            enc_out(0)
            add_late(2, 0)
            add(0, 0)
            split_hi(0, 0)
            split_hi(2, 0)
            fc_quant(0, 0)
            project(1, 2)
            project(1, 0)
            fc_weights(2, 1, "S")
            split_rest(0, 0)
            split_b(0, 0, "S")
            split_rest(2, 0)
            split_b(2, 0, "S")
            natural(0, 1)
            fc_weights(4, 0, "S")
            natural(2, 1)
            enc_out(1)
            add(0, 1)
            split_hi(0, 1)
            split_hi(2, 1)
            fc_quant(1, 0)
            fc_weights(4, 1, "S")
            split_rest(0, 1)
            split_b(0, 1)
            split_rest(2, 1)
            split_b(2, 1)
            for b in (1, 2, 3):
                move_rows(b)
            tanh_old(0, 0)
            fc_weights(6, 0, "S")
            add(1, 0)
            tanh_old(0, 1)
            fc_weights(6, 1, "S")
            add(1, 1)
            add(2, 1)
            quant(0)
            fc_quant(0, 1)
            fc_quant(1, 1)
            tanh_old(1, 0)
            tanh_old(1, 1)
            matmul(0)

        zpool = ctx.enter_context(tc.tile_pool(name="zpool", bufs=5))

        def on(b, step):
            if 0 <= b < B - 1:
                chain((b, 0, 4), step)

        def tile_ok(i):
            return 0 <= i < 4 * B

        def esum(i):
            if tile_ok(i):
                exp_sum(i)

        def badd(i, v):
            if tile_ok(i):
                bias_add(i, v)

        def rmax(i):
            if tile_ok(i):
                row_max(i)

        def fin(b, n):
            if 0 <= b < B - 1:
                finish(4 * b + n, (b, 0, 4), "G")

        def mm(i):
            if tile_ok(i):
                matmul(i)

        def hidden(i, g):
            h, n = divmod(i, 2)
            if h >= ADDED:
                tanh(i, g)
            elif n == 0:
                tanh_old(h, g)

        def cmm(i):
            if tile_ok(i) and i // 2 >= ADDED:
                comb_mm(i)

        gate = const.tile([P, 8], F32, name="gate")

        def hold(i):
            nc.gpsimd.tensor_scalar(
                out=gate[:, 0:1], in0=zrow(i)[:, 0:1], scalar1=1.0, scalar2=0.0, op0=ALU.mult, op1=ALU.add
            )

        def new_entry(u):
            zbt[u] = zpool.tile([P, 4 * V], F32, name="zb", tag="zb")
            for k in range(2 if u == B - 1 else 1):
                xx[u, k] = stat.tile([P, 8 * (4 * STEPS + 5)], F32, name="xx", tag="xx")

        for u in range(0, B - 1):
            new_entry(u)
            i = 4 * u
            quant(i // 2 + 1)
            rmax(i - 1)
            badd(i, 0)
            badd(i, 1)
            hidden(i + 4, 0)
            hidden(i + 4, 1)
            on(u - 2, "g2")
            if u > 2:
                hold(i)
                fin(u - 3, 3)
            on(u - 2, "t2")
            esum(i - 1)
            mm(i + 1)
            cmm(i + 5)

            i = 4 * u + 1
            badd(i, 0)
            rmax(i - 1)
            badd(i, 1)
            hidden(i + 4, 0)
            hidden(i + 4, 1)
            on(u - 2, "g3")
            on(u - 2, "t3")
            on(u - 1, "ab")
            on(u - 1, "zc")
            on(u - 1, "mx")
            on(u - 1, "ev")
            esum(i - 1)
            on(u - 1, "q")
            if u == 0:
                natural(1, 0)
                split_hi(1, 0)
            mm(i + 1)
            cmm(i + 5)

            i = 4 * u + 2
            quant(i // 2 + 1)
            on(u - 1, "x0")
            on(u - 2, "nc")
            on(u - 2, "z0")
            rmax(i - 1)
            badd(i, 0)
            hidden(i + 4, 0)
            on(u - 1, "g0")
            badd(i, 1)
            hidden(i + 4, 1)
            esum(i - 1)
            fin(u - 2, 0)
            fin(u - 2, 1)
            on(u - 1, "t0")
            if u == 0:
                split_rest(1, 0)
                split_b(1, 0)
                natural(1, 1)
                split_hi(1, 1)
            mm(i + 1)
            cmm(i + 5)

            i = 4 * u + 3
            badd(i, 0)
            rmax(i - 1)
            hidden(i + 4, 0)
            badd(i, 1)
            hidden(i + 4, 1)
            on(u - 1, "g1")
            esum(i - 1)
            fin(u - 2, 2)
            on(u - 1, "t1")
            if u == 0:
                split_rest(1, 1)
                split_b(1, 1)
                for b in range(4, 8):
                    move_rows(b)
            mm(i + 1)
            cmm(i + 5)

        u = B - 1
        new_entry(u)
        ga, gb, gc, gd = (u - 2, 0, 4), (u - 1, 0, 4), (u, 0, 2), (u, 2, 4)
        i = 4 * u

        def steps(grp, names):
            for name in names:
                chain(grp, name)

        quant(i // 2 + 1)
        chain(ga, "g2")
        rmax(i - 1)
        chain(ga, "t2")
        badd(i, 0)
        steps(gb, ("ab", "zc", "ev", "mx", "q"))
        hold(i)
        fin(u - 3, 3)
        chain(ga, "g3")
        badd(i, 1)
        esum(i - 1)
        chain(ga, "t3")
        steps(gb, ("x0", "g0"))
        mm(i + 1)

        badd(i + 1, 0)
        chain(ga, "nc")
        chain(ga, "z0")
        finish(4 * (u - 2) + 0, ga, "G")
        chain(gb, "t0")
        chain(gb, "g1")
        finish(4 * (u - 2) + 3, ga, "S")
        rmax(i)
        chain(gb, "t1")
        chain(gb, "g2")
        badd(i + 1, 1)
        finish(4 * (u - 2) + 1, ga, "G")
        chain(gb, "t2")
        esum(i)
        chain(gb, "g3")
        mm(i + 2)

        badd(i + 2, 0)
        finish(4 * (u - 2) + 2, ga, "G")
        rmax(i + 1)
        chain(gb, "t3")
        badd(i + 2, 1)
        chain(gb, "nc")
        chain(gb, "z0")
        steps(gc, ("ab", "zc", "ev", "mx", "q"))
        esum(i + 1)
        steps(gc, ("x0", "g0"))
        finish(4 * (u - 1) + 0, gb, "G")
        finish(4 * (u - 1) + 1, gb, "G")
        mm(i + 3)

        badd(i + 3, 0)
        rmax(i + 2)
        chain(gc, "t0")
        finish(4 * (u - 1) + 2, gb, "G")
        steps(gd, ("ab", "zc", "ev", "mx", "q"))
        chain(gc, "g1")
        badd(i + 3, 1)
        chain(gc, "t1")
        esum(i + 2)
        chain(gc, "g2")
        finish(4 * (u - 1) + 3, gb, "G")
        rmax(i + 3)
        chain(gc, "t2")
        chain(gc, "g3")
        esum(i + 3)
        steps(gd, ("ln",))
        chain(gc, "t3")
        chain(gc, "nc")
        chain(gc, "z0")
        finish(i, gc, "V")
        finish(i + 1, gc, "V")
        chain(gd, "nc")
        chain(gd, "z0")
        finish(i + 2, gd, "V")
        finish(i + 3, gd, "S", 0, 512)
        finish(i + 3, gd, "V", 512, V)
